import numpy as np
import ml_dtypes


def mxq(x, axis, fmt="e4m3"):
    dtype, down = {"e4m3": (ml_dtypes.float8_e4m3fn, 7), "e5m2": (ml_dtypes.float8_e5m2, 14)}[fmt]
    v = np.moveaxis(np.asarray(x, np.float32).astype(ml_dtypes.bfloat16).astype(np.float64), axis, -1)
    blocks = v.reshape(v.shape[:-1] + (-1, 32))
    amax = np.abs(blocks).max(-1, keepdims=True)
    byte = np.maximum(np.where(amax > 0, np.frexp(amax)[1] - 1 + 127, 0) - down, 1)
    scale = np.exp2(byte - 127.0)
    codes = (blocks / scale).astype(np.float32).astype(dtype).astype(np.float64)
    return np.moveaxis((codes * scale).reshape(v.shape), -1, axis)


WIDE = False


def mx_kscale(k):
    if not WIDE:
        return np.ones(k)
    levels = np.array([10, -10, 5, -5, 0])
    a = np.random.permutation(np.resize(levels, k // 512 * 4)).reshape(k // 512, 4)
    idx = np.arange(k)
    return np.exp2(a[idx // 512, idx % 128 // 32])


BF16 = ml_dtypes.bfloat16


def bf(x):
    return np.asarray(x, np.float32).astype(BF16)


def f64(x):
    return np.asarray(x).astype(np.float64)


S, H, E, P, C = 1024, 256, 416, 64, 32
D = 2 * H


def sigmoid(v):
    return 1.0 / (1.0 + np.exp(-v))


def lstm_gates(g, c):
    i, f, gg, o = np.split(g, 4, axis=-1)
    c2 = sigmoid(f) * c + sigmoid(i) * np.tanh(gg)
    return sigmoid(o) * np.tanh(c2)


def setup_inputs():
    n = np.random.standard_normal
    s = mx_kscale(D)
    d = {"y": bf(n((S, D)) * 0.3 * s), "h0": bf(n((2, S, H))), "c0": bf(n((2, S, H)))}
    for k in ("f", "b"):
        d["wih_" + k] = bf(n((4 * H, D)) * 3.0 / np.sqrt(D) / s)
        d["whh_" + k] = bf(n((4 * H, H)) * 0.7 / np.sqrt(H))
        d["bih_" + k] = bf(n(4 * H) * 0.2)
        d["bhh_" + k] = bf(n(4 * H) * 0.2)
    d["wd"] = bf(n(D))
    d["fc_w"] = bf(n((1, D)) * 12.0 / np.sqrt(D))
    d["fc_b"] = bf(0.5 + 0.1 * n(1))
    return d


def reference(y, h0, c0, wih_f, whh_f, bih_f, bhh_f, wih_b, whh_b, bih_b, bhh_b, wd, fc_w, fc_b):
    yq = mxq(f64(y), 1, "e4m3")
    gf = (yq @ mxq(f64(wih_f), 1, "e4m3").T) + f64(bih_f) + f64(h0)[0] @ f64(whh_f).T + f64(bhh_f)
    gb = (yq @ mxq(f64(wih_b), 1, "e4m3").T) + f64(bih_b) + f64(h0)[1] @ f64(whh_b).T + f64(bhh_b)
    hid = np.concatenate([lstm_gates(gf, f64(c0)[0]), lstm_gates(gb, f64(c0)[1])], axis=-1)
    scores = (mxq(hid * (f64(wd) * f64(fc_w)[0]), 1, "e4m3") @ mxq(hid, 1, "e4m3").T) + f64(fc_b)[0]
    keep = np.triu(np.ones((S, S), dtype=bool))
    scores = np.where(keep, scores, 0.0)
    return scores, hid[None]

@@ -1,0 +1,267 @@
+from contextlib import ExitStack
+
+import concourse.mybir as mybir
+from concourse.masks import make_identity
+
+BF16 = mybir.dt.bfloat16
+F32 = mybir.dt.float32
+U32 = mybir.dt.uint32
+U8 = mybir.dt.uint8
+FP8X4 = mybir.dt.float8_e4m3fn_x4
+ACT = mybir.ActivationFunctionType
+ALU = mybir.AluOpType
+
+P = 128
+PACK = 4
+S = 1024
+H = 256
+D = 2 * H
+CHUNK = 512
+ROW_TILES = CHUNK // P
+HALVES = S // CHUNK
+H_TILES = H // P
+DIRECTIONS = 2
+FEATURE_TILES = DIRECTIONS * H_TILES
+
+GATES = (("in_gate", ACT.Sigmoid), ("forget_gate", ACT.Sigmoid), ("candidate", ACT.Tanh), ("out_gate", ACT.Sigmoid))
+
+FLOPS = 2 * S * (4 * H) * D * DIRECTIONS + 2 * S * (4 * H) * H * DIRECTIONS + 2 * S * S * D
+
+
+def load_chunk(nc, pool, rows, name):
+    raw = pool.tile([P, ROW_TILES, rows.shape[1]], BF16, name=name)
+    nc.sync.dma_start(out=raw[:], in_=rows.rearrange("(a p) k -> p a k", p=P))
+    return raw
+
+
+def quantise_chunk(nc, psum, stage, raw, ident_f32, codes, scales):
+    grouped = stage.tile([P, CHUNK * PACK], BF16, tag="grouped", align_bytes=64)
+    grouped_words = grouped[:].bitcast(F32).rearrange("p (r u) -> p r u", u=2)
+    for pair in range(ROW_TILES // 2):
+        words_T = psum.tile([P, 2, 2 * P], F32, tag="flip")
+        for i in range(2):
+            raw_words = raw[:, 2 * pair + i, :].bitcast(F32)
+            for u in range(2):
+                nc.tensor.transpose(words_T[:, u, P * i : P * (i + 1)], raw_words[:, P * u : P * (u + 1)], ident_f32[:])
+        copy = nc.vector.tensor_copy if pair == 0 else nc.scalar.copy
+        copy(out=grouped_words[:, 2 * P * pair : 2 * P * (pair + 1), :], in_=words_T[:].rearrange("p u r -> p r u"))
+    nc.vector.quantize_mx(out=codes[:].bitcast(FP8X4), scales=scales[:], in_=grouped[:])
+
+
+def transpose_chunk(nc, psum, raw, ident_bf16, flipped):
+    for j in range(H_TILES):
+        flip = psum.tile([P, ROW_TILES, P], BF16, tag="flip")
+        for a in range(ROW_TILES):
+            nc.tensor.transpose(flip[:, a, :], raw[:, a, P * j : P * (j + 1)], ident_bf16[:])
+        copy = nc.vector.tensor_copy if j == 0 else nc.scalar.copy
+        copy(out=flipped[:, j, :], in_=flip[:].rearrange("p a r -> p (a r)"))
+
+
+def tile_dependency_pb_kernel(
+    tc, y, h0, c0, wih_f, whh_f, bih_f, bhh_f, wih_b, whh_b, bih_b, bhh_b, wd, fc_w, fc_b, out_0, out_1
+):
+    nc = tc.nc
+    wih = (wih_f, wih_b)
+    whh = (whh_f, whh_b)
+    with ExitStack() as stack:
+        const = stack.enter_context(tc.tile_pool(name="const", bufs=1))
+        raws = stack.enter_context(tc.tile_pool(name="raws", bufs=1))
+        keep = stack.enter_context(tc.tile_pool(name="keep", bufs=1))
+        stage = stack.enter_context(tc.tile_pool(name="stage", bufs=2))
+        sums = stack.enter_context(tc.tile_pool(name="sums", bufs=4))
+        work = stack.enter_context(tc.tile_pool(name="work", bufs=2))
+        outs = stack.enter_context(tc.tile_pool(name="outs", bufs=3))
+        psum_flip = stack.enter_context(tc.psum_pool(name="psum_flip", bufs=2))
+        psum_plain = stack.enter_context(tc.psum_pool(name="psum_plain", bufs=3))
+        psum_mx = stack.enter_context(tc.psum_pool(name="psum_mx", bufs=3))
+
+        ident_bf16 = const.tile([P, P], BF16)
+        make_identity(nc, ident_bf16[:])
+        ident_f32 = const.tile([P, P], F32)
+        make_identity(nc, ident_f32[:])
+
+        vector_rows = const.tile([P, P], BF16)
+        nc.vector.memset(vector_rows[:], 0.0)
+        row = 0
+        first_row = {}
+        for name, vec in (("bih0", bih_f), ("bhh0", bhh_f), ("bih1", bih_b), ("bhh1", bhh_b), ("wd", wd), ("fc_w", fc_w[0])):
+            n_rows = vec.shape[0] // P
+            nc.gpsimd.dma_start(out=vector_rows[row : row + n_rows, :], in_=vec.rearrange("(r c) -> r c", c=P))
+            first_row[name] = row
+            row += n_rows
+        fc_b_bf16 = const.tile([P, 1], BF16)
+        nc.gpsimd.dma_start(out=fc_b_bf16[:], in_=fc_b.partition_broadcast(P))
+
+        on_or_above = const.tile([P, CHUNK], F32)
+        nc.gpsimd.memset(on_or_above[:], 1.0)
+        nc.gpsimd.affine_select(
+            out=on_or_above[:],
+            in_=on_or_above[:],
+            pattern=[[1, CHUNK]],
+            compare_op=ALU.is_ge,
+            fill=0.0,
+            base=0,
+            channel_multiplier=-1,
+        )
+        zeros = const.tile([P, S - P], F32)
+        nc.vector.memset(zeros[:], 0.0)
+
+        y_codes, y_scales, wih_codes, wih_scales, whhT, h0T, c0T = {}, {}, {}, {}, {}, {}, {}
+
+        def prepare_weights(d):
+            for c in range(2):
+                whh_raw = load_chunk(nc, raws, whh[d][CHUNK * c : CHUNK * (c + 1), :], "whh_raw_%d_%d" % (d, c))
+                whhT[d, c] = keep.tile([P, H_TILES, CHUNK], BF16, name="whhT_%d_%d" % (d, c))
+                transpose_chunk(nc, psum_flip, whh_raw, ident_bf16, whhT[d, c])
+            for c in range(2):
+                wih_raw = load_chunk(nc, raws, wih[d][CHUNK * c : CHUNK * (c + 1), :], "wih_raw_%d_%d" % (d, c))
+                wih_codes[d, c] = keep.tile([P, CHUNK], U32, name="wih_codes_%d_%d" % (d, c), align_bytes=64)
+                wih_scales[d, c] = keep.tile([P, CHUNK], U8, name="wih_scales_%d_%d" % (d, c), align_bytes=64)
+                quantise_chunk(nc, psum_flip, stage, wih_raw, ident_f32, wih_codes[d, c], wih_scales[d, c])
+
+        def prepare_y(n):
+            y_raw = load_chunk(nc, raws, y[CHUNK * n : CHUNK * (n + 1), :], "y_raw_%d" % n)
+            y_codes[n] = keep.tile([P, CHUNK], U32, name="y_codes_%d" % n, align_bytes=64)
+            y_scales[n] = keep.tile([P, CHUNK], U8, name="y_scales_%d" % n, align_bytes=64)
+            quantise_chunk(nc, psum_flip, stage, y_raw, ident_f32, y_codes[n], y_scales[n])
+
+        def prepare_state(d, n):
+            for what, state, flipped in (("h0", h0, h0T), ("c0", c0, c0T)):
+                state_raw = load_chunk(nc, raws, state[d, CHUNK * n : CHUNK * (n + 1), :], "%s_raw_%d_%d" % (what, d, n))
+                flipped[d, n] = keep.tile([P, H_TILES, CHUNK], BF16, name="%sT_%d_%d" % (what, d, n))
+                transpose_chunk(nc, psum_flip, state_raw, ident_bf16, flipped[d, n])
+
+        prepare_weights(0)
+        prepare_y(0)
+        prepare_state(0, 0)
+
+        vector_cols_ps = psum_flip.tile([P, P], BF16, tag="flip")
+        nc.tensor.transpose(vector_cols_ps[:], vector_rows[:], ident_bf16[:])
+        vector_cols = const.tile([P, P], F32)
+        nc.vector.tensor_copy(out=vector_cols[:], in_=vector_cols_ps[:])
+        gate_tiles = 4 * H // P
+        bias = []
+        for d in range(DIRECTIONS):
+            bias_d = const.tile([P, gate_tiles], F32, name="bias_%d" % d)
+            ih, hh = first_row["bih%d" % d], first_row["bhh%d" % d]
+            nc.vector.tensor_tensor(
+                out=bias_d[:], in0=vector_cols[:, ih : ih + gate_tiles], in1=vector_cols[:, hh : hh + gate_tiles], op=ALU.add
+            )
+            bias.append(bias_d)
+        pair_weight = const.tile([P, FEATURE_TILES], F32)
+        nc.vector.tensor_tensor(
+            out=pair_weight[:],
+            in0=vector_cols[:, first_row["wd"] : first_row["wd"] + FEATURE_TILES],
+            in1=vector_cols[:, first_row["fc_w"] : first_row["fc_w"] + FEATURE_TILES],
+            op=ALU.mult,
+        )
+        fc_b_col = const.tile([P, 1], F32)
+        nc.vector.tensor_copy(out=fc_b_col[:], in_=fc_b_bf16[:])
+
+        prepare_weights(1)
+        prepare_state(1, 0)
+        prepare_y(1)
+        prepare_state(0, 1)
+        prepare_state(1, 1)
+
+        for r in range(1, S // P):
+            nc.sync.dma_start(out=out_0[P * r : P * (r + 1), 0 : P * r], in_=zeros[:, 0 : P * r])
+
+        hid_codes, hid_scales, u_codes, u_scales = {}, {}, {}, {}
+
+        def lstm_tile(n, d, j, hidT):
+            gate = {}
+            for q, (name, func) in enumerate(GATES):
+                g = H_TILES * q + j
+                c, cols = g // ROW_TILES, slice(P * (g % ROW_TILES), P * (g % ROW_TILES + 1))
+                recurrent_ps = psum_plain.tile([P, CHUNK], F32, tag="plain")
+                for k in range(H_TILES):
+                    nc.tensor.matmul(
+                        recurrent_ps[:], lhsT=whhT[d, c][:, k, cols], rhs=h0T[d, n][:, k, :], start=(k == 0), stop=(k == H_TILES - 1)
+                    )
+                input_ps = psum_mx.tile([P, CHUNK], F32, tag="mx")
+                nc.tensor.matmul_mx(
+                    out=input_ps[:],
+                    lhsT=wih_codes[d, c][:, cols].bitcast(FP8X4),
+                    lhsT_scale=wih_scales[d, c][:, cols],
+                    rhs=y_codes[n][:].bitcast(FP8X4),
+                    rhs_scale=y_scales[n][:],
+                    start=True,
+                    stop=True,
+                )
+                pre = sums.tile([P, CHUNK], F32, tag="pre")
+                nc.scalar.copy(out=pre[:], in_=recurrent_ps[:])
+                nc.vector.tensor_tensor(out=pre[:], in0=input_ps[:], in1=pre[:], op=ALU.add)
+                gate[name] = work.tile([P, CHUNK], F32, name=name, tag=name)
+                nc.scalar.activation(out=gate[name][:], in_=pre[:], func=func, bias=bias[d][:, g : g + 1], scale=1.0)
+            cell = work.tile([P, CHUNK], F32, tag="cell")
+            nc.vector.tensor_tensor(out=cell[:], in0=gate["forget_gate"][:], in1=c0T[d, n][:, j, :], op=ALU.mult)
+            fresh = work.tile([P, CHUNK], F32, tag="fresh")
+            nc.vector.tensor_tensor(out=fresh[:], in0=gate["in_gate"][:], in1=gate["candidate"][:], op=ALU.mult)
+            nc.vector.tensor_tensor(out=cell[:], in0=cell[:], in1=fresh[:], op=ALU.add)
+            tanh_cell = work.tile([P, CHUNK], F32, tag="tanh_cell")
+            nc.scalar.activation(out=tanh_cell[:], in_=cell[:], func=ACT.Tanh)
+            nc.vector.tensor_tensor(out=hidT[:, H_TILES * d + j, :], in0=gate["out_gate"][:], in1=tanh_cell[:], op=ALU.mult)
+
+        def quantise_hid(n, hidT):
+            by_token = hidT[:].rearrange("p t r -> p r t")
+            hid_grouped = stage.tile([P, CHUNK, PACK], BF16, tag="hid_grouped", align_bytes=64)
+            nc.scalar.copy(out=hid_grouped[:], in_=by_token)
+            u_grouped = stage.tile([P, CHUNK, PACK], BF16, tag="u_grouped", align_bytes=64)
+            nc.vector.tensor_tensor(
+                out=u_grouped[:], in0=by_token, in1=pair_weight[:].unsqueeze(1).to_broadcast([P, CHUNK, PACK]), op=ALU.mult
+            )
+            for what, grouped, codes, scales in (("hid", hid_grouped, hid_codes, hid_scales), ("u", u_grouped, u_codes, u_scales)):
+                codes[n] = keep.tile([P, CHUNK], U32, name="%s_codes_%d" % (what, n), align_bytes=64)
+                scales[n] = keep.tile([P, CHUNK], U8, name="%s_scales_%d" % (what, n), align_bytes=64)
+                nc.vector.quantize_mx(
+                    out=codes[n][:].bitcast(FP8X4), scales=scales[n][:], in_=grouped[:].rearrange("p r t -> p (r t)")
+                )
+
+        def store_hid(n, hidT):
+            for a in range(ROW_TILES):
+                hid_ps = psum_flip.tile([P, FEATURE_TILES, P], F32, tag="flip")
+                for t in range(FEATURE_TILES):
+                    nc.tensor.transpose(hid_ps[:, t, :], hidT[:, t, P * a : P * (a + 1)], ident_f32[:])
+                hid_rows = outs.tile([P, D], F32, tag="hid_rows")
+                nc.scalar.copy(out=hid_rows[:], in_=hid_ps[:].rearrange("p t c -> p (t c)"))
+                first = CHUNK * n + P * a
+                nc.sync.dma_start(out=out_1[0, first : first + P, :], in_=hid_rows[:])
+
+        def score_piece(r, n):
+            score_ps = psum_mx.tile([P, CHUNK], F32, tag="mx")
+            u_cols = slice(P * (r % ROW_TILES), P * (r % ROW_TILES + 1))
+            nc.tensor.matmul_mx(
+                out=score_ps[:],
+                lhsT=u_codes[r // ROW_TILES][:, u_cols].bitcast(FP8X4),
+                lhsT_scale=u_scales[r // ROW_TILES][:, u_cols],
+                rhs=hid_codes[n][:].bitcast(FP8X4),
+                rhs_scale=hid_scales[n][:],
+                start=True,
+                stop=True,
+            )
+            first = max(P * r - CHUNK * n, 0)
+            width = CHUNK - first
+            piece = outs.tile([P, CHUNK], F32, tag="piece")
+            if P * r >= CHUNK * n:
+                nc.vector.scalar_tensor_tensor(
+                    out=piece[:, 0:width],
+                    in0=score_ps[:, first:CHUNK],
+                    scalar=fc_b_col[:, 0:1],
+                    in1=on_or_above[:, 0:width],
+                    op0=ALU.add,
+                    op1=ALU.mult,
+                )
+            else:
+                nc.scalar.activation(out=piece[:], in_=score_ps[:], func=ACT.Identity, bias=fc_b_col[:, 0:1], scale=1.0)
+            nc.sync.dma_start(out=out_0[P * r : P * (r + 1), CHUNK * n + first : CHUNK * (n + 1)], in_=piece[:, 0:width])
+
+        for n in range(HALVES):
+            hidT = keep.tile([P, FEATURE_TILES, CHUNK], F32, name="hidT_%d" % n)
+            for d in range(DIRECTIONS):
+                for j in range(H_TILES):
+                    lstm_tile(n, d, j, hidT)
+            quantise_hid(n, hidT)
+            store_hid(n, hidT)
+            for r in range(ROW_TILES * (n + 1)):
+                score_piece(r, n)

@@ -22,55 +22,60 @@ HALVES = S // CHUNK
 H_TILES = H // P
 DIRECTIONS = 2
 FEATURE_TILES = DIRECTIONS * H_TILES
+GATE_TILES = 4 * H // P
 
-GATES = (("in_gate", ACT.Sigmoid), ("forget_gate", ACT.Sigmoid), ("candidate", ACT.Tanh), ("out_gate", ACT.Sigmoid))
+GATES = (
+    ("forget_gate", 1, ACT.Sigmoid),
+    ("in_gate", 0, ACT.Sigmoid),
+    ("candidate", 2, ACT.Tanh),
+    ("out_gate", 3, ACT.Sigmoid),
+)
+LSTM_TILES = HALVES * FEATURE_TILES
+UNITS = LSTM_TILES * len(GATES)
+
+PLAIN_STEP = 3
+MX_STEP = 7
+ACT_STEP = 9
+TANH_LAG = 3
+FINISH_STEPS = 2 * ROW_TILES + 1
+FIRST_FINISH_DELAY = 6
 
 FLOPS = 2 * S * (4 * H) * D * DIRECTIONS + 2 * S * (4 * H) * H * DIRECTIONS + 2 * S * S * D
 
 
-def load_chunk(nc, pool, rows, name):
-    raw = pool.tile([P, ROW_TILES, rows.shape[1]], BF16, name=name)
-    nc.sync.dma_start(out=raw[:], in_=rows.rearrange("(a p) k -> p a k", p=P))
-    return raw
-
-
-def quantise_chunk(nc, psum, stage, raw, ident_f32, codes, scales):
-    grouped = stage.tile([P, CHUNK * PACK], BF16, tag="grouped", align_bytes=64)
-    grouped_words = grouped[:].bitcast(F32).rearrange("p (r u) -> p r u", u=2)
-    for pair in range(ROW_TILES // 2):
-        words_T = psum.tile([P, 2, 2 * P], F32, tag="flip")
-        for i in range(2):
-            raw_words = raw[:, 2 * pair + i, :].bitcast(F32)
-            for u in range(2):
-                nc.tensor.transpose(words_T[:, u, P * i : P * (i + 1)], raw_words[:, P * u : P * (u + 1)], ident_f32[:])
-        copy = nc.vector.tensor_copy if pair == 0 else nc.scalar.copy
-        copy(out=grouped_words[:, 2 * P * pair : 2 * P * (pair + 1), :], in_=words_T[:].rearrange("p u r -> p r u"))
-    nc.vector.quantize_mx(out=codes[:].bitcast(FP8X4), scales=scales[:], in_=grouped[:])
-
-
-def transpose_chunk(nc, psum, raw, ident_bf16, flipped):
-    for j in range(H_TILES):
-        flip = psum.tile([P, ROW_TILES, P], BF16, tag="flip")
-        for a in range(ROW_TILES):
-            nc.tensor.transpose(flip[:, a, :], raw[:, a, P * j : P * (j + 1)], ident_bf16[:])
-        copy = nc.vector.tensor_copy if j == 0 else nc.scalar.copy
-        copy(out=flipped[:, j, :], in_=flip[:].rearrange("p a r -> p (a r)"))
+def operand_chunks():
+    chunks = []
+    for n in range(HALVES):
+        for d in range(DIRECTIONS):
+            if n == 0:
+                chunks.extend([("whh", d, 0), ("whh", d, 1)])
+            chunks.append(("h0", d, n))
+            if n == 0 and d == 0:
+                chunks.append(("bias", 0, 0))
+            if n == 0:
+                chunks.append(("wih", d, 0))
+            if d == 0:
+                chunks.append(("y", 0, n))
+            if n == 0:
+                chunks.append(("wih", d, 1))
+            chunks.append(("c0", d, n))
+    chunks.append(("pair", 0, 0))
+    return chunks
 
 
 def tile_dependency_pb_kernel(
     tc, y, h0, c0, wih_f, whh_f, bih_f, bhh_f, wih_b, whh_b, bih_b, bhh_b, wd, fc_w, fc_b, out_0, out_1
 ):
     nc = tc.nc
-    wih = (wih_f, wih_b)
-    whh = (whh_f, whh_b)
     with ExitStack() as stack:
+        stack.enter_context(tc.manual_schedule())
         const = stack.enter_context(tc.tile_pool(name="const", bufs=1))
         raws = stack.enter_context(tc.tile_pool(name="raws", bufs=1))
         keep = stack.enter_context(tc.tile_pool(name="keep", bufs=1))
         stage = stack.enter_context(tc.tile_pool(name="stage", bufs=2))
-        sums = stack.enter_context(tc.tile_pool(name="sums", bufs=4))
+        sums = stack.enter_context(tc.tile_pool(name="sums", bufs=ACT_STEP - PLAIN_STEP + 2))
         work = stack.enter_context(tc.tile_pool(name="work", bufs=2))
-        outs = stack.enter_context(tc.tile_pool(name="outs", bufs=3))
+        outs = stack.enter_context(tc.tile_pool(name="outs", bufs=1))
         psum_flip = stack.enter_context(tc.psum_pool(name="psum_flip", bufs=2))
         psum_plain = stack.enter_context(tc.psum_pool(name="psum_plain", bufs=3))
         psum_mx = stack.enter_context(tc.psum_pool(name="psum_mx", bufs=3))
@@ -79,19 +84,6 @@ def tile_dependency_pb_kernel(
         make_identity(nc, ident_bf16[:])
         ident_f32 = const.tile([P, P], F32)
         make_identity(nc, ident_f32[:])
-
-        vector_rows = const.tile([P, P], BF16)
-        nc.vector.memset(vector_rows[:], 0.0)
-        row = 0
-        first_row = {}
-        for name, vec in (("bih0", bih_f), ("bhh0", bhh_f), ("bih1", bih_b), ("bhh1", bhh_b), ("wd", wd), ("fc_w", fc_w[0])):
-            n_rows = vec.shape[0] // P
-            nc.gpsimd.dma_start(out=vector_rows[row : row + n_rows, :], in_=vec.rearrange("(r c) -> r c", c=P))
-            first_row[name] = row
-            row += n_rows
-        fc_b_bf16 = const.tile([P, 1], BF16)
-        nc.gpsimd.dma_start(out=fc_b_bf16[:], in_=fc_b.partition_broadcast(P))
-
         on_or_above = const.tile([P, CHUNK], F32)
         nc.gpsimd.memset(on_or_above[:], 1.0)
         nc.gpsimd.affine_select(
@@ -106,143 +98,206 @@ def tile_dependency_pb_kernel(
         zeros = const.tile([P, S - P], F32)
         nc.vector.memset(zeros[:], 0.0)
 
-        y_codes, y_scales, wih_codes, wih_scales, whhT, h0T, c0T = {}, {}, {}, {}, {}, {}, {}
-
-        def prepare_weights(d):
-            for c in range(2):
-                whh_raw = load_chunk(nc, raws, whh[d][CHUNK * c : CHUNK * (c + 1), :], "whh_raw_%d_%d" % (d, c))
-                whhT[d, c] = keep.tile([P, H_TILES, CHUNK], BF16, name="whhT_%d_%d" % (d, c))
-                transpose_chunk(nc, psum_flip, whh_raw, ident_bf16, whhT[d, c])
-            for c in range(2):
-                wih_raw = load_chunk(nc, raws, wih[d][CHUNK * c : CHUNK * (c + 1), :], "wih_raw_%d_%d" % (d, c))
-                wih_codes[d, c] = keep.tile([P, CHUNK], U32, name="wih_codes_%d_%d" % (d, c), align_bytes=64)
-                wih_scales[d, c] = keep.tile([P, CHUNK], U8, name="wih_scales_%d_%d" % (d, c), align_bytes=64)
-                quantise_chunk(nc, psum_flip, stage, wih_raw, ident_f32, wih_codes[d, c], wih_scales[d, c])
-
-        def prepare_y(n):
-            y_raw = load_chunk(nc, raws, y[CHUNK * n : CHUNK * (n + 1), :], "y_raw_%d" % n)
-            y_codes[n] = keep.tile([P, CHUNK], U32, name="y_codes_%d" % n, align_bytes=64)
-            y_scales[n] = keep.tile([P, CHUNK], U8, name="y_scales_%d" % n, align_bytes=64)
-            quantise_chunk(nc, psum_flip, stage, y_raw, ident_f32, y_codes[n], y_scales[n])
-
-        def prepare_state(d, n):
-            for what, state, flipped in (("h0", h0, h0T), ("c0", c0, c0T)):
-                state_raw = load_chunk(nc, raws, state[d, CHUNK * n : CHUNK * (n + 1), :], "%s_raw_%d_%d" % (what, d, n))
-                flipped[d, n] = keep.tile([P, H_TILES, CHUNK], BF16, name="%sT_%d_%d" % (what, d, n))
-                transpose_chunk(nc, psum_flip, state_raw, ident_bf16, flipped[d, n])
-
-        prepare_weights(0)
-        prepare_y(0)
-        prepare_state(0, 0)
-
-        vector_cols_ps = psum_flip.tile([P, P], BF16, tag="flip")
-        nc.tensor.transpose(vector_cols_ps[:], vector_rows[:], ident_bf16[:])
-        vector_cols = const.tile([P, P], F32)
-        nc.vector.tensor_copy(out=vector_cols[:], in_=vector_cols_ps[:])
-        gate_tiles = 4 * H // P
-        bias = []
-        for d in range(DIRECTIONS):
-            bias_d = const.tile([P, gate_tiles], F32, name="bias_%d" % d)
-            ih, hh = first_row["bih%d" % d], first_row["bhh%d" % d]
-            nc.vector.tensor_tensor(
-                out=bias_d[:], in0=vector_cols[:, ih : ih + gate_tiles], in1=vector_cols[:, hh : hh + gate_tiles], op=ALU.add
-            )
-            bias.append(bias_d)
-        pair_weight = const.tile([P, FEATURE_TILES], F32)
-        nc.vector.tensor_tensor(
-            out=pair_weight[:],
-            in0=vector_cols[:, first_row["wd"] : first_row["wd"] + FEATURE_TILES],
-            in1=vector_cols[:, first_row["fc_w"] : first_row["fc_w"] + FEATURE_TILES],
-            op=ALU.mult,
-        )
-        fc_b_col = const.tile([P, 1], F32)
-        nc.vector.tensor_copy(out=fc_b_col[:], in_=fc_b_bf16[:])
-
-        prepare_weights(1)
-        prepare_state(1, 0)
-        prepare_y(1)
-        prepare_state(0, 1)
-        prepare_state(1, 1)
-
+        matrices = {"y": (y, y), "h0": (h0[0], h0[1]), "c0": (c0[0], c0[1]), "wih": (wih_f, wih_b), "whh": (whh_f, whh_b)}
+        vectors = {"bias": (bih_f, bhh_f, bih_b, bhh_b), "pair": (wd, fc_w[0])}
+        chunks = operand_chunks()
+        raw = {}
+        for chunk in chunks:
+            kind, d, c = chunk
+            if kind in vectors:
+                raw[chunk] = raws.tile([P, P], BF16, name="%s_rows" % kind)
+                nc.vector.memset(raw[chunk][:], 0.0)
+                row = 0
+                for vec in vectors[kind]:
+                    n_rows = vec.shape[0] // P
+                    nc.sync.dma_start(out=raw[chunk][row : row + n_rows, :], in_=vec.rearrange("(r c) -> r c", c=P))
+                    row += n_rows
+            else:
+                rows = matrices[kind][d][CHUNK * c : CHUNK * (c + 1), :]
+                raw[chunk] = raws.tile([P, ROW_TILES, rows.shape[1]], BF16, name="%s_raw_%d_%d" % chunk)
+                nc.sync.dma_start(out=raw[chunk][:], in_=rows.rearrange("(a p) k -> p a k", p=P))
+        fc_b_bf16 = const.tile([P, 1], BF16)
+        nc.sync.dma_start(out=fc_b_bf16[:], in_=fc_b.partition_broadcast(P))
         for r in range(1, S // P):
             nc.sync.dma_start(out=out_0[P * r : P * (r + 1), 0 : P * r], in_=zeros[:, 0 : P * r])
 
-        hid_codes, hid_scales, u_codes, u_scales = {}, {}, {}, {}
+        flipped = {}
+        grouped = {}
+        codes, scales = {}, {}
+        columns = {}
+        bias = const.tile([P, DIRECTIONS, GATE_TILES], F32)
+        pair_weight = const.tile([P, FEATURE_TILES], F32)
+        fc_b_col = const.tile([P, 1], F32)
 
-        def lstm_tile(n, d, j, hidT):
-            gate = {}
-            for q, (name, func) in enumerate(GATES):
-                g = H_TILES * q + j
-                c, cols = g // ROW_TILES, slice(P * (g % ROW_TILES), P * (g % ROW_TILES + 1))
-                recurrent_ps = psum_plain.tile([P, CHUNK], F32, tag="plain")
-                for k in range(H_TILES):
-                    nc.tensor.matmul(
-                        recurrent_ps[:], lhsT=whhT[d, c][:, k, cols], rhs=h0T[d, n][:, k, :], start=(k == 0), stop=(k == H_TILES - 1)
-                    )
-                input_ps = psum_mx.tile([P, CHUNK], F32, tag="mx")
-                nc.tensor.matmul_mx(
-                    out=input_ps[:],
-                    lhsT=wih_codes[d, c][:, cols].bitcast(FP8X4),
-                    lhsT_scale=wih_scales[d, c][:, cols],
-                    rhs=y_codes[n][:].bitcast(FP8X4),
-                    rhs_scale=y_scales[n][:],
-                    start=True,
-                    stop=True,
+        def flip_vectors(chunk):
+            kind = chunk[0]
+            cols_ps = psum_flip.tile([P, P], BF16, tag="flip")
+            nc.tensor.transpose(cols_ps[:], raw[chunk][:], ident_bf16[:])
+            cols = const.tile([P, P], F32, name="%s_cols" % kind)
+            nc.vector.tensor_copy(out=cols[:], in_=cols_ps[:])
+            if kind == "bias":
+                by_kind = cols[:, 0 : 2 * DIRECTIONS * GATE_TILES].rearrange("p (d i g) -> p d i g", d=DIRECTIONS, i=2)
+                nc.vector.tensor_tensor(out=bias[:], in0=by_kind[:, :, 0, :], in1=by_kind[:, :, 1, :], op=ALU.add)
+            else:
+                nc.vector.tensor_tensor(
+                    out=pair_weight[:], in0=cols[:, 0:FEATURE_TILES], in1=cols[:, FEATURE_TILES : 2 * FEATURE_TILES], op=ALU.mult
                 )
-                pre = sums.tile([P, CHUNK], F32, tag="pre")
-                nc.scalar.copy(out=pre[:], in_=recurrent_ps[:])
-                nc.vector.tensor_tensor(out=pre[:], in0=input_ps[:], in1=pre[:], op=ALU.add)
-                gate[name] = work.tile([P, CHUNK], F32, name=name, tag=name)
-                nc.scalar.activation(out=gate[name][:], in_=pre[:], func=func, bias=bias[d][:, g : g + 1], scale=1.0)
-            cell = work.tile([P, CHUNK], F32, tag="cell")
-            nc.vector.tensor_tensor(out=cell[:], in0=gate["forget_gate"][:], in1=c0T[d, n][:, j, :], op=ALU.mult)
-            fresh = work.tile([P, CHUNK], F32, tag="fresh")
-            nc.vector.tensor_tensor(out=fresh[:], in0=gate["in_gate"][:], in1=gate["candidate"][:], op=ALU.mult)
-            nc.vector.tensor_tensor(out=cell[:], in0=cell[:], in1=fresh[:], op=ALU.add)
-            tanh_cell = work.tile([P, CHUNK], F32, tag="tanh_cell")
-            nc.scalar.activation(out=tanh_cell[:], in_=cell[:], func=ACT.Tanh)
-            nc.vector.tensor_tensor(out=hidT[:, H_TILES * d + j, :], in0=gate["out_gate"][:], in1=tanh_cell[:], op=ALU.mult)
+                nc.vector.tensor_copy(out=fc_b_col[:], in_=fc_b_bf16[:])
 
-        def quantise_hid(n, hidT):
-            by_token = hidT[:].rearrange("p t r -> p r t")
-            hid_grouped = stage.tile([P, CHUNK, PACK], BF16, tag="hid_grouped", align_bytes=64)
-            nc.scalar.copy(out=hid_grouped[:], in_=by_token)
-            u_grouped = stage.tile([P, CHUNK, PACK], BF16, tag="u_grouped", align_bytes=64)
-            nc.vector.tensor_tensor(
-                out=u_grouped[:], in0=by_token, in1=pair_weight[:].unsqueeze(1).to_broadcast([P, CHUNK, PACK]), op=ALU.mult
+        def flip_bf16(chunk):
+            flipped[chunk] = keep.tile([P, H_TILES, CHUNK], BF16, name="%sT_%d_%d" % chunk)
+            for j in range(H_TILES):
+                flip = psum_flip.tile([P, ROW_TILES, P], BF16, tag="flip")
+                for a in range(ROW_TILES):
+                    nc.tensor.transpose(flip[:, a, :], raw[chunk][:, a, P * j : P * (j + 1)], ident_bf16[:])
+                nc.scalar.copy(out=flipped[chunk][:, j, :], in_=flip[:].rearrange("p a r -> p (a r)"))
+
+        def flip_words(chunk):
+            grouped[chunk] = stage.tile([P, CHUNK * PACK], BF16, tag="grouped", name="grouped_%s_%d_%d" % chunk, align_bytes=64)
+            grouped_words = grouped[chunk][:].bitcast(F32).rearrange("p (r u) -> p r u", u=2)
+            for pair in range(ROW_TILES // 2):
+                words_T = psum_flip.tile([P, 2, 2 * P], F32, tag="flip")
+                for i in range(2):
+                    raw_words = raw[chunk][:, 2 * pair + i, :].bitcast(F32)
+                    for u in range(2):
+                        nc.tensor.transpose(words_T[:, u, P * i : P * (i + 1)], raw_words[:, P * u : P * (u + 1)], ident_f32[:])
+                copy = nc.vector.tensor_copy if pair == 0 else nc.scalar.copy
+                copy(out=grouped_words[:, 2 * P * pair : 2 * P * (pair + 1), :], in_=words_T[:].rearrange("p u r -> p r u"))
+
+        def quantise(key, values):
+            codes[key] = keep.tile([P, CHUNK], U32, name="%s_codes_%d_%d" % key, align_bytes=64)
+            scales[key] = keep.tile([P, CHUNK], U8, name="%s_scales_%d_%d" % key, align_bytes=64)
+            nc.vector.quantize_mx(out=codes[key][:].bitcast(FP8X4), scales=scales[key][:], in_=values)
+
+        def flip_chunk(i):
+            if 0 <= i < len(chunks):
+                kind = chunks[i][0]
+                if kind in vectors:
+                    flip_vectors(chunks[i])
+                elif kind in ("wih", "y"):
+                    flip_words(chunks[i])
+                else:
+                    flip_bf16(chunks[i])
+
+        def quantise_chunk(i):
+            if 0 <= i < len(chunks) and chunks[i][0] in ("wih", "y"):
+                quantise(chunks[i], grouped[chunks[i]][:])
+
+        def place(u):
+            lstm_tile, which = divmod(u, len(GATES))
+            n, t = divmod(lstm_tile, FEATURE_TILES)
+            d, j = divmod(t, H_TILES)
+            name, q, func = GATES[which]
+            g = H_TILES * q + j
+            return n, d, j, name, func, g, g // ROW_TILES, slice(P * (g % ROW_TILES), P * (g % ROW_TILES + 1))
+
+        pre = {}
+        gate = {}
+
+        def plain_product(u):
+            if not 0 <= u < UNITS:
+                return
+            n, d, j, name, func, g, c, cols = place(u)
+            recurrent_ps = psum_plain.tile([P, CHUNK], F32, tag="plain")
+            for k in range(H_TILES):
+                nc.tensor.matmul(
+                    recurrent_ps[:],
+                    lhsT=flipped["whh", d, c][:, k, cols],
+                    rhs=flipped["h0", d, n][:, k, :],
+                    start=(k == 0),
+                    stop=(k == H_TILES - 1),
+                )
+            pre[u] = sums.tile([P, CHUNK], F32, tag="pre", name="pre_%d" % u)
+            copy = nc.vector.tensor_copy if name == "out_gate" else nc.scalar.copy
+            copy(out=pre[u][:], in_=recurrent_ps[:])
+
+        def input_product(u):
+            if not 0 <= u < UNITS:
+                return
+            n, d, j, name, func, g, c, cols = place(u)
+            input_ps = psum_mx.tile([P, CHUNK], F32, tag="mx")
+            nc.tensor.matmul_mx(
+                out=input_ps[:],
+                lhsT=codes["wih", d, c][:, cols].bitcast(FP8X4),
+                lhsT_scale=scales["wih", d, c][:, cols],
+                rhs=codes["y", 0, n][:].bitcast(FP8X4),
+                rhs_scale=scales["y", 0, n][:],
+                start=True,
+                stop=True,
             )
-            for what, grouped, codes, scales in (("hid", hid_grouped, hid_codes, hid_scales), ("u", u_grouped, u_codes, u_scales)):
-                codes[n] = keep.tile([P, CHUNK], U32, name="%s_codes_%d" % (what, n), align_bytes=64)
-                scales[n] = keep.tile([P, CHUNK], U8, name="%s_scales_%d" % (what, n), align_bytes=64)
-                nc.vector.quantize_mx(
-                    out=codes[n][:].bitcast(FP8X4), scales=scales[n][:], in_=grouped[:].rearrange("p r t -> p (r t)")
+            nc.vector.tensor_tensor(out=pre[u][:], in0=input_ps[:], in1=pre[u][:], op=ALU.add)
+
+        def activate(u):
+            if not 0 <= u < UNITS:
+                return
+            n, d, j, name, func, g, c, cols = place(u)
+            lstm_tile = u // len(GATES)
+            gate[lstm_tile, name] = work.tile([P, CHUNK], F32, tag=name, name="%s_%d" % (name, lstm_tile))
+            nc.scalar.activation(out=gate[lstm_tile, name][:], in_=pre[u][:], func=func, bias=bias[:, d, g : g + 1], scale=1.0)
+            if name == "forget_gate":
+                gate[lstm_tile, "cell"] = work.tile([P, CHUNK], F32, tag="cell", name="cell_%d" % lstm_tile)
+                nc.gpsimd.tensor_tensor(
+                    out=gate[lstm_tile, "cell"][:], in0=gate[lstm_tile, name][:], in1=flipped["c0", d, n][:, j, :], op=ALU.mult
+                )
+            if name == "candidate":
+                fresh = work.tile([P, CHUNK], F32, tag="fresh")
+                nc.gpsimd.tensor_tensor(out=fresh[:], in0=gate[lstm_tile, "in_gate"][:], in1=gate[lstm_tile, name][:], op=ALU.mult)
+                nc.gpsimd.tensor_tensor(out=gate[lstm_tile, "cell"][:], in0=gate[lstm_tile, "cell"][:], in1=fresh[:], op=ALU.add)
+
+        hidT = {}
+
+        def tanh_of_cell(lstm_tile):
+            if 0 <= lstm_tile < LSTM_TILES:
+                gate[lstm_tile, "tanh_cell"] = work.tile([P, CHUNK], F32, tag="tanh_cell", name="tanh_cell_%d" % lstm_tile)
+                nc.scalar.activation(out=gate[lstm_tile, "tanh_cell"][:], in_=gate[lstm_tile, "cell"][:], func=ACT.Tanh)
+
+        def hidden(lstm_tile):
+            if 0 <= lstm_tile < LSTM_TILES:
+                n, t = divmod(lstm_tile, FEATURE_TILES)
+                if t == 0:
+                    hidT[n] = keep.tile([P, FEATURE_TILES, CHUNK], F32, name="hidT_%d" % n)
+                nc.vector.tensor_tensor(
+                    out=hidT[n][:, t, :], in0=gate[lstm_tile, "out_gate"][:], in1=gate[lstm_tile, "tanh_cell"][:], op=ALU.mult
                 )
 
-        def store_hid(n, hidT):
-            for a in range(ROW_TILES):
-                hid_ps = psum_flip.tile([P, FEATURE_TILES, P], F32, tag="flip")
-                for t in range(FEATURE_TILES):
-                    nc.tensor.transpose(hid_ps[:, t, :], hidT[:, t, P * a : P * (a + 1)], ident_f32[:])
-                hid_rows = outs.tile([P, D], F32, tag="hid_rows")
-                nc.scalar.copy(out=hid_rows[:], in_=hid_ps[:].rearrange("p t c -> p (t c)"))
-                first = CHUNK * n + P * a
-                nc.sync.dma_start(out=out_1[0, first : first + P, :], in_=hid_rows[:])
+        def store_hid(lstm_tile):
+            if 0 <= lstm_tile < LSTM_TILES:
+                n, t = divmod(lstm_tile, FEATURE_TILES)
+                hid_ps = psum_flip.tile([P, ROW_TILES, P], F32, tag="flip")
+                for a in range(ROW_TILES):
+                    nc.tensor.transpose(hid_ps[:, a, :], hidT[n][:, t, P * a : P * (a + 1)], ident_f32[:])
+                hid_rows = outs.tile([P, ROW_TILES, P], F32, tag="hid_rows", bufs=3)
+                nc.vector.tensor_copy(out=hid_rows[:], in_=hid_ps[:])
+                nc.sync.dma_start(
+                    out=out_1[0, CHUNK * n : CHUNK * (n + 1), P * t : P * (t + 1)].rearrange("(a p) c -> p a c", p=P), in_=hid_rows[:]
+                )
+
+        def round_tokens(n, a):
+            if a == 0:
+                for what in ("hid", "u"):
+                    grouped[what, 0, n] = stage.tile([P, CHUNK, PACK], BF16, tag=what, name="grouped_%s_%d" % (what, n), align_bytes=64)
+            tokens = slice(P * a, P * (a + 1))
+            by_token = hidT[n][:, :, tokens].rearrange("p t r -> p r t")
+            nc.scalar.copy(out=grouped["hid", 0, n][:, tokens, :], in_=by_token)
+            nc.vector.tensor_tensor(
+                out=grouped["u", 0, n][:, tokens, :], in0=by_token, in1=pair_weight[:].unsqueeze(1).to_broadcast([P, P, PACK]), op=ALU.mult
+            )
 
         def score_piece(r, n):
             score_ps = psum_mx.tile([P, CHUNK], F32, tag="mx")
             u_cols = slice(P * (r % ROW_TILES), P * (r % ROW_TILES + 1))
             nc.tensor.matmul_mx(
                 out=score_ps[:],
-                lhsT=u_codes[r // ROW_TILES][:, u_cols].bitcast(FP8X4),
-                lhsT_scale=u_scales[r // ROW_TILES][:, u_cols],
-                rhs=hid_codes[n][:].bitcast(FP8X4),
-                rhs_scale=hid_scales[n][:],
+                lhsT=codes["u", 0, r // ROW_TILES][:, u_cols].bitcast(FP8X4),
+                lhsT_scale=scales["u", 0, r // ROW_TILES][:, u_cols],
+                rhs=codes["hid", 0, n][:].bitcast(FP8X4),
+                rhs_scale=scales["hid", 0, n][:],
                 start=True,
                 stop=True,
             )
             first = max(P * r - CHUNK * n, 0)
             width = CHUNK - first
-            piece = outs.tile([P, CHUNK], F32, tag="piece")
+            piece = outs.tile([P, CHUNK], F32, tag="piece", bufs=S // P)
             if P * r >= CHUNK * n:
                 nc.vector.scalar_tensor_tensor(
                     out=piece[:, 0:width],
@@ -252,16 +307,38 @@ def tile_dependency_pb_kernel(
                     op0=ALU.add,
                     op1=ALU.mult,
                 )
-            else:
+            elif r % 2 == 0:
                 nc.scalar.activation(out=piece[:], in_=score_ps[:], func=ACT.Identity, bias=fc_b_col[:, 0:1], scale=1.0)
+            else:
+                nc.vector.tensor_scalar(out=piece[:], in0=score_ps[:], scalar1=fc_b_col[:, 0:1], scalar2=None, op0=ALU.add)
             nc.sync.dma_start(out=out_0[P * r : P * (r + 1), CHUNK * n + first : CHUNK * (n + 1)], in_=piece[:, 0:width])
 
-        for n in range(HALVES):
-            hidT = keep.tile([P, FEATURE_TILES, CHUNK], F32, name="hidT_%d" % n)
-            for d in range(DIRECTIONS):
-                for j in range(H_TILES):
-                    lstm_tile(n, d, j, hidT)
-            quantise_hid(n, hidT)
-            store_hid(n, hidT)
-            for r in range(ROW_TILES * (n + 1)):
-                score_piece(r, n)
+        def finish_half(n, i):
+            if 0 <= i < ROW_TILES:
+                round_tokens(n, i)
+            if i == ROW_TILES:
+                for what in ("u", "hid"):
+                    quantise((what, 0, n), grouped[what, 0, n][:].rearrange("p r t -> p (r t)"))
+            if ROW_TILES < i < FINISH_STEPS:
+                a = i - ROW_TILES - 1
+                for m in range(n, -1, -1):
+                    score_piece(ROW_TILES * m + a, n)
+
+        candidate_step = ACT_STEP + 2
+        finish_step = [candidate_step + TANH_LAG + len(GATES) * (FEATURE_TILES * (n + 1) - 1) + 2 for n in range(HALVES)]
+        finish_step[0] += FIRST_FINISH_DELAY
+        for s in range(finish_step[-1] + FINISH_STEPS):
+            activate(s - ACT_STEP)
+            since_tanh, lstm_tile = (s - candidate_step - TANH_LAG) % len(GATES), (s - candidate_step - TANH_LAG) // len(GATES)
+            if since_tanh == 0:
+                tanh_of_cell(lstm_tile)
+            if since_tanh == 1:
+                hidden(lstm_tile)
+            if since_tanh == 2:
+                store_hid(lstm_tile)
+            plain_product(s - PLAIN_STEP)
+            quantise_chunk(s - 1)
+            input_product(s - MX_STEP)
+            flip_chunk(s)
+            for n in range(HALVES):
+                finish_half(n, s - finish_step[n])

@@ -13,32 +13,41 @@ ALU = mybir.AluOpType
 
 P = 128
 PACK = 4
+BANK = 512
 S = 1024
 H = 256
 D = 2 * H
+DIRECTIONS = 2
+H_TILES = H // P
+FEATURE_TILES = D // P
+GATE_TILES = 4 * H // P
 CHUNK = 512
 ROW_TILES = CHUNK // P
 HALVES = S // CHUNK
-H_TILES = H // P
-DIRECTIONS = 2
-FEATURE_TILES = DIRECTIONS * H_TILES
-GATE_TILES = 4 * H // P
+QUARTER = 256
+QUARTERS = S // QUARTER
+QUARTER_TILES = QUARTER // P
 
+LSTM_TILES = ((0, 0), (1, 0), (0, 1), (1, 1), (2, 0), (2, 1), (3, 0), (3, 1))
 GATES = (
     ("forget_gate", 1, ACT.Sigmoid),
     ("in_gate", 0, ACT.Sigmoid),
     ("candidate", 2, ACT.Tanh),
     ("out_gate", 3, ACT.Sigmoid),
 )
-LSTM_TILES = HALVES * FEATURE_TILES
-UNITS = LSTM_TILES * len(GATES)
+UNITS = len(LSTM_TILES) * len(GATES)
 
-PLAIN_STEP = 3
-MX_STEP = 7
-ACT_STEP = 9
-TANH_LAG = 3
-FINISH_STEPS = 2 * ROW_TILES + 1
-FIRST_FINISH_DELAY = 6
+PLAIN_STEP = 4
+MX_STEP = 8
+ADD_STEP = MX_STEP + 1
+ACT_STEP = ADD_STEP + 1
+TANH_STEP = 5
+HID_STEP = TANH_STEP + 1
+BACK_STEP = HID_STEP + 1
+STORE_STEP = BACK_STEP + 1
+ROUND_STEP = 1
+QUANTISE_STEP = ROUND_STEP + QUARTER_TILES
+SCORE_STEP = QUANTISE_STEP + 1
 
 FLOPS = 2 * S * (4 * H) * D * DIRECTIONS + 2 * S * (4 * H) * H * DIRECTIONS + 2 * S * S * D
 
@@ -72,30 +81,30 @@ def tile_dependency_pb_kernel(
         const = stack.enter_context(tc.tile_pool(name="const", bufs=1))
         raws = stack.enter_context(tc.tile_pool(name="raws", bufs=1))
         keep = stack.enter_context(tc.tile_pool(name="keep", bufs=1))
-        stage = stack.enter_context(tc.tile_pool(name="stage", bufs=2))
-        sums = stack.enter_context(tc.tile_pool(name="sums", bufs=ACT_STEP - PLAIN_STEP + 2))
+        stage = stack.enter_context(tc.tile_pool(name="stage", bufs=3))
+        sums = stack.enter_context(tc.tile_pool(name="sums", bufs=ACT_STEP - PLAIN_STEP + 1))
         work = stack.enter_context(tc.tile_pool(name="work", bufs=2))
-        outs = stack.enter_context(tc.tile_pool(name="outs", bufs=1))
-        psum_flip = stack.enter_context(tc.psum_pool(name="psum_flip", bufs=2))
-        psum_plain = stack.enter_context(tc.psum_pool(name="psum_plain", bufs=3))
+        outs = stack.enter_context(tc.tile_pool(name="outs", bufs=4))
+        psum_flip = stack.enter_context(tc.psum_pool(name="psum_flip", bufs=3))
+        psum_plain = stack.enter_context(tc.psum_pool(name="psum_plain", bufs=2))
         psum_mx = stack.enter_context(tc.psum_pool(name="psum_mx", bufs=3))
 
         ident_bf16 = const.tile([P, P], BF16)
         make_identity(nc, ident_bf16[:])
         ident_f32 = const.tile([P, P], F32)
         make_identity(nc, ident_f32[:])
-        on_or_above = const.tile([P, CHUNK], F32)
+        on_or_above = const.tile([P, QUARTER_TILES, QUARTER], F32)
         nc.gpsimd.memset(on_or_above[:], 1.0)
         nc.gpsimd.affine_select(
             out=on_or_above[:],
             in_=on_or_above[:],
-            pattern=[[1, CHUNK]],
+            pattern=[[-P, QUARTER_TILES], [1, QUARTER]],
             compare_op=ALU.is_ge,
             fill=0.0,
             base=0,
             channel_multiplier=-1,
         )
-        zeros = const.tile([P, S - P], F32)
+        zeros = const.tile([P, S - QUARTER], F32)
         nc.vector.memset(zeros[:], 0.0)
 
         matrices = {"y": (y, y), "h0": (h0[0], h0[1]), "c0": (c0[0], c0[1]), "wih": (wih_f, wih_b), "whh": (whh_f, whh_b)}
@@ -118,227 +127,252 @@ def tile_dependency_pb_kernel(
                 nc.sync.dma_start(out=raw[chunk][:], in_=rows.rearrange("(a p) k -> p a k", p=P))
         fc_b_bf16 = const.tile([P, 1], BF16)
         nc.sync.dma_start(out=fc_b_bf16[:], in_=fc_b.partition_broadcast(P))
-        for r in range(1, S // P):
-            nc.sync.dma_start(out=out_0[P * r : P * (r + 1), 0 : P * r], in_=zeros[:, 0 : P * r])
+        for r in range(QUARTER_TILES, S // P):
+            width = QUARTER * (r // QUARTER_TILES)
+            nc.sync.dma_start(out=out_0[P * r : P * (r + 1), 0:width], in_=zeros[:, 0:width])
 
+        flips = {}
         flipped = {}
         grouped = {}
         codes, scales = {}, {}
-        columns = {}
         bias = const.tile([P, DIRECTIONS, GATE_TILES], F32)
         pair_weight = const.tile([P, FEATURE_TILES], F32)
         fc_b_col = const.tile([P, 1], F32)
 
-        def flip_vectors(chunk):
-            kind = chunk[0]
-            cols_ps = psum_flip.tile([P, P], BF16, tag="flip")
-            nc.tensor.transpose(cols_ps[:], raw[chunk][:], ident_bf16[:])
-            cols = const.tile([P, P], F32, name="%s_cols" % kind)
-            nc.vector.tensor_copy(out=cols[:], in_=cols_ps[:])
-            if kind == "bias":
-                by_kind = cols[:, 0 : 2 * DIRECTIONS * GATE_TILES].rearrange("p (d i g) -> p d i g", d=DIRECTIONS, i=2)
-                nc.vector.tensor_tensor(out=bias[:], in0=by_kind[:, :, 0, :], in1=by_kind[:, :, 1, :], op=ALU.add)
-            else:
-                nc.vector.tensor_tensor(
-                    out=pair_weight[:], in0=cols[:, 0:FEATURE_TILES], in1=cols[:, FEATURE_TILES : 2 * FEATURE_TILES], op=ALU.mult
-                )
-                nc.vector.tensor_copy(out=fc_b_col[:], in_=fc_b_bf16[:])
-
-        def flip_bf16(chunk):
-            flipped[chunk] = keep.tile([P, H_TILES, CHUNK], BF16, name="%sT_%d_%d" % chunk)
-            for j in range(H_TILES):
-                flip = psum_flip.tile([P, ROW_TILES, P], BF16, tag="flip")
-                for a in range(ROW_TILES):
-                    nc.tensor.transpose(flip[:, a, :], raw[chunk][:, a, P * j : P * (j + 1)], ident_bf16[:])
-                nc.scalar.copy(out=flipped[chunk][:, j, :], in_=flip[:].rearrange("p a r -> p (a r)"))
-
-        def flip_words(chunk):
-            grouped[chunk] = stage.tile([P, CHUNK * PACK], BF16, tag="grouped", name="grouped_%s_%d_%d" % chunk, align_bytes=64)
-            grouped_words = grouped[chunk][:].bitcast(F32).rearrange("p (r u) -> p r u", u=2)
-            for pair in range(ROW_TILES // 2):
-                words_T = psum_flip.tile([P, 2, 2 * P], F32, tag="flip")
-                for i in range(2):
-                    raw_words = raw[chunk][:, 2 * pair + i, :].bitcast(F32)
-                    for u in range(2):
-                        nc.tensor.transpose(words_T[:, u, P * i : P * (i + 1)], raw_words[:, P * u : P * (u + 1)], ident_f32[:])
-                copy = nc.vector.tensor_copy if pair == 0 else nc.scalar.copy
-                copy(out=grouped_words[:, 2 * P * pair : 2 * P * (pair + 1), :], in_=words_T[:].rearrange("p u r -> p r u"))
-
-        def quantise(key, values):
-            codes[key] = keep.tile([P, CHUNK], U32, name="%s_codes_%d_%d" % key, align_bytes=64)
-            scales[key] = keep.tile([P, CHUNK], U8, name="%s_scales_%d_%d" % key, align_bytes=64)
-            nc.vector.quantize_mx(out=codes[key][:].bitcast(FP8X4), scales=scales[key][:], in_=values)
-
         def flip_chunk(i):
-            if 0 <= i < len(chunks):
-                kind = chunks[i][0]
-                if kind in vectors:
-                    flip_vectors(chunks[i])
-                elif kind in ("wih", "y"):
-                    flip_words(chunks[i])
+            if not 0 <= i < len(chunks):
+                return
+            chunk = chunks[i]
+            kind = chunk[0]
+            if kind in vectors:
+                cols_ps = psum_flip.tile([P, P], BF16, tag="flip", name="flip_%s" % kind)
+                nc.tensor.transpose(cols_ps[:], raw[chunk][:], ident_bf16[:])
+                flips[chunk] = [cols_ps]
+            elif kind in ("wih", "y"):
+                flips[chunk] = []
+                for pair in range(ROW_TILES // 2):
+                    words_T = psum_flip.tile([P, 2, 2 * P], F32, tag="flip", name="flip_%s_%d_%d_%d" % (chunk + (pair,)))
+                    for i2 in range(2):
+                        raw_words = raw[chunk][:, 2 * pair + i2, :].bitcast(F32)
+                        for u in range(2):
+                            nc.tensor.transpose(words_T[:, u, P * i2 : P * (i2 + 1)], raw_words[:, P * u : P * (u + 1)], ident_f32[:])
+                    flips[chunk].append(words_T)
+            else:
+                flips[chunk] = []
+                for j in range(H_TILES):
+                    flip = psum_flip.tile([P, ROW_TILES, P], BF16, tag="flip", name="flip_%s_%d_%d_%d" % (chunk + (j,)))
+                    for a in range(ROW_TILES):
+                        nc.tensor.transpose(flip[:, a, :], raw[chunk][:, a, P * j : P * (j + 1)], ident_bf16[:])
+                    flips[chunk].append(flip)
+
+        def save_chunk(i):
+            if not 0 <= i < len(chunks):
+                return
+            chunk = chunks[i]
+            kind = chunk[0]
+            copies = (nc.vector.tensor_copy, nc.scalar.copy)
+            if kind in vectors:
+                cols = const.tile([P, P], F32, name="%s_cols" % kind)
+                nc.vector.tensor_copy(out=cols[:], in_=flips[chunk][0][:])
+                if kind == "bias":
+                    by_kind = cols[:, 0 : 2 * DIRECTIONS * GATE_TILES].rearrange("p (d i g) -> p d i g", d=DIRECTIONS, i=2)
+                    nc.vector.tensor_tensor(out=bias[:], in0=by_kind[:, :, 0, :], in1=by_kind[:, :, 1, :], op=ALU.add)
                 else:
-                    flip_bf16(chunks[i])
+                    nc.vector.tensor_tensor(
+                        out=pair_weight[:], in0=cols[:, 0:FEATURE_TILES], in1=cols[:, FEATURE_TILES : 2 * FEATURE_TILES], op=ALU.mult
+                    )
+                    nc.vector.tensor_copy(out=fc_b_col[:], in_=fc_b_bf16[:])
+            elif kind in ("wih", "y"):
+                grouped[chunk] = stage.tile([P, CHUNK * PACK], BF16, tag="grouped", name="grouped_%s_%d_%d" % chunk, align_bytes=64)
+                grouped_words = grouped[chunk][:].bitcast(F32).rearrange("p (r u) -> p r u", u=2)
+                for pair in range(ROW_TILES // 2):
+                    copies[pair](
+                        out=grouped_words[:, 2 * P * pair : 2 * P * (pair + 1), :], in_=flips[chunk][pair][:].rearrange("p u r -> p r u")
+                    )
+            else:
+                flipped[chunk] = keep.tile([P, H_TILES, CHUNK], BF16, name="%sT_%d_%d" % chunk)
+                for j in range(H_TILES):
+                    copies[j](out=flipped[chunk][:, j, :], in_=flips[chunk][j][:].rearrange("p a r -> p (a r)"))
+
+        def quantise(key, values, width):
+            codes[key] = keep.tile([P, width], U32, name="%s_codes_%d_%d" % key, align_bytes=64)
+            scales[key] = keep.tile([P, width], U8, name="%s_scales_%d_%d" % key, align_bytes=64)
+            nc.vector.quantize_mx(out=codes[key][:].bitcast(FP8X4), scales=scales[key][:], in_=values)
 
         def quantise_chunk(i):
             if 0 <= i < len(chunks) and chunks[i][0] in ("wih", "y"):
-                quantise(chunks[i], grouped[chunks[i]][:])
+                quantise(chunks[i], grouped[chunks[i]][:], CHUNK)
 
         def place(u):
             lstm_tile, which = divmod(u, len(GATES))
-            n, t = divmod(lstm_tile, FEATURE_TILES)
-            d, j = divmod(t, H_TILES)
-            name, q, func = GATES[which]
-            g = H_TILES * q + j
-            return n, d, j, name, func, g, g // ROW_TILES, slice(P * (g % ROW_TILES), P * (g % ROW_TILES + 1))
+            quarter, d = LSTM_TILES[lstm_tile]
+            n, in_half = divmod(quarter, QUARTERS // HALVES)
+            return lstm_tile, d, n, slice(QUARTER * in_half, QUARTER * (in_half + 1)), GATES[which]
 
+        def gate_rows(q, j):
+            g = H_TILES * q + j
+            return g, g // ROW_TILES, slice(P * (g % ROW_TILES), P * (g % ROW_TILES + 1))
+
+        plain_ps, input_ps = {}, {}
         pre = {}
         gate = {}
 
         def plain_product(u):
             if not 0 <= u < UNITS:
                 return
-            n, d, j, name, func, g, c, cols = place(u)
-            recurrent_ps = psum_plain.tile([P, CHUNK], F32, tag="plain")
-            for k in range(H_TILES):
-                nc.tensor.matmul(
-                    recurrent_ps[:],
-                    lhsT=flipped["whh", d, c][:, k, cols],
-                    rhs=flipped["h0", d, n][:, k, :],
-                    start=(k == 0),
-                    stop=(k == H_TILES - 1),
-                )
-            pre[u] = sums.tile([P, CHUNK], F32, tag="pre", name="pre_%d" % u)
-            copy = nc.vector.tensor_copy if name == "out_gate" else nc.scalar.copy
-            copy(out=pre[u][:], in_=recurrent_ps[:])
+            lstm_tile, d, n, tokens, (name, q, func) = place(u)
+            plain_ps[u] = psum_plain.tile([P, H_TILES, QUARTER], F32, tag="plain", name="plain_%d" % u)
+            for j in range(H_TILES):
+                g, c, cols = gate_rows(q, j)
+                for k in range(H_TILES):
+                    nc.tensor.matmul(
+                        plain_ps[u][:, j, :],
+                        lhsT=flipped["whh", d, c][:, k, cols],
+                        rhs=flipped["h0", d, n][:, k, tokens],
+                        start=(k == 0),
+                        stop=(k == H_TILES - 1),
+                    )
+
+        def save_plain(u):
+            if not 0 <= u < UNITS:
+                return
+            pre[u] = sums.tile([P, H_TILES, QUARTER], F32, tag="pre", name="pre_%d" % u)
+            copy = nc.vector.tensor_copy if place(u)[4][0] == "out_gate" else nc.scalar.copy
+            copy(out=pre[u][:], in_=plain_ps[u][:])
 
         def input_product(u):
             if not 0 <= u < UNITS:
                 return
-            n, d, j, name, func, g, c, cols = place(u)
-            input_ps = psum_mx.tile([P, CHUNK], F32, tag="mx")
-            nc.tensor.matmul_mx(
-                out=input_ps[:],
-                lhsT=codes["wih", d, c][:, cols].bitcast(FP8X4),
-                lhsT_scale=scales["wih", d, c][:, cols],
-                rhs=codes["y", 0, n][:].bitcast(FP8X4),
-                rhs_scale=scales["y", 0, n][:],
-                start=True,
-                stop=True,
-            )
-            nc.vector.tensor_tensor(out=pre[u][:], in0=input_ps[:], in1=pre[u][:], op=ALU.add)
+            lstm_tile, d, n, tokens, (name, q, func) = place(u)
+            input_ps[u] = psum_mx.tile([P, H_TILES, QUARTER], F32, tag="mx", name="input_%d" % u)
+            for j in range(H_TILES):
+                g, c, cols = gate_rows(q, j)
+                nc.tensor.matmul_mx(
+                    out=input_ps[u][:, j, :],
+                    lhsT=codes["wih", d, c][:, cols].bitcast(FP8X4),
+                    lhsT_scale=scales["wih", d, c][:, cols],
+                    rhs=codes["y", 0, n][:, tokens].bitcast(FP8X4),
+                    rhs_scale=scales["y", 0, n][:, tokens],
+                    start=True,
+                    stop=True,
+                )
+
+        def add_products(u):
+            if 0 <= u < UNITS:
+                nc.vector.tensor_tensor(out=pre[u][:], in0=input_ps[u][:], in1=pre[u][:], op=ALU.add)
 
         def activate(u):
             if not 0 <= u < UNITS:
                 return
-            n, d, j, name, func, g, c, cols = place(u)
-            lstm_tile = u // len(GATES)
-            gate[lstm_tile, name] = work.tile([P, CHUNK], F32, tag=name, name="%s_%d" % (name, lstm_tile))
-            nc.scalar.activation(out=gate[lstm_tile, name][:], in_=pre[u][:], func=func, bias=bias[:, d, g : g + 1], scale=1.0)
+            lstm_tile, d, n, tokens, (name, q, func) = place(u)
+            gate[lstm_tile, name] = work.tile([P, H_TILES, QUARTER], F32, tag=name, name="%s_%d" % (name, lstm_tile))
+            for j in range(H_TILES):
+                g = gate_rows(q, j)[0]
+                nc.scalar.activation(out=gate[lstm_tile, name][:, j, :], in_=pre[u][:, j, :], func=func, bias=bias[:, d, g : g + 1], scale=1.0)
             if name == "forget_gate":
-                gate[lstm_tile, "cell"] = work.tile([P, CHUNK], F32, tag="cell", name="cell_%d" % lstm_tile)
+                gate[lstm_tile, "cell"] = work.tile([P, H_TILES, QUARTER], F32, tag="cell", name="cell_%d" % lstm_tile)
                 nc.gpsimd.tensor_tensor(
-                    out=gate[lstm_tile, "cell"][:], in0=gate[lstm_tile, name][:], in1=flipped["c0", d, n][:, j, :], op=ALU.mult
+                    out=gate[lstm_tile, "cell"][:], in0=gate[lstm_tile, name][:], in1=flipped["c0", d, n][:, :, tokens], op=ALU.mult
                 )
             if name == "candidate":
-                fresh = work.tile([P, CHUNK], F32, tag="fresh")
+                fresh = work.tile([P, H_TILES, QUARTER], F32, tag="fresh")
                 nc.gpsimd.tensor_tensor(out=fresh[:], in0=gate[lstm_tile, "in_gate"][:], in1=gate[lstm_tile, name][:], op=ALU.mult)
                 nc.gpsimd.tensor_tensor(out=gate[lstm_tile, "cell"][:], in0=gate[lstm_tile, "cell"][:], in1=fresh[:], op=ALU.add)
 
         hidT = {}
+        hid_ps = {}
 
-        def tanh_of_cell(lstm_tile):
-            if 0 <= lstm_tile < LSTM_TILES:
-                gate[lstm_tile, "tanh_cell"] = work.tile([P, CHUNK], F32, tag="tanh_cell", name="tanh_cell_%d" % lstm_tile)
+        def finish_tile(lstm_tile, i):
+            if not 0 <= lstm_tile < len(LSTM_TILES):
+                return
+            quarter, d = LSTM_TILES[lstm_tile]
+            own = slice(H_TILES * d, H_TILES * (d + 1))
+            if i == TANH_STEP:
+                gate[lstm_tile, "tanh_cell"] = work.tile([P, H_TILES, QUARTER], F32, tag="tanh_cell", name="tanh_cell_%d" % lstm_tile)
                 nc.scalar.activation(out=gate[lstm_tile, "tanh_cell"][:], in_=gate[lstm_tile, "cell"][:], func=ACT.Tanh)
-
-        def hidden(lstm_tile):
-            if 0 <= lstm_tile < LSTM_TILES:
-                n, t = divmod(lstm_tile, FEATURE_TILES)
-                if t == 0:
-                    hidT[n] = keep.tile([P, FEATURE_TILES, CHUNK], F32, name="hidT_%d" % n)
+            if i == HID_STEP:
+                if d == 0:
+                    hidT[quarter] = keep.tile([P, FEATURE_TILES, QUARTER], F32, name="hidT_%d" % quarter)
                 nc.vector.tensor_tensor(
-                    out=hidT[n][:, t, :], in0=gate[lstm_tile, "out_gate"][:], in1=gate[lstm_tile, "tanh_cell"][:], op=ALU.mult
+                    out=hidT[quarter][:, own, :], in0=gate[lstm_tile, "out_gate"][:], in1=gate[lstm_tile, "tanh_cell"][:], op=ALU.mult
                 )
-
-        def store_hid(lstm_tile):
-            if 0 <= lstm_tile < LSTM_TILES:
-                n, t = divmod(lstm_tile, FEATURE_TILES)
-                hid_ps = psum_flip.tile([P, ROW_TILES, P], F32, tag="flip")
-                for a in range(ROW_TILES):
-                    nc.tensor.transpose(hid_ps[:, a, :], hidT[n][:, t, P * a : P * (a + 1)], ident_f32[:])
-                hid_rows = outs.tile([P, ROW_TILES, P], F32, tag="hid_rows", bufs=3)
-                nc.vector.tensor_copy(out=hid_rows[:], in_=hid_ps[:])
+            if i == BACK_STEP:
+                hid_ps[lstm_tile] = psum_flip.tile([P, QUARTER_TILES, H_TILES, P], F32, tag="flip", name="hid_ps_%d" % lstm_tile)
+                for a in range(QUARTER_TILES):
+                    for j in range(H_TILES):
+                        nc.tensor.transpose(hid_ps[lstm_tile][:, a, j, :], hidT[quarter][:, H_TILES * d + j, P * a : P * (a + 1)], ident_f32[:])
+            if i == STORE_STEP:
+                hid_rows = outs.tile([P, QUARTER_TILES, H], F32, tag="hid_rows")
+                nc.vector.tensor_copy(out=hid_rows[:], in_=hid_ps[lstm_tile][:].rearrange("p a j c -> p a (j c)"))
                 nc.sync.dma_start(
-                    out=out_1[0, CHUNK * n : CHUNK * (n + 1), P * t : P * (t + 1)].rearrange("(a p) c -> p a c", p=P), in_=hid_rows[:]
+                    out=out_1[0, QUARTER * quarter : QUARTER * (quarter + 1), H * d : H * (d + 1)].rearrange("(a p) f -> p a f", p=P),
+                    in_=hid_rows[:],
                 )
 
-        def round_tokens(n, a):
-            if a == 0:
-                for what in ("hid", "u"):
-                    grouped[what, 0, n] = stage.tile([P, CHUNK, PACK], BF16, tag=what, name="grouped_%s_%d" % (what, n), align_bytes=64)
-            tokens = slice(P * a, P * (a + 1))
-            by_token = hidT[n][:, :, tokens].rearrange("p t r -> p r t")
-            nc.scalar.copy(out=grouped["hid", 0, n][:, tokens, :], in_=by_token)
-            nc.vector.tensor_tensor(
-                out=grouped["u", 0, n][:, tokens, :], in0=by_token, in1=pair_weight[:].unsqueeze(1).to_broadcast([P, P, PACK]), op=ALU.mult
-            )
+        score_ps = {}
 
-        def score_piece(r, n):
-            score_ps = psum_mx.tile([P, CHUNK], F32, tag="mx")
-            u_cols = slice(P * (r % ROW_TILES), P * (r % ROW_TILES + 1))
-            nc.tensor.matmul_mx(
-                out=score_ps[:],
-                lhsT=codes["u", 0, r // ROW_TILES][:, u_cols].bitcast(FP8X4),
-                lhsT_scale=scales["u", 0, r // ROW_TILES][:, u_cols],
-                rhs=codes["hid", 0, n][:].bitcast(FP8X4),
-                rhs_scale=scales["hid", 0, n][:],
-                start=True,
-                stop=True,
-            )
-            first = max(P * r - CHUNK * n, 0)
-            width = CHUNK - first
-            piece = outs.tile([P, CHUNK], F32, tag="piece", bufs=S // P)
-            if P * r >= CHUNK * n:
-                nc.vector.scalar_tensor_tensor(
-                    out=piece[:, 0:width],
-                    in0=score_ps[:, first:CHUNK],
-                    scalar=fc_b_col[:, 0:1],
-                    in1=on_or_above[:, 0:width],
-                    op0=ALU.add,
-                    op1=ALU.mult,
+        def finish_quarter(quarter, i):
+            if ROUND_STEP <= i < QUANTISE_STEP:
+                if i == ROUND_STEP:
+                    for what in ("hid", "u"):
+                        grouped[what, 0, quarter] = stage.tile(
+                            [P, QUARTER, PACK], BF16, tag=what, name="grouped_%s_%d" % (what, quarter), align_bytes=64, bufs=2
+                        )
+                tokens = slice(P * (i - ROUND_STEP), P * (i - ROUND_STEP + 1))
+                by_token = hidT[quarter][:, :, tokens].rearrange("p t r -> p r t")
+                nc.scalar.copy(out=grouped["hid", 0, quarter][:, tokens, :], in_=by_token)
+                nc.vector.tensor_tensor(
+                    out=grouped["u", 0, quarter][:, tokens, :],
+                    in0=by_token,
+                    in1=pair_weight[:].unsqueeze(1).to_broadcast([P, P, PACK]),
+                    op=ALU.mult,
                 )
-            elif r % 2 == 0:
-                nc.scalar.activation(out=piece[:], in_=score_ps[:], func=ACT.Identity, bias=fc_b_col[:, 0:1], scale=1.0)
-            else:
-                nc.vector.tensor_scalar(out=piece[:], in0=score_ps[:], scalar1=fc_b_col[:, 0:1], scalar2=None, op0=ALU.add)
-            nc.sync.dma_start(out=out_0[P * r : P * (r + 1), CHUNK * n + first : CHUNK * (n + 1)], in_=piece[:, 0:width])
-
-        def finish_half(n, i):
-            if 0 <= i < ROW_TILES:
-                round_tokens(n, i)
-            if i == ROW_TILES:
+            if i == QUANTISE_STEP:
                 for what in ("u", "hid"):
-                    quantise((what, 0, n), grouped[what, 0, n][:].rearrange("p r t -> p (r t)"))
-            if ROW_TILES < i < FINISH_STEPS:
-                a = i - ROW_TILES - 1
-                for m in range(n, -1, -1):
-                    score_piece(ROW_TILES * m + a, n)
+                    quantise((what, 0, quarter), grouped[what, 0, quarter][:].rearrange("p r t -> p (r t)"), QUARTER)
+            rows = quarter - (i - SCORE_STEP)
+            if i >= SCORE_STEP and rows >= 0:
+                score_ps[rows, quarter] = psum_mx.tile([P, QUARTER_TILES, QUARTER], F32, tag="mx", name="score_%d_%d" % (rows, quarter))
+                for a in range(QUARTER_TILES):
+                    nc.tensor.matmul_mx(
+                        out=score_ps[rows, quarter][:, a, :],
+                        lhsT=codes["u", 0, rows][:, P * a : P * (a + 1)].bitcast(FP8X4),
+                        lhsT_scale=scales["u", 0, rows][:, P * a : P * (a + 1)],
+                        rhs=codes["hid", 0, quarter][:].bitcast(FP8X4),
+                        rhs_scale=scales["hid", 0, quarter][:],
+                        start=True,
+                        stop=True,
+                    )
+            rows += 1
+            if i > SCORE_STEP and 0 <= rows <= quarter:
+                piece = outs.tile([P, QUARTER_TILES, QUARTER], F32, tag="piece")
+                if rows == quarter:
+                    nc.vector.scalar_tensor_tensor(
+                        out=piece[:], in0=score_ps[rows, quarter][:], scalar=fc_b_col[:, 0:1], in1=on_or_above[:], op0=ALU.add, op1=ALU.mult
+                    )
+                elif rows % 2 == 0:
+                    nc.scalar.activation(out=piece[:], in_=score_ps[rows, quarter][:], func=ACT.Identity, bias=fc_b_col[:, 0:1], scale=1.0)
+                else:
+                    nc.vector.tensor_scalar(out=piece[:], in0=score_ps[rows, quarter][:], scalar1=fc_b_col[:, 0:1], scalar2=None, op0=ALU.add)
+                nc.sync.dma_start(
+                    out=out_0[QUARTER * rows : QUARTER * (rows + 1), QUARTER * quarter : QUARTER * (quarter + 1)].rearrange(
+                        "(a p) c -> p a c", p=P
+                    ),
+                    in_=piece[:],
+                )
 
-        candidate_step = ACT_STEP + 2
-        finish_step = [candidate_step + TANH_LAG + len(GATES) * (FEATURE_TILES * (n + 1) - 1) + 2 for n in range(HALVES)]
-        finish_step[0] += FIRST_FINISH_DELAY
-        for s in range(finish_step[-1] + FINISH_STEPS):
+        first_act = [ACT_STEP + len(GATES) * lstm_tile for lstm_tile in range(len(LSTM_TILES))]
+        quarter_done = [first_act[LSTM_TILES.index((quarter, 1))] + HID_STEP for quarter in range(QUARTERS)]
+        for s in range(quarter_done[-1] + SCORE_STEP + QUARTERS + 1):
+            save_plain(s - PLAIN_STEP - 1)
+            add_products(s - ADD_STEP)
+            save_chunk(s - 1)
+            quantise_chunk(s - 2)
             activate(s - ACT_STEP)
-            since_tanh, lstm_tile = (s - candidate_step - TANH_LAG) % len(GATES), (s - candidate_step - TANH_LAG) // len(GATES)
-            if since_tanh == 0:
-                tanh_of_cell(lstm_tile)
-            if since_tanh == 1:
-                hidden(lstm_tile)
-            if since_tanh == 2:
-                store_hid(lstm_tile)
             plain_product(s - PLAIN_STEP)
-            quantise_chunk(s - 1)
             input_product(s - MX_STEP)
+            for lstm_tile in range(len(LSTM_TILES)):
+                finish_tile(lstm_tile, s - first_act[lstm_tile])
+            for quarter in range(QUARTERS):
+                finish_quarter(quarter, s - quarter_done[quarter])
             flip_chunk(s)
-            for n in range(HALVES):
-                finish_half(n, s - finish_step[n])

@@ -41,12 +41,12 @@ PLAIN_STEP = 4
 MX_STEP = 8
 ADD_STEP = MX_STEP + 1
 ACT_STEP = ADD_STEP + 1
-TANH_STEP = 5
+TANH_STEP = 6
 HID_STEP = TANH_STEP + 1
-BACK_STEP = HID_STEP + 1
+BACK_STEP = HID_STEP + 3
 STORE_STEP = BACK_STEP + 1
 ROUND_STEP = 1
-QUANTISE_STEP = ROUND_STEP + QUARTER_TILES
+QUANTISE_STEP = ROUND_STEP + 1
 SCORE_STEP = QUANTISE_STEP + 1
 
 FLOPS = 2 * S * (4 * H) * D * DIRECTIONS + 2 * S * (4 * H) * H * DIRECTIONS + 2 * S * S * D
@@ -85,9 +85,7 @@ def tile_dependency_pb_kernel(
         sums = stack.enter_context(tc.tile_pool(name="sums", bufs=ACT_STEP - PLAIN_STEP + 1))
         work = stack.enter_context(tc.tile_pool(name="work", bufs=2))
         outs = stack.enter_context(tc.tile_pool(name="outs", bufs=4))
-        psum_flip = stack.enter_context(tc.psum_pool(name="psum_flip", bufs=3))
-        psum_plain = stack.enter_context(tc.psum_pool(name="psum_plain", bufs=2))
-        psum_mx = stack.enter_context(tc.psum_pool(name="psum_mx", bufs=3))
+        psum = stack.enter_context(tc.psum_pool(name="psum", bufs=8))
 
         ident_bf16 = const.tile([P, P], BF16)
         make_identity(nc, ident_bf16[:])
@@ -145,13 +143,13 @@ def tile_dependency_pb_kernel(
             chunk = chunks[i]
             kind = chunk[0]
             if kind in vectors:
-                cols_ps = psum_flip.tile([P, P], BF16, tag="flip", name="flip_%s" % kind)
+                cols_ps = psum.tile([P, P], BF16, tag="bank", name="flip_%s" % kind)
                 nc.tensor.transpose(cols_ps[:], raw[chunk][:], ident_bf16[:])
                 flips[chunk] = [cols_ps]
             elif kind in ("wih", "y"):
                 flips[chunk] = []
                 for pair in range(ROW_TILES // 2):
-                    words_T = psum_flip.tile([P, 2, 2 * P], F32, tag="flip", name="flip_%s_%d_%d_%d" % (chunk + (pair,)))
+                    words_T = psum.tile([P, 2, 2 * P], F32, tag="bank", name="flip_%s_%d_%d_%d" % (chunk + (pair,)))
                     for i2 in range(2):
                         raw_words = raw[chunk][:, 2 * pair + i2, :].bitcast(F32)
                         for u in range(2):
@@ -160,7 +158,7 @@ def tile_dependency_pb_kernel(
             else:
                 flips[chunk] = []
                 for j in range(H_TILES):
-                    flip = psum_flip.tile([P, ROW_TILES, P], BF16, tag="flip", name="flip_%s_%d_%d_%d" % (chunk + (j,)))
+                    flip = psum.tile([P, ROW_TILES, P], BF16, tag="bank", name="flip_%s_%d_%d_%d" % (chunk + (j,)))
                     for a in range(ROW_TILES):
                         nc.tensor.transpose(flip[:, a, :], raw[chunk][:, a, P * j : P * (j + 1)], ident_bf16[:])
                     flips[chunk].append(flip)
@@ -221,7 +219,7 @@ def tile_dependency_pb_kernel(
             if not 0 <= u < UNITS:
                 return
             lstm_tile, d, n, tokens, (name, q, func) = place(u)
-            plain_ps[u] = psum_plain.tile([P, H_TILES, QUARTER], F32, tag="plain", name="plain_%d" % u)
+            plain_ps[u] = psum.tile([P, H_TILES, QUARTER], F32, tag="bank", name="plain_%d" % u)
             for j in range(H_TILES):
                 g, c, cols = gate_rows(q, j)
                 for k in range(H_TILES):
@@ -244,7 +242,7 @@ def tile_dependency_pb_kernel(
             if not 0 <= u < UNITS:
                 return
             lstm_tile, d, n, tokens, (name, q, func) = place(u)
-            input_ps[u] = psum_mx.tile([P, H_TILES, QUARTER], F32, tag="mx", name="input_%d" % u)
+            input_ps[u] = psum.tile([P, H_TILES, QUARTER], F32, tag="bank", name="input_%d" % u)
             for j in range(H_TILES):
                 g, c, cols = gate_rows(q, j)
                 nc.tensor.matmul_mx(
@@ -297,7 +295,7 @@ def tile_dependency_pb_kernel(
                     out=hidT[quarter][:, own, :], in0=gate[lstm_tile, "out_gate"][:], in1=gate[lstm_tile, "tanh_cell"][:], op=ALU.mult
                 )
             if i == BACK_STEP:
-                hid_ps[lstm_tile] = psum_flip.tile([P, QUARTER_TILES, H_TILES, P], F32, tag="flip", name="hid_ps_%d" % lstm_tile)
+                hid_ps[lstm_tile] = psum.tile([P, QUARTER_TILES, H_TILES, P], F32, tag="bank", name="hid_ps_%d" % lstm_tile)
                 for a in range(QUARTER_TILES):
                     for j in range(H_TILES):
                         nc.tensor.transpose(hid_ps[lstm_tile][:, a, j, :], hidT[quarter][:, H_TILES * d + j, P * a : P * (a + 1)], ident_f32[:])
@@ -312,19 +310,17 @@ def tile_dependency_pb_kernel(
         score_ps = {}
 
         def finish_quarter(quarter, i):
-            if ROUND_STEP <= i < QUANTISE_STEP:
-                if i == ROUND_STEP:
-                    for what in ("hid", "u"):
-                        grouped[what, 0, quarter] = stage.tile(
-                            [P, QUARTER, PACK], BF16, tag=what, name="grouped_%s_%d" % (what, quarter), align_bytes=64, bufs=2
-                        )
-                tokens = slice(P * (i - ROUND_STEP), P * (i - ROUND_STEP + 1))
-                by_token = hidT[quarter][:, :, tokens].rearrange("p t r -> p r t")
-                nc.scalar.copy(out=grouped["hid", 0, quarter][:, tokens, :], in_=by_token)
+            if i == ROUND_STEP:
+                for what in ("hid", "u"):
+                    grouped[what, 0, quarter] = stage.tile(
+                        [P, QUARTER, PACK], BF16, tag=what, name="grouped_%s_%d" % (what, quarter), align_bytes=64, bufs=2
+                    )
+                by_token = hidT[quarter][:].rearrange("p t r -> p r t")
+                nc.scalar.copy(out=grouped["hid", 0, quarter][:], in_=by_token)
                 nc.vector.tensor_tensor(
-                    out=grouped["u", 0, quarter][:, tokens, :],
+                    out=grouped["u", 0, quarter][:],
                     in0=by_token,
-                    in1=pair_weight[:].unsqueeze(1).to_broadcast([P, P, PACK]),
+                    in1=pair_weight[:].unsqueeze(1).to_broadcast([P, QUARTER, PACK]),
                     op=ALU.mult,
                 )
             if i == QUANTISE_STEP:
@@ -332,7 +328,7 @@ def tile_dependency_pb_kernel(
                     quantise((what, 0, quarter), grouped[what, 0, quarter][:].rearrange("p r t -> p (r t)"), QUARTER)
             rows = quarter - (i - SCORE_STEP)
             if i >= SCORE_STEP and rows >= 0:
-                score_ps[rows, quarter] = psum_mx.tile([P, QUARTER_TILES, QUARTER], F32, tag="mx", name="score_%d_%d" % (rows, quarter))
+                score_ps[rows, quarter] = psum.tile([P, QUARTER_TILES, QUARTER], F32, tag="bank", name="score_%d_%d" % (rows, quarter))
                 for a in range(QUARTER_TILES):
                     nc.tensor.matmul_mx(
                         out=score_ps[rows, quarter][:, a, :],

@@ -13,7 +13,6 @@ ALU = mybir.AluOpType
 
 P = 128
 PACK = 4
-BANK = 512
 S = 1024
 H = 256
 D = 2 * H
@@ -56,9 +55,9 @@ def operand_chunks():
     chunks = []
     for n in range(HALVES):
         for d in range(DIRECTIONS):
+            chunks.append(("h0", d, n))
             if n == 0:
                 chunks.extend([("whh", d, 0), ("whh", d, 1)])
-            chunks.append(("h0", d, n))
             if n == 0 and d == 0:
                 chunks.append(("bias", 0, 0))
             if n == 0:
@@ -104,6 +103,8 @@ def tile_dependency_pb_kernel(
         )
         zeros = const.tile([P, S - QUARTER], F32)
         nc.vector.memset(zeros[:], 0.0)
+        first_sigmoid = const.tile([P, 1], F32)
+        nc.scalar.activation(out=first_sigmoid[:], in_=zeros[:, 0:1], func=ACT.Sigmoid)
 
         matrices = {"y": (y, y), "h0": (h0[0], h0[1]), "c0": (c0[0], c0[1]), "wih": (wih_f, wih_b), "whh": (whh_f, whh_b)}
         vectors = {"bias": (bih_f, bhh_f, bih_b, bhh_b), "pair": (wd, fc_w[0])}

@@ -17,58 +17,65 @@ S = 1024
 H = 256
 D = 2 * H
 DIRECTIONS = 2
-H_TILES = H // P
-FEATURE_TILES = D // P
+K_TILES = H // P
 GATE_TILES = 4 * H // P
 CHUNK = 512
 ROW_TILES = CHUNK // P
-HALVES = S // CHUNK
-QUARTER = 256
-QUARTERS = S // QUARTER
-QUARTER_TILES = QUARTER // P
+BANKS = 2
+TOKEN_TILES = S // P
 
-LSTM_TILES = ((0, 0), (1, 0), (0, 1), (1, 1), (2, 0), (2, 1), (3, 0), (3, 1))
-GATES = (
-    ("forget_gate", 1, ACT.Sigmoid),
-    ("in_gate", 0, ACT.Sigmoid),
-    ("candidate", 2, ACT.Tanh),
-    ("out_gate", 3, ACT.Sigmoid),
+TURNS = (
+    (7, 0), (6, 0), (5, 0), (4, 0), (7, 1), (6, 1), (5, 1), (4, 1),
+    (3, 0), (2, 0), (3, 1), (2, 1), (1, 0), (1, 1), (0, 0), (0, 1),
 )
-UNITS = len(LSTM_TILES) * len(GATES)
+MX_ORDER = ((1, 0), (1, 1), (0, 0), (0, 1))
 
-PLAIN_STEP = 4
-MX_STEP = 8
-ADD_STEP = MX_STEP + 1
-ACT_STEP = ADD_STEP + 1
-TANH_STEP = 6
-HID_STEP = TANH_STEP + 1
-BACK_STEP = HID_STEP + 3
-STORE_STEP = BACK_STEP + 1
-ROUND_STEP = 1
-QUANTISE_STEP = ROUND_STEP + 1
-SCORE_STEP = QUANTISE_STEP + 1
+FLIPS = (
+    ("y", 0, 1), ("wih", 0, 0), ("wih", 0, 1), ("h0", 0, 1), ("whh", 0, 0), ("whh", 0, 1),
+    ("wih", 1, 0), ("wih", 1, 1), ("h0", 1, 1), ("whh", 1, 0), ("whh", 1, 1), ("y", 0, 0),
+    ("h0", 0, 0), ("h0", 1, 0),
+)
+FLIP_STEP = (0, 1, 2, 3, 4, 5, 6, 7, 7, 8, 9, 9, 10, 11)
+MX_COUNTS = (0, 0, 0, 4, 4, 0, 0, 0, 4, 4, 0, 3, 3, 3, 3, 4)
+TURN_STEP = 6
+
+ACT_STEP = 1
+TANH_STEP = 2
+HID_STEP = 3
+FLIP_BACK_STEP = 3
+GROUP_STEP = 4
+SCORE_STEP = 5
 
 FLOPS = 2 * S * (4 * H) * D * DIRECTIONS + 2 * S * (4 * H) * H * DIRECTIONS + 2 * S * S * D
 
 
-def operand_chunks():
+def load_chunks():
     chunks = []
-    for n in range(HALVES):
-        for d in range(DIRECTIONS):
-            chunks.append(("h0", d, n))
-            if n == 0:
-                chunks.extend([("whh", d, 0), ("whh", d, 1)])
-            if n == 0 and d == 0:
-                chunks.append(("bias", 0, 0))
-            if n == 0:
-                chunks.append(("wih", d, 0))
-            if d == 0:
-                chunks.append(("y", 0, n))
-            if n == 0:
-                chunks.append(("wih", d, 1))
-            chunks.append(("c0", d, n))
-    chunks.append(("pair", 0, 0))
+    for chunk in FLIPS:
+        chunks.append(chunk)
+        if chunk == ("wih", 0, 0):
+            chunks.append(("bias", 0, 0))
+        if chunk == ("whh", 0, 1):
+            chunks.append(("c0", 0, 1))
+        if chunk == ("whh", 1, 1):
+            chunks.append(("c0", 1, 1))
+    chunks.extend([("c0", 0, 0), ("c0", 1, 0)])
     return chunks
+
+
+def score_pieces(tile):
+    banks, first = [], P * tile
+    while first < S:
+        bank, room = [], CHUNK
+        while first < S and room:
+            width = CHUNK
+            while width > min(room, S - first):
+                width //= 2
+            bank.append((first, width))
+            first += width
+            room -= width
+        banks.append(bank)
+    return banks
 
 
 def tile_dependency_pb_kernel(
@@ -81,295 +88,330 @@ def tile_dependency_pb_kernel(
         raws = stack.enter_context(tc.tile_pool(name="raws", bufs=1))
         keep = stack.enter_context(tc.tile_pool(name="keep", bufs=1))
         stage = stack.enter_context(tc.tile_pool(name="stage", bufs=3))
-        sums = stack.enter_context(tc.tile_pool(name="sums", bufs=ACT_STEP - PLAIN_STEP + 1))
-        work = stack.enter_context(tc.tile_pool(name="work", bufs=2))
-        outs = stack.enter_context(tc.tile_pool(name="outs", bufs=4))
+        work = stack.enter_context(tc.tile_pool(name="work", bufs=3))
+        outs = stack.enter_context(tc.tile_pool(name="outs", bufs=3))
         psum = stack.enter_context(tc.psum_pool(name="psum", bufs=8))
 
-        ident_bf16 = const.tile([P, P], BF16)
-        make_identity(nc, ident_bf16[:])
         ident_f32 = const.tile([P, P], F32)
         make_identity(nc, ident_f32[:])
-        on_or_above = const.tile([P, QUARTER_TILES, QUARTER], F32)
+        ident_bf16 = const.tile([P, P], BF16)
+        make_identity(nc, ident_bf16[:])
+        ones = const.tile([P, P], BF16)
+        nc.gpsimd.memset(ones[:], 1.0)
+        on_or_above = const.tile([P, CHUNK], F32)
         nc.gpsimd.memset(on_or_above[:], 1.0)
         nc.gpsimd.affine_select(
             out=on_or_above[:],
             in_=on_or_above[:],
-            pattern=[[-P, QUARTER_TILES], [1, QUARTER]],
+            pattern=[[1, CHUNK]],
             compare_op=ALU.is_ge,
             fill=0.0,
             base=0,
             channel_multiplier=-1,
         )
-        zeros = const.tile([P, S - QUARTER], F32)
+        zeros = const.tile([P, S - P], F32)
         nc.vector.memset(zeros[:], 0.0)
         first_sigmoid = const.tile([P, 1], F32)
         nc.scalar.activation(out=first_sigmoid[:], in_=zeros[:, 0:1], func=ACT.Sigmoid)
 
         matrices = {"y": (y, y), "h0": (h0[0], h0[1]), "c0": (c0[0], c0[1]), "wih": (wih_f, wih_b), "whh": (whh_f, whh_b)}
-        vectors = {"bias": (bih_f, bhh_f, bih_b, bhh_b), "pair": (wd, fc_w[0])}
-        chunks = operand_chunks()
+        biases = (bih_f, bhh_f, bih_b, bhh_b)
         raw = {}
-        for chunk in chunks:
+        for chunk in load_chunks():
             kind, d, c = chunk
-            if kind in vectors:
-                raw[chunk] = raws.tile([P, P], BF16, name="%s_rows" % kind)
-                nc.vector.memset(raw[chunk][:], 0.0)
-                row = 0
-                for vec in vectors[kind]:
-                    n_rows = vec.shape[0] // P
-                    nc.sync.dma_start(out=raw[chunk][row : row + n_rows, :], in_=vec.rearrange("(r c) -> r c", c=P))
-                    row += n_rows
+            if kind == "bias":
+                bias_rows = raws.tile([P, P], BF16)
+                nc.vector.memset(bias_rows[:], 0.0)
+                pair_rows = raws.tile([P, 2, D], BF16)
+                nc.vector.memset(pair_rows[:], 0.0)
+                for i, vec in enumerate((wd, fc_w[0])):
+                    nc.sync.dma_start(out=pair_rows[0:1, i, :], in_=vec.unsqueeze(0))
+                for i, vec in enumerate(biases):
+                    nc.sync.dma_start(out=bias_rows[GATE_TILES * i : GATE_TILES * (i + 1), :], in_=vec.rearrange("(r c) -> r c", c=P))
             else:
                 rows = matrices[kind][d][CHUNK * c : CHUNK * (c + 1), :]
                 raw[chunk] = raws.tile([P, ROW_TILES, rows.shape[1]], BF16, name="%s_raw_%d_%d" % chunk)
                 nc.sync.dma_start(out=raw[chunk][:], in_=rows.rearrange("(a p) k -> p a k", p=P))
         fc_b_bf16 = const.tile([P, 1], BF16)
         nc.sync.dma_start(out=fc_b_bf16[:], in_=fc_b.partition_broadcast(P))
-        for r in range(QUARTER_TILES, S // P):
-            width = QUARTER * (r // QUARTER_TILES)
-            nc.sync.dma_start(out=out_0[P * r : P * (r + 1), 0:width], in_=zeros[:, 0:width])
+        for tile in range(1, TOKEN_TILES):
+            nc.sync.dma_start(out=out_0[P * tile : P * (tile + 1), 0 : P * tile], in_=zeros[:, 0 : P * tile])
 
         flips = {}
         flipped = {}
         grouped = {}
         codes, scales = {}, {}
         bias = const.tile([P, DIRECTIONS, GATE_TILES], F32)
-        pair_weight = const.tile([P, FEATURE_TILES], F32)
+        pair_weight = const.tile([P, D], F32)
         fc_b_col = const.tile([P, 1], F32)
+        nc.gpsimd.tensor_copy(out=fc_b_col[:], in_=fc_b_bf16[:])
 
-        def flip_chunk(i):
-            if not 0 <= i < len(chunks):
-                return
-            chunk = chunks[i]
-            kind = chunk[0]
-            if kind in vectors:
-                cols_ps = psum.tile([P, P], BF16, tag="bank", name="flip_%s" % kind)
-                nc.tensor.transpose(cols_ps[:], raw[chunk][:], ident_bf16[:])
-                flips[chunk] = [cols_ps]
-            elif kind in ("wih", "y"):
-                flips[chunk] = []
+        def flip_words(words_T, i, row_words):
+            for v in range(2):
+                nc.tensor.transpose(words_T[:, v, P * i : P * (i + 1)], row_words[:, P * v : P * (v + 1)], ident_f32[:])
+
+        def flip_chunk(chunk):
+            flips[chunk] = []
+            if chunk[0] in ("wih", "y"):
                 for pair in range(ROW_TILES // 2):
                     words_T = psum.tile([P, 2, 2 * P], F32, tag="bank", name="flip_%s_%d_%d_%d" % (chunk + (pair,)))
-                    for i2 in range(2):
-                        raw_words = raw[chunk][:, 2 * pair + i2, :].bitcast(F32)
-                        for u in range(2):
-                            nc.tensor.transpose(words_T[:, u, P * i2 : P * (i2 + 1)], raw_words[:, P * u : P * (u + 1)], ident_f32[:])
+                    for i in range(2):
+                        flip_words(words_T, i, raw[chunk][:, 2 * pair + i, :].bitcast(F32))
                     flips[chunk].append(words_T)
             else:
-                flips[chunk] = []
-                for j in range(H_TILES):
+                for j in range(K_TILES):
                     flip = psum.tile([P, ROW_TILES, P], BF16, tag="bank", name="flip_%s_%d_%d_%d" % (chunk + (j,)))
                     for a in range(ROW_TILES):
                         nc.tensor.transpose(flip[:, a, :], raw[chunk][:, a, P * j : P * (j + 1)], ident_bf16[:])
                     flips[chunk].append(flip)
 
-        def save_chunk(i):
-            if not 0 <= i < len(chunks):
-                return
-            chunk = chunks[i]
-            kind = chunk[0]
-            copies = (nc.vector.tensor_copy, nc.scalar.copy)
-            if kind in vectors:
-                cols = const.tile([P, P], F32, name="%s_cols" % kind)
-                nc.vector.tensor_copy(out=cols[:], in_=flips[chunk][0][:])
-                if kind == "bias":
-                    by_kind = cols[:, 0 : 2 * DIRECTIONS * GATE_TILES].rearrange("p (d i g) -> p d i g", d=DIRECTIONS, i=2)
-                    nc.vector.tensor_tensor(out=bias[:], in0=by_kind[:, :, 0, :], in1=by_kind[:, :, 1, :], op=ALU.add)
-                else:
-                    nc.vector.tensor_tensor(
-                        out=pair_weight[:], in0=cols[:, 0:FEATURE_TILES], in1=cols[:, FEATURE_TILES : 2 * FEATURE_TILES], op=ALU.mult
-                    )
-                    nc.vector.tensor_copy(out=fc_b_col[:], in_=fc_b_bf16[:])
-            elif kind in ("wih", "y"):
+        def save_chunk(chunk):
+            if chunk[0] in ("wih", "y"):
                 grouped[chunk] = stage.tile([P, CHUNK * PACK], BF16, tag="grouped", name="grouped_%s_%d_%d" % chunk, align_bytes=64)
-                grouped_words = grouped[chunk][:].bitcast(F32).rearrange("p (r u) -> p r u", u=2)
-                for pair in range(ROW_TILES // 2):
-                    copies[pair](
-                        out=grouped_words[:, 2 * P * pair : 2 * P * (pair + 1), :], in_=flips[chunk][pair][:].rearrange("p u r -> p r u")
-                    )
+                grouped_words = grouped[chunk][:].bitcast(F32).rearrange("p (r v) -> p r v", v=2)
+                for pair, copy in enumerate((nc.scalar.copy, nc.vector.tensor_copy)):
+                    copy(out=grouped_words[:, 2 * P * pair : 2 * P * (pair + 1), :], in_=flips[chunk][pair][:].rearrange("p v r -> p r v"))
             else:
-                flipped[chunk] = keep.tile([P, H_TILES, CHUNK], BF16, name="%sT_%d_%d" % chunk)
-                for j in range(H_TILES):
-                    copies[j](out=flipped[chunk][:, j, :], in_=flips[chunk][j][:].rearrange("p a r -> p (a r)"))
+                flipped[chunk] = keep.tile([P, K_TILES, CHUNK], BF16, name="%sT_%d_%d" % chunk)
+                for j in range(K_TILES):
+                    nc.vector.tensor_copy(out=flipped[chunk][:, j, :], in_=flips[chunk][j][:].rearrange("p a r -> p (a r)"))
 
-        def quantise(key, values, width):
-            codes[key] = keep.tile([P, width], U32, name="%s_codes_%d_%d" % key, align_bytes=64)
-            scales[key] = keep.tile([P, width], U8, name="%s_scales_%d_%d" % key, align_bytes=64)
-            nc.vector.quantize_mx(out=codes[key][:].bitcast(FP8X4), scales=scales[key][:], in_=values)
+        def quantise_chunk(chunk):
+            if chunk[0] in ("wih", "y"):
+                codes[chunk] = keep.tile([P, CHUNK], U32, name="%s_codes_%d_%d" % chunk, align_bytes=64)
+                scales[chunk] = keep.tile([P, CHUNK], U8, name="%s_scales_%d_%d" % chunk, align_bytes=64)
+                nc.vector.quantize_mx(out=codes[chunk][:].bitcast(FP8X4), scales=scales[chunk][:], in_=grouped[chunk][:])
 
-        def quantise_chunk(i):
-            if 0 <= i < len(chunks) and chunks[i][0] in ("wih", "y"):
-                quantise(chunks[i], grouped[chunks[i]][:], CHUNK)
+        def flip_biases():
+            cols_ps = psum.tile([P, P], BF16, tag="bank", name="flip_bias")
+            nc.tensor.transpose(cols_ps[:], bias_rows[:], ident_bf16[:])
+            cols = const.tile([P, P], F32, name="bias_cols")
+            nc.vector.tensor_copy(out=cols[:], in_=cols_ps[:])
+            by_kind = cols[:, 0 : 2 * DIRECTIONS * GATE_TILES].rearrange("p (d i g) -> p d i g", d=DIRECTIONS, i=2)
+            nc.vector.tensor_tensor(out=bias[:], in0=by_kind[:, :, 0, :], in1=by_kind[:, :, 1, :], op=ALU.add)
 
-        def place(u):
-            lstm_tile, which = divmod(u, len(GATES))
-            quarter, d = LSTM_TILES[lstm_tile]
-            n, in_half = divmod(quarter, QUARTERS // HALVES)
-            return lstm_tile, d, n, slice(QUARTER * in_half, QUARTER * (in_half + 1)), GATES[which]
+        def spread_pair():
+            spread = []
+            for i in range(2):
+                spread.append(psum.tile([P, D], F32, tag="bank", name="spread_%d" % i))
+                nc.tensor.matmul(spread[i][:], lhsT=ones[:], rhs=pair_rows[:, i, :], start=True, stop=True)
+            nc.vector.tensor_copy(out=pair_weight[:], in_=spread[0][:])
+            nc.vector.tensor_tensor(out=pair_weight[:], in0=spread[1][:], in1=pair_weight[:], op=ALU.mult)
 
-        def gate_rows(q, j):
-            g = H_TILES * q + j
-            return g, g // ROW_TILES, slice(P * (g % ROW_TILES), P * (g % ROW_TILES + 1))
+        mx_ps = {}
+        mx_rows = {}
 
-        plain_ps, input_ps = {}, {}
-        pre = {}
-        gate = {}
+        def mx_product(m):
+            order, g = divmod(m, GATE_TILES)
+            n, d = MX_ORDER[order]
+            wih, cols = ("wih", d, g // ROW_TILES), slice(P * (g % ROW_TILES), P * (g % ROW_TILES + 1))
+            mx_ps[m] = psum.tile([P, CHUNK], F32, tag="bank", name="mx_%d" % m)
+            nc.tensor.matmul_mx(
+                out=mx_ps[m][:],
+                lhsT=codes[wih][:, cols].bitcast(FP8X4),
+                lhsT_scale=scales[wih][:, cols],
+                rhs=codes["y", 0, n][:].bitcast(FP8X4),
+                rhs_scale=scales["y", 0, n][:],
+                start=True,
+                stop=True,
+            )
 
-        def plain_product(u):
-            if not 0 <= u < UNITS:
-                return
-            lstm_tile, d, n, tokens, (name, q, func) = place(u)
-            plain_ps[u] = psum.tile([P, H_TILES, QUARTER], F32, tag="bank", name="plain_%d" % u)
-            for j in range(H_TILES):
-                g, c, cols = gate_rows(q, j)
-                for k in range(H_TILES):
+        def save_mx_product(m):
+            order, g = divmod(m, GATE_TILES)
+            n, d = MX_ORDER[order]
+            if g == 0:
+                mx_rows[n, d] = keep.tile([P, GATE_TILES, CHUNK], F32, tag="mx_rows", name="mx_rows_%d_%d" % (n, d), bufs=3)
+            bias_col = bias[:, d, g : g + 1]
+            if g % 4 != 3:
+                nc.scalar.activation(out=mx_rows[n, d][:, g, :], in_=mx_ps[m][:], func=ACT.Identity, bias=bias_col, scale=1.0)
+            else:
+                nc.vector.tensor_scalar(out=mx_rows[n, d][:, g, :], in0=mx_ps[m][:], scalar1=bias_col, scalar2=None, op0=ALU.add)
+
+        gates_ps = {}
+        forget_in, candidate, out_gate, cell, tanh_c = {}, {}, {}, {}, {}
+
+        def products(turn):
+            tile, d = TURNS[turn]
+            n, a = divmod(tile, ROW_TILES)
+            tokens = slice(P * a, P * (a + 1))
+            gates_ps[turn] = []
+            for b in range(BANKS):
+                bank = psum.tile([P, CHUNK], F32, tag="bank", name="gates_%d_%d" % (turn, b))
+                gates_ps[turn].append(bank)
+                for k in range(K_TILES):
                     nc.tensor.matmul(
-                        plain_ps[u][:, j, :],
-                        lhsT=flipped["whh", d, c][:, k, cols],
-                        rhs=flipped["h0", d, n][:, k, tokens],
-                        start=(k == 0),
-                        stop=(k == H_TILES - 1),
+                        bank[:], lhsT=flipped["h0", d, n][:, k, tokens], rhs=flipped["whh", d, b][:, k, :], start=(k == 0), stop=False
+                    )
+            for b in range(BANKS):
+                for q in range(ROW_TILES):
+                    nc.tensor.matmul(
+                        gates_ps[turn][b][:, P * q : P * (q + 1)],
+                        lhsT=mx_rows[n, d][:, ROW_TILES * b + q, tokens],
+                        rhs=ident_f32[:],
+                        start=False,
+                        stop=(q == ROW_TILES - 1),
+                        is_transpose=True,
                     )
 
-        def save_plain(u):
-            if not 0 <= u < UNITS:
-                return
-            pre[u] = sums.tile([P, H_TILES, QUARTER], F32, tag="pre", name="pre_%d" % u)
-            copy = nc.vector.tensor_copy if place(u)[4][0] == "out_gate" else nc.scalar.copy
-            copy(out=pre[u][:], in_=plain_ps[u][:])
+        def activate(turn):
+            forget_in[turn] = work.tile([P, 2, H], F32, tag="in_forget", name="in_forget_%d" % turn)
+            nc.scalar.activation(out=forget_in[turn][:].rearrange("p i f -> p (i f)"), in_=gates_ps[turn][0][:], func=ACT.Sigmoid)
+            candidate[turn] = work.tile([P, H], F32, tag="candidate", name="candidate_%d" % turn)
+            nc.scalar.activation(out=candidate[turn][:], in_=gates_ps[turn][1][:, 0:H], func=ACT.Tanh)
+            out_gate[turn] = work.tile([P, H], F32, tag="out_gate", name="out_gate_%d" % turn)
+            nc.scalar.activation(out=out_gate[turn][:], in_=gates_ps[turn][1][:, H : 2 * H], func=ACT.Sigmoid)
 
-        def input_product(u):
-            if not 0 <= u < UNITS:
-                return
-            lstm_tile, d, n, tokens, (name, q, func) = place(u)
-            input_ps[u] = psum.tile([P, H_TILES, QUARTER], F32, tag="bank", name="input_%d" % u)
-            for j in range(H_TILES):
-                g, c, cols = gate_rows(q, j)
-                nc.tensor.matmul_mx(
-                    out=input_ps[u][:, j, :],
-                    lhsT=codes["wih", d, c][:, cols].bitcast(FP8X4),
-                    lhsT_scale=scales["wih", d, c][:, cols],
-                    rhs=codes["y", 0, n][:, tokens].bitcast(FP8X4),
-                    rhs_scale=scales["y", 0, n][:, tokens],
-                    start=True,
-                    stop=True,
-                )
+        def keep_cell(turn):
+            tile, d = TURNS[turn]
+            n, a = divmod(tile, ROW_TILES)
+            cell[turn] = work.tile([P, H], F32, tag="cell", name="cell_%d" % turn)
+            nc.vector.tensor_tensor(out=cell[turn][:], in0=forget_in[turn][:, 1, :], in1=raw["c0", d, n][:, a, :], op=ALU.mult)
 
-        def add_products(u):
-            if 0 <= u < UNITS:
-                nc.vector.tensor_tensor(out=pre[u][:], in0=input_ps[u][:], in1=pre[u][:], op=ALU.add)
+        def fresh_cell(turn):
+            nc.vector.tensor_tensor(out=candidate[turn][:], in0=forget_in[turn][:, 0, :], in1=candidate[turn][:], op=ALU.mult)
 
-        def activate(u):
-            if not 0 <= u < UNITS:
-                return
-            lstm_tile, d, n, tokens, (name, q, func) = place(u)
-            gate[lstm_tile, name] = work.tile([P, H_TILES, QUARTER], F32, tag=name, name="%s_%d" % (name, lstm_tile))
-            for j in range(H_TILES):
-                g = gate_rows(q, j)[0]
-                nc.scalar.activation(out=gate[lstm_tile, name][:, j, :], in_=pre[u][:, j, :], func=func, bias=bias[:, d, g : g + 1], scale=1.0)
-            if name == "forget_gate":
-                gate[lstm_tile, "cell"] = work.tile([P, H_TILES, QUARTER], F32, tag="cell", name="cell_%d" % lstm_tile)
-                nc.gpsimd.tensor_tensor(
-                    out=gate[lstm_tile, "cell"][:], in0=gate[lstm_tile, name][:], in1=flipped["c0", d, n][:, :, tokens], op=ALU.mult
-                )
-            if name == "candidate":
-                fresh = work.tile([P, H_TILES, QUARTER], F32, tag="fresh")
-                nc.gpsimd.tensor_tensor(out=fresh[:], in0=gate[lstm_tile, "in_gate"][:], in1=gate[lstm_tile, name][:], op=ALU.mult)
-                nc.gpsimd.tensor_tensor(out=gate[lstm_tile, "cell"][:], in0=gate[lstm_tile, "cell"][:], in1=fresh[:], op=ALU.add)
+        def add_cell(turn):
+            nc.vector.tensor_tensor(out=cell[turn][:], in0=cell[turn][:], in1=candidate[turn][:], op=ALU.add)
 
-        hidT = {}
-        hid_ps = {}
+        def tanh_cell(turn):
+            tanh_c[turn] = work.tile([P, H], F32, tag="tanh_c", name="tanh_c_%d" % turn)
+            nc.scalar.activation(out=tanh_c[turn][:], in_=cell[turn][:], func=ACT.Tanh)
 
-        def finish_tile(lstm_tile, i):
-            if not 0 <= lstm_tile < len(LSTM_TILES):
-                return
-            quarter, d = LSTM_TILES[lstm_tile]
-            own = slice(H_TILES * d, H_TILES * (d + 1))
-            if i == TANH_STEP:
-                gate[lstm_tile, "tanh_cell"] = work.tile([P, H_TILES, QUARTER], F32, tag="tanh_cell", name="tanh_cell_%d" % lstm_tile)
-                nc.scalar.activation(out=gate[lstm_tile, "tanh_cell"][:], in_=gate[lstm_tile, "cell"][:], func=ACT.Tanh)
-            if i == HID_STEP:
-                if d == 0:
-                    hidT[quarter] = keep.tile([P, FEATURE_TILES, QUARTER], F32, name="hidT_%d" % quarter)
-                nc.vector.tensor_tensor(
-                    out=hidT[quarter][:, own, :], in0=gate[lstm_tile, "out_gate"][:], in1=gate[lstm_tile, "tanh_cell"][:], op=ALU.mult
-                )
-            if i == BACK_STEP:
-                hid_ps[lstm_tile] = psum.tile([P, QUARTER_TILES, H_TILES, P], F32, tag="bank", name="hid_ps_%d" % lstm_tile)
-                for a in range(QUARTER_TILES):
-                    for j in range(H_TILES):
-                        nc.tensor.transpose(hid_ps[lstm_tile][:, a, j, :], hidT[quarter][:, H_TILES * d + j, P * a : P * (a + 1)], ident_f32[:])
-            if i == STORE_STEP:
-                hid_rows = outs.tile([P, QUARTER_TILES, H], F32, tag="hid_rows")
-                nc.vector.tensor_copy(out=hid_rows[:], in_=hid_ps[lstm_tile][:].rearrange("p a j c -> p a (j c)"))
-                nc.sync.dma_start(
-                    out=out_1[0, QUARTER * quarter : QUARTER * (quarter + 1), H * d : H * (d + 1)].rearrange("(a p) f -> p a f", p=P),
-                    in_=hid_rows[:],
-                )
+        hid = {}
+        rounded = {}
 
+        def make_hid(turn):
+            tile, d = TURNS[turn]
+            if d == 0:
+                hid[tile] = outs.tile([P, D], F32, tag="hid", name="hid_%d" % tile, bufs=5)
+                rounded[tile] = outs.tile([P, 2, D], BF16, tag="rounded", name="rounded_%d" % tile, bufs=5)
+            nc.vector.tensor_tensor(out=hid[tile][:, H * d : H * (d + 1)], in0=out_gate[turn][:], in1=tanh_c[turn][:], op=ALU.mult)
+            if d == 1:
+                nc.sync.dma_start(out=out_1[0, P * tile : P * (tile + 1), :], in_=hid[tile][:])
+
+        def round_u(turn):
+            tile, d = TURNS[turn]
+            own = slice(H * d, H * (d + 1))
+            nc.vector.tensor_tensor(out=rounded[tile][:, 1, own], in0=hid[tile][:, own], in1=pair_weight[:, own], op=ALU.mult)
+
+        def round_hid(turn):
+            tile, d = TURNS[turn]
+            own = slice(H * d, H * (d + 1))
+            nc.vector.tensor_copy(out=rounded[tile][:, 0, own], in_=hid[tile][:, own])
+
+        back_ps = {}
         score_ps = {}
+        hid_codes = keep.tile([P, S], U32, align_bytes=64)
+        hid_scales = keep.tile([P, S], U8, align_bytes=64)
 
-        def finish_quarter(quarter, i):
-            if i == ROUND_STEP:
-                for what in ("hid", "u"):
-                    grouped[what, 0, quarter] = stage.tile(
-                        [P, QUARTER, PACK], BF16, tag=what, name="grouped_%s_%d" % (what, quarter), align_bytes=64, bufs=2
-                    )
-                by_token = hidT[quarter][:].rearrange("p t r -> p r t")
-                nc.scalar.copy(out=grouped["hid", 0, quarter][:], in_=by_token)
-                nc.vector.tensor_tensor(
-                    out=grouped["u", 0, quarter][:],
-                    in0=by_token,
-                    in1=pair_weight[:].unsqueeze(1).to_broadcast([P, QUARTER, PACK]),
-                    op=ALU.mult,
-                )
-            if i == QUANTISE_STEP:
-                for what in ("u", "hid"):
-                    quantise((what, 0, quarter), grouped[what, 0, quarter][:].rearrange("p r t -> p (r t)"), QUARTER)
-            rows = quarter - (i - SCORE_STEP)
-            if i >= SCORE_STEP and rows >= 0:
-                score_ps[rows, quarter] = psum.tile([P, QUARTER_TILES, QUARTER], F32, tag="bank", name="score_%d_%d" % (rows, quarter))
-                for a in range(QUARTER_TILES):
+        def flip_hid(tile):
+            back_ps[tile] = psum.tile([P, 2, 2 * P], F32, tag="bank", name="back_%d" % tile)
+            for what in range(2):
+                flip_words(back_ps[tile], what, rounded[tile][:, what, :].bitcast(F32))
+
+        def group_hid(tile):
+            grouped[tile] = stage.tile([P, 2 * P * PACK], BF16, tag="grouped_hid", name="grouped_hid_%d" % tile, align_bytes=64)
+            nc.scalar.copy(
+                out=grouped[tile][:].bitcast(F32).rearrange("p (r v) -> p r v", v=2), in_=back_ps[tile][:].rearrange("p v r -> p r v")
+            )
+
+        def quantise_hid(tile):
+            codes["u", tile] = work.tile([P, P], U32, tag="u_codes", name="u_codes_%d" % tile, align_bytes=64)
+            scales["u", tile] = work.tile([P, P], U8, tag="u_scales", name="u_scales_%d" % tile, align_bytes=64)
+            own = slice(P * tile, P * (tile + 1))
+            nc.vector.quantize_mx(out=hid_codes[:, own].bitcast(FP8X4), scales=hid_scales[:, own], in_=grouped[tile][:, 0 : P * PACK])
+            nc.vector.quantize_mx(
+                out=codes["u", tile][:].bitcast(FP8X4), scales=scales["u", tile][:], in_=grouped[tile][:, P * PACK : 2 * P * PACK]
+            )
+
+        def score(tile):
+            score_ps[tile] = []
+            for i, pieces in enumerate(score_pieces(tile)):
+                bank = psum.tile([P, CHUNK], F32, tag="bank", name="score_%d_%d" % (tile, i))
+                score_ps[tile].append(bank)
+                for first, width in pieces:
+                    cols = slice(first, first + width)
+                    at = first - pieces[0][0]
                     nc.tensor.matmul_mx(
-                        out=score_ps[rows, quarter][:, a, :],
-                        lhsT=codes["u", 0, rows][:, P * a : P * (a + 1)].bitcast(FP8X4),
-                        lhsT_scale=scales["u", 0, rows][:, P * a : P * (a + 1)],
-                        rhs=codes["hid", 0, quarter][:].bitcast(FP8X4),
-                        rhs_scale=scales["hid", 0, quarter][:],
+                        out=bank[:, at : at + width],
+                        lhsT=codes["u", tile][:].bitcast(FP8X4),
+                        lhsT_scale=scales["u", tile][:],
+                        rhs=hid_codes[:, cols].bitcast(FP8X4),
+                        rhs_scale=hid_scales[:, cols],
                         start=True,
                         stop=True,
                     )
-            rows += 1
-            if i > SCORE_STEP and 0 <= rows <= quarter:
-                piece = outs.tile([P, QUARTER_TILES, QUARTER], F32, tag="piece")
-                if rows == quarter:
-                    nc.vector.scalar_tensor_tensor(
-                        out=piece[:], in0=score_ps[rows, quarter][:], scalar=fc_b_col[:, 0:1], in1=on_or_above[:], op0=ALU.add, op1=ALU.mult
-                    )
-                elif rows % 2 == 0:
-                    nc.scalar.activation(out=piece[:], in_=score_ps[rows, quarter][:], func=ACT.Identity, bias=fc_b_col[:, 0:1], scale=1.0)
-                else:
-                    nc.vector.tensor_scalar(out=piece[:], in0=score_ps[rows, quarter][:], scalar1=fc_b_col[:, 0:1], scalar2=None, op0=ALU.add)
-                nc.sync.dma_start(
-                    out=out_0[QUARTER * rows : QUARTER * (rows + 1), QUARTER * quarter : QUARTER * (quarter + 1)].rearrange(
-                        "(a p) c -> p a c", p=P
-                    ),
-                    in_=piece[:],
-                )
 
-        first_act = [ACT_STEP + len(GATES) * lstm_tile for lstm_tile in range(len(LSTM_TILES))]
-        quarter_done = [first_act[LSTM_TILES.index((quarter, 1))] + HID_STEP for quarter in range(QUARTERS)]
-        for s in range(quarter_done[-1] + SCORE_STEP + QUARTERS + 1):
-            save_plain(s - PLAIN_STEP - 1)
-            add_products(s - ADD_STEP)
-            save_chunk(s - 1)
-            quantise_chunk(s - 2)
-            activate(s - ACT_STEP)
-            plain_product(s - PLAIN_STEP)
-            input_product(s - MX_STEP)
-            for lstm_tile in range(len(LSTM_TILES)):
-                finish_tile(lstm_tile, s - first_act[lstm_tile])
-            for quarter in range(QUARTERS):
-                finish_quarter(quarter, s - quarter_done[quarter])
-            flip_chunk(s)
+        def store_scores(tile):
+            first = P * tile
+            for i, bank in enumerate(score_ps[tile]):
+                width = min(CHUNK, S - first)
+                piece = outs.tile([P, CHUNK], F32, tag="piece", name="piece_%d_%d" % (tile, i), bufs=4)
+                if i == 0:
+                    nc.vector.scalar_tensor_tensor(
+                        out=piece[:, 0:width],
+                        in0=bank[:, 0:width],
+                        scalar=fc_b_col[:, 0:1],
+                        in1=on_or_above[:, 0:width],
+                        op0=ALU.add,
+                        op1=ALU.mult,
+                    )
+                else:
+                    nc.scalar.activation(out=piece[:, 0:width], in_=bank[:, 0:width], func=ACT.Identity, bias=fc_b_col[:, 0:1], scale=1.0)
+                nc.sync.dma_start(out=out_0[P * tile : P * (tile + 1), first : first + width], in_=piece[:, 0:width])
+                first += width
+
+        def at(step, offset):
+            turn = step - TURN_STEP - offset
+            return [turn] if 0 <= turn < len(TURNS) else []
+
+        def finished(step, offset):
+            return [TURNS[turn][0] for turn in at(step, offset) if TURNS[turn][1] == 1]
+
+        mx_done = 0
+        for s in range(TURN_STEP + len(TURNS) + SCORE_STEP):
+            mx_now = range(mx_done, mx_done + (MX_COUNTS[s] if s < len(MX_COUNTS) else 0))
+            mx_done += len(mx_now)
+            for i, step in enumerate(FLIP_STEP):
+                if step == s:
+                    flip_chunk(FLIPS[i])
+            if s == 1:
+                flip_biases()
+                spread_pair()
+            for turn in at(s, HID_STEP):
+                make_hid(turn)
+            for turn in at(s, ACT_STEP):
+                activate(turn)
+                keep_cell(turn)
+            for turn in at(s, TANH_STEP):
+                tanh_cell(turn)
+            for tile in finished(s, GROUP_STEP):
+                group_hid(tile)
+            for turn in at(s, HID_STEP):
+                round_u(turn)
+            for turn in at(s, ACT_STEP):
+                fresh_cell(turn)
+            for turn in at(s, HID_STEP):
+                round_hid(turn)
+            for i, step in enumerate(FLIP_STEP):
+                if step == s - 1:
+                    quantise_chunk(FLIPS[i])
+            for m in mx_now:
+                mx_product(m)
+            for tile in finished(s, SCORE_STEP):
+                score(tile)
+            for turn in at(s, ACT_STEP):
+                add_cell(turn)
+            for i, step in enumerate(FLIP_STEP):
+                if step == s:
+                    save_chunk(FLIPS[i])
+            for tile in finished(s, GROUP_STEP):
+                quantise_hid(tile)
+            for m in mx_now:
+                save_mx_product(m)
+            for tile in finished(s, SCORE_STEP):
+                store_scores(tile)
+            for turn in at(s, 0):
+                products(turn)
+            for tile in finished(s, FLIP_BACK_STEP):
+                flip_hid(tile)

@@ -35,16 +35,18 @@ FLIPS = (
     ("wih", 1, 0), ("wih", 1, 1), ("h0", 1, 1), ("whh", 1, 0), ("whh", 1, 1), ("y", 0, 0),
     ("h0", 0, 0), ("h0", 1, 0),
 )
-FLIP_STEP = (0, 1, 2, 3, 4, 5, 6, 7, 7, 8, 9, 9, 10, 11)
-MX_COUNTS = (0, 0, 0, 4, 4, 0, 0, 0, 4, 4, 0, 3, 3, 3, 3, 4)
+FLIP_STEP = (0, 1, 2, 3, 4, 5, 6, 7, 7, 8, 8, 9, 10, 11)
+MX_COUNTS = (0, 0, 0, 3, 3, 0, 2, 0, 4, 4, 0, 4, 4, 4, 4)
 TURN_STEP = 6
+BIAS_STEPS = (1, 7)
+SPREAD_STEP = 6
 
 ACT_STEP = 1
 TANH_STEP = 2
 HID_STEP = 3
 FLIP_BACK_STEP = 3
 GROUP_STEP = 4
-SCORE_STEP = 5
+SCORE_STEP = 6
 
 FLOPS = 2 * S * (4 * H) * D * DIRECTIONS + 2 * S * (4 * H) * H * DIRECTIONS + 2 * S * S * D
 
@@ -53,10 +55,12 @@ def load_chunks():
     chunks = []
     for chunk in FLIPS:
         chunks.append(chunk)
-        if chunk == ("wih", 0, 0):
+        if chunk == ("y", 0, 1):
             chunks.append(("bias", 0, 0))
         if chunk == ("whh", 0, 1):
-            chunks.append(("c0", 0, 1))
+            chunks.extend([("c0", 0, 1), ("pair", 0, 0)])
+        if chunk == ("wih", 1, 0):
+            chunks.append(("bias", 1, 0))
         if chunk == ("whh", 1, 1):
             chunks.append(("c0", 1, 1))
     chunks.extend([("c0", 0, 0), ("c0", 1, 0)])
@@ -115,23 +119,31 @@ def tile_dependency_pb_kernel(
         nc.scalar.activation(out=first_sigmoid[:], in_=zeros[:, 0:1], func=ACT.Sigmoid)
 
         matrices = {"y": (y, y), "h0": (h0[0], h0[1]), "c0": (c0[0], c0[1]), "wih": (wih_f, wih_b), "whh": (whh_f, whh_b)}
-        biases = (bih_f, bhh_f, bih_b, bhh_b)
+        biases = ((bih_f, bhh_f), (bih_b, bhh_b))
         raw = {}
+        bias_rows = []
+        for d in range(DIRECTIONS):
+            bias_rows.append(raws.tile([P, P], BF16, name="bias_rows_%d" % d))
+            nc.vector.memset(bias_rows[d][:], 0.0)
+        pair_rows = raws.tile([P, 2, D], BF16)
+        nc.vector.memset(pair_rows[:], 0.0)
         for chunk in load_chunks():
             kind, d, c = chunk
             if kind == "bias":
-                bias_rows = raws.tile([P, P], BF16)
-                nc.vector.memset(bias_rows[:], 0.0)
-                pair_rows = raws.tile([P, 2, D], BF16)
-                nc.vector.memset(pair_rows[:], 0.0)
+                for i, vec in enumerate(biases[d]):
+                    nc.sync.dma_start(out=bias_rows[d][GATE_TILES * i : GATE_TILES * (i + 1), :], in_=vec.rearrange("(r c) -> r c", c=P))
+            elif kind == "pair":
                 for i, vec in enumerate((wd, fc_w[0])):
                     nc.sync.dma_start(out=pair_rows[0:1, i, :], in_=vec.unsqueeze(0))
-                for i, vec in enumerate(biases):
-                    nc.sync.dma_start(out=bias_rows[GATE_TILES * i : GATE_TILES * (i + 1), :], in_=vec.rearrange("(r c) -> r c", c=P))
             else:
                 rows = matrices[kind][d][CHUNK * c : CHUNK * (c + 1), :]
                 raw[chunk] = raws.tile([P, ROW_TILES, rows.shape[1]], BF16, name="%s_raw_%d_%d" % chunk)
-                nc.sync.dma_start(out=raw[chunk][:], in_=rows.rearrange("(a p) k -> p a k", p=P))
+                pieces = 2 if kind in ("y", "wih") else 1
+                for i in range(pieces):
+                    slots = slice(ROW_TILES * i // pieces, ROW_TILES * (i + 1) // pieces)
+                    nc.sync.dma_start(
+                        out=raw[chunk][:, slots, :], in_=rows[P * slots.start : P * slots.stop, :].rearrange("(a p) k -> p a k", p=P)
+                    )
         fc_b_bf16 = const.tile([P, 1], BF16)
         nc.sync.dma_start(out=fc_b_bf16[:], in_=fc_b.partition_broadcast(P))
         for tile in range(1, TOKEN_TILES):
@@ -169,12 +181,12 @@ def tile_dependency_pb_kernel(
             if chunk[0] in ("wih", "y"):
                 grouped[chunk] = stage.tile([P, CHUNK * PACK], BF16, tag="grouped", name="grouped_%s_%d_%d" % chunk, align_bytes=64)
                 grouped_words = grouped[chunk][:].bitcast(F32).rearrange("p (r v) -> p r v", v=2)
-                for pair, copy in enumerate((nc.scalar.copy, nc.vector.tensor_copy)):
-                    copy(out=grouped_words[:, 2 * P * pair : 2 * P * (pair + 1), :], in_=flips[chunk][pair][:].rearrange("p v r -> p r v"))
+                for pair in range(ROW_TILES // 2):
+                    nc.scalar.copy(out=grouped_words[:, 2 * P * pair : 2 * P * (pair + 1), :], in_=flips[chunk][pair][:].rearrange("p v r -> p r v"))
             else:
                 flipped[chunk] = keep.tile([P, K_TILES, CHUNK], BF16, name="%sT_%d_%d" % chunk)
                 for j in range(K_TILES):
-                    nc.vector.tensor_copy(out=flipped[chunk][:, j, :], in_=flips[chunk][j][:].rearrange("p a r -> p (a r)"))
+                    nc.scalar.copy(out=flipped[chunk][:, j, :], in_=flips[chunk][j][:].rearrange("p a r -> p (a r)"))
 
         def quantise_chunk(chunk):
             if chunk[0] in ("wih", "y"):
@@ -182,13 +194,12 @@ def tile_dependency_pb_kernel(
                 scales[chunk] = keep.tile([P, CHUNK], U8, name="%s_scales_%d_%d" % chunk, align_bytes=64)
                 nc.vector.quantize_mx(out=codes[chunk][:].bitcast(FP8X4), scales=scales[chunk][:], in_=grouped[chunk][:])
 
-        def flip_biases():
-            cols_ps = psum.tile([P, P], BF16, tag="bank", name="flip_bias")
-            nc.tensor.transpose(cols_ps[:], bias_rows[:], ident_bf16[:])
-            cols = const.tile([P, P], F32, name="bias_cols")
-            nc.vector.tensor_copy(out=cols[:], in_=cols_ps[:])
-            by_kind = cols[:, 0 : 2 * DIRECTIONS * GATE_TILES].rearrange("p (d i g) -> p d i g", d=DIRECTIONS, i=2)
-            nc.vector.tensor_tensor(out=bias[:], in0=by_kind[:, :, 0, :], in1=by_kind[:, :, 1, :], op=ALU.add)
+        def flip_biases(d):
+            cols_ps = psum.tile([P, P], BF16, tag="bank", name="flip_bias_%d" % d)
+            nc.tensor.transpose(cols_ps[:], bias_rows[d][:], ident_bf16[:])
+            cols = const.tile([P, 2, GATE_TILES], F32, name="bias_cols_%d" % d)
+            nc.vector.tensor_copy(out=cols[:], in_=cols_ps[:, 0 : 2 * GATE_TILES].rearrange("p (i g) -> p i g", i=2))
+            nc.vector.tensor_tensor(out=bias[:, d, :], in0=cols[:, 0, :], in1=cols[:, 1, :], op=ALU.add)
 
         def spread_pair():
             spread = []
@@ -222,13 +233,13 @@ def tile_dependency_pb_kernel(
             if g == 0:
                 mx_rows[n, d] = keep.tile([P, GATE_TILES, CHUNK], F32, tag="mx_rows", name="mx_rows_%d_%d" % (n, d), bufs=3)
             bias_col = bias[:, d, g : g + 1]
-            if g % 4 != 3:
+            if g % 2 == 0:
                 nc.scalar.activation(out=mx_rows[n, d][:, g, :], in_=mx_ps[m][:], func=ACT.Identity, bias=bias_col, scale=1.0)
             else:
                 nc.vector.tensor_scalar(out=mx_rows[n, d][:, g, :], in0=mx_ps[m][:], scalar1=bias_col, scalar2=None, op0=ALU.add)
 
         gates_ps = {}
-        forget_in, candidate, out_gate, cell, tanh_c = {}, {}, {}, {}, {}
+        forget_in, candidate, out_gate, kept, fresh, cell, tanh_c = {}, {}, {}, {}, {}, {}, {}
 
         def products(turn):
             tile, d = TURNS[turn]
@@ -264,14 +275,16 @@ def tile_dependency_pb_kernel(
         def keep_cell(turn):
             tile, d = TURNS[turn]
             n, a = divmod(tile, ROW_TILES)
-            cell[turn] = work.tile([P, H], F32, tag="cell", name="cell_%d" % turn)
-            nc.vector.tensor_tensor(out=cell[turn][:], in0=forget_in[turn][:, 1, :], in1=raw["c0", d, n][:, a, :], op=ALU.mult)
+            kept[turn] = work.tile([P, H], F32, tag="kept", name="kept_%d" % turn)
+            nc.vector.tensor_tensor(out=kept[turn][:], in0=forget_in[turn][:, 1, :], in1=raw["c0", d, n][:, a, :], op=ALU.mult)
 
         def fresh_cell(turn):
-            nc.vector.tensor_tensor(out=candidate[turn][:], in0=forget_in[turn][:, 0, :], in1=candidate[turn][:], op=ALU.mult)
+            fresh[turn] = work.tile([P, H], F32, tag="fresh", name="fresh_%d" % turn)
+            nc.vector.tensor_tensor(out=fresh[turn][:], in0=forget_in[turn][:, 0, :], in1=candidate[turn][:], op=ALU.mult)
 
         def add_cell(turn):
-            nc.vector.tensor_tensor(out=cell[turn][:], in0=cell[turn][:], in1=candidate[turn][:], op=ALU.add)
+            cell[turn] = work.tile([P, H], F32, tag="cell", name="cell_%d" % turn)
+            nc.vector.tensor_tensor(out=cell[turn][:], in0=kept[turn][:], in1=fresh[turn][:], op=ALU.add)
 
         def tanh_cell(turn):
             tanh_c[turn] = work.tile([P, H], F32, tag="tanh_c", name="tanh_c_%d" % turn)
@@ -297,7 +310,7 @@ def tile_dependency_pb_kernel(
         def round_hid(turn):
             tile, d = TURNS[turn]
             own = slice(H * d, H * (d + 1))
-            nc.vector.tensor_copy(out=rounded[tile][:, 0, own], in_=hid[tile][:, own])
+            nc.scalar.copy(out=rounded[tile][:, 0, own], in_=hid[tile][:, own])
 
         back_ps = {}
         score_ps = {}
@@ -346,16 +359,15 @@ def tile_dependency_pb_kernel(
             first = P * tile
             for i, bank in enumerate(score_ps[tile]):
                 width = min(CHUNK, S - first)
-                piece = outs.tile([P, CHUNK], F32, tag="piece", name="piece_%d_%d" % (tile, i), bufs=4)
+                piece = outs.tile([P, CHUNK], F32, tag="piece", name="piece_%d_%d" % (tile, i), bufs=8)
                 if i == 0:
                     nc.vector.scalar_tensor_tensor(
-                        out=piece[:, 0:width],
-                        in0=bank[:, 0:width],
-                        scalar=fc_b_col[:, 0:1],
-                        in1=on_or_above[:, 0:width],
-                        op0=ALU.add,
-                        op1=ALU.mult,
+                        out=piece[:, 0:P], in0=bank[:, 0:P], scalar=fc_b_col[:, 0:1], in1=on_or_above[:, 0:P], op0=ALU.add, op1=ALU.mult
                     )
+                    if width > P:
+                        nc.scalar.activation(
+                            out=piece[:, P:width], in_=bank[:, P:width], func=ACT.Identity, bias=fc_b_col[:, 0:1], scale=1.0
+                        )
                 else:
                     nc.scalar.activation(out=piece[:, 0:width], in_=bank[:, 0:width], func=ACT.Identity, bias=fc_b_col[:, 0:1], scale=1.0)
                 nc.sync.dma_start(out=out_0[P * tile : P * (tile + 1), first : first + width], in_=piece[:, 0:width])
@@ -368,50 +380,52 @@ def tile_dependency_pb_kernel(
         def finished(step, offset):
             return [TURNS[turn][0] for turn in at(step, offset) if TURNS[turn][1] == 1]
 
+        def flips_of(step):
+            return [chunk for i, chunk in enumerate(FLIPS) if FLIP_STEP[i] == step]
+
         mx_done = 0
         for s in range(TURN_STEP + len(TURNS) + SCORE_STEP):
             mx_now = range(mx_done, mx_done + (MX_COUNTS[s] if s < len(MX_COUNTS) else 0))
             mx_done += len(mx_now)
-            for i, step in enumerate(FLIP_STEP):
-                if step == s:
-                    flip_chunk(FLIPS[i])
-            if s == 1:
-                flip_biases()
-                spread_pair()
             for turn in at(s, HID_STEP):
                 make_hid(turn)
             for turn in at(s, ACT_STEP):
                 activate(turn)
-                keep_cell(turn)
-            for turn in at(s, TANH_STEP):
-                tanh_cell(turn)
-            for tile in finished(s, GROUP_STEP):
-                group_hid(tile)
-            for turn in at(s, HID_STEP):
-                round_u(turn)
-            for turn in at(s, ACT_STEP):
-                fresh_cell(turn)
-            for turn in at(s, HID_STEP):
-                round_hid(turn)
-            for i, step in enumerate(FLIP_STEP):
-                if step == s - 1:
-                    quantise_chunk(FLIPS[i])
             for m in mx_now:
                 mx_product(m)
+            for chunk in flips_of(s - 1):
+                save_chunk(chunk)
+            for turn in at(s, ACT_STEP):
+                keep_cell(turn)
             for tile in finished(s, SCORE_STEP):
                 score(tile)
             for turn in at(s, ACT_STEP):
-                add_cell(turn)
-            for i, step in enumerate(FLIP_STEP):
-                if step == s:
-                    save_chunk(FLIPS[i])
+                fresh_cell(turn)
             for tile in finished(s, GROUP_STEP):
-                quantise_hid(tile)
+                group_hid(tile)
+            for turn in at(s, TANH_STEP):
+                tanh_cell(turn)
             for m in mx_now:
                 save_mx_product(m)
+            for chunk in flips_of(s - 1):
+                quantise_chunk(chunk)
+            for turn in at(s, HID_STEP):
+                round_hid(turn)
             for tile in finished(s, SCORE_STEP):
                 store_scores(tile)
+            for turn in at(s, HID_STEP):
+                round_u(turn)
+            for tile in finished(s, GROUP_STEP):
+                quantise_hid(tile)
+            for turn in at(s, ACT_STEP):
+                add_cell(turn)
             for turn in at(s, 0):
                 products(turn)
             for tile in finished(s, FLIP_BACK_STEP):
                 flip_hid(tile)
+            for chunk in flips_of(s):
+                flip_chunk(chunk)
+            if s in BIAS_STEPS:
+                flip_biases(BIAS_STEPS.index(s))
+            if s == SPREAD_STEP:
+                spread_pair()

@@ -35,18 +35,18 @@ FLIPS = (
     ("wih", 1, 0), ("wih", 1, 1), ("h0", 1, 1), ("whh", 1, 0), ("whh", 1, 1), ("y", 0, 0),
     ("h0", 0, 0), ("h0", 1, 0),
 )
-FLIP_STEP = (0, 1, 2, 3, 4, 5, 6, 7, 7, 8, 8, 9, 10, 11)
+FLIP_STEP = (0, 1, 2, 3, 4, 5, 6, 7, 7, 8, 9, 9, 10, 11)
 MX_COUNTS = (0, 0, 0, 3, 3, 0, 2, 0, 4, 4, 0, 4, 4, 4, 4)
 TURN_STEP = 6
 BIAS_STEPS = (1, 7)
-SPREAD_STEP = 6
+PAIR_STEP = 6
 
 ACT_STEP = 1
 TANH_STEP = 2
 HID_STEP = 3
-FLIP_BACK_STEP = 3
-GROUP_STEP = 4
-SCORE_STEP = 6
+FLIP_BACK_STEP = 4
+GROUP_STEP = 6
+SCORE_STEP = 8
 
 FLOPS = 2 * S * (4 * H) * D * DIRECTIONS + 2 * S * (4 * H) * H * DIRECTIONS + 2 * S * S * D
 
@@ -100,8 +100,6 @@ def tile_dependency_pb_kernel(
         make_identity(nc, ident_f32[:])
         ident_bf16 = const.tile([P, P], BF16)
         make_identity(nc, ident_bf16[:])
-        ones = const.tile([P, P], BF16)
-        nc.gpsimd.memset(ones[:], 1.0)
         on_or_above = const.tile([P, CHUNK], F32)
         nc.gpsimd.memset(on_or_above[:], 1.0)
         nc.gpsimd.affine_select(
@@ -125,7 +123,7 @@ def tile_dependency_pb_kernel(
         for d in range(DIRECTIONS):
             bias_rows.append(raws.tile([P, P], BF16, name="bias_rows_%d" % d))
             nc.vector.memset(bias_rows[d][:], 0.0)
-        pair_rows = raws.tile([P, 2, D], BF16)
+        pair_rows = raws.tile([P, P], BF16)
         nc.vector.memset(pair_rows[:], 0.0)
         for chunk in load_chunks():
             kind, d, c = chunk
@@ -134,7 +132,7 @@ def tile_dependency_pb_kernel(
                     nc.sync.dma_start(out=bias_rows[d][GATE_TILES * i : GATE_TILES * (i + 1), :], in_=vec.rearrange("(r c) -> r c", c=P))
             elif kind == "pair":
                 for i, vec in enumerate((wd, fc_w[0])):
-                    nc.sync.dma_start(out=pair_rows[0:1, i, :], in_=vec.unsqueeze(0))
+                    nc.sync.dma_start(out=pair_rows[PACK * i : PACK * (i + 1), :], in_=vec.rearrange("(r c) -> r c", c=P))
             else:
                 rows = matrices[kind][d][CHUNK * c : CHUNK * (c + 1), :]
                 raw[chunk] = raws.tile([P, ROW_TILES, rows.shape[1]], BF16, name="%s_raw_%d_%d" % chunk)
@@ -154,7 +152,7 @@ def tile_dependency_pb_kernel(
         grouped = {}
         codes, scales = {}, {}
         bias = const.tile([P, DIRECTIONS, GATE_TILES], F32)
-        pair_weight = const.tile([P, D], F32)
+        pair_weight = const.tile([P, PACK], F32)
         fc_b_col = const.tile([P, 1], F32)
         nc.gpsimd.tensor_copy(out=fc_b_col[:], in_=fc_b_bf16[:])
 
@@ -185,8 +183,8 @@ def tile_dependency_pb_kernel(
                     nc.scalar.copy(out=grouped_words[:, 2 * P * pair : 2 * P * (pair + 1), :], in_=flips[chunk][pair][:].rearrange("p v r -> p r v"))
             else:
                 flipped[chunk] = keep.tile([P, K_TILES, CHUNK], BF16, name="%sT_%d_%d" % chunk)
-                for j in range(K_TILES):
-                    nc.scalar.copy(out=flipped[chunk][:, j, :], in_=flips[chunk][j][:].rearrange("p a r -> p (a r)"))
+                for j, copy in enumerate((nc.scalar.copy, nc.vector.tensor_copy)):
+                    copy(out=flipped[chunk][:, j, :], in_=flips[chunk][j][:].rearrange("p a r -> p (a r)"))
 
         def quantise_chunk(chunk):
             if chunk[0] in ("wih", "y"):
@@ -201,13 +199,12 @@ def tile_dependency_pb_kernel(
             nc.vector.tensor_copy(out=cols[:], in_=cols_ps[:, 0 : 2 * GATE_TILES].rearrange("p (i g) -> p i g", i=2))
             nc.vector.tensor_tensor(out=bias[:, d, :], in0=cols[:, 0, :], in1=cols[:, 1, :], op=ALU.add)
 
-        def spread_pair():
-            spread = []
-            for i in range(2):
-                spread.append(psum.tile([P, D], F32, tag="bank", name="spread_%d" % i))
-                nc.tensor.matmul(spread[i][:], lhsT=ones[:], rhs=pair_rows[:, i, :], start=True, stop=True)
-            nc.vector.tensor_copy(out=pair_weight[:], in_=spread[0][:])
-            nc.vector.tensor_tensor(out=pair_weight[:], in0=spread[1][:], in1=pair_weight[:], op=ALU.mult)
+        def flip_pair():
+            cols_ps = psum.tile([P, P], BF16, tag="bank", name="flip_pair")
+            nc.tensor.transpose(cols_ps[:], pair_rows[:], ident_bf16[:])
+            cols = const.tile([P, 2, PACK], F32, name="pair_cols")
+            nc.vector.tensor_copy(out=cols[:], in_=cols_ps[:, 0 : 2 * PACK].rearrange("p (i t) -> p i t", i=2))
+            nc.vector.tensor_tensor(out=pair_weight[:], in0=cols[:, 0, :], in1=cols[:, 1, :], op=ALU.mult)
 
         mx_ps = {}
         mx_rows = {}
@@ -291,26 +288,14 @@ def tile_dependency_pb_kernel(
             nc.scalar.activation(out=tanh_c[turn][:], in_=cell[turn][:], func=ACT.Tanh)
 
         hid = {}
-        rounded = {}
 
         def make_hid(turn):
             tile, d = TURNS[turn]
             if d == 0:
-                hid[tile] = outs.tile([P, D], F32, tag="hid", name="hid_%d" % tile, bufs=5)
-                rounded[tile] = outs.tile([P, 2, D], BF16, tag="rounded", name="rounded_%d" % tile, bufs=5)
+                hid[tile] = outs.tile([P, D], F32, tag="hid", name="hid_%d" % tile, bufs=6)
             nc.vector.tensor_tensor(out=hid[tile][:, H * d : H * (d + 1)], in0=out_gate[turn][:], in1=tanh_c[turn][:], op=ALU.mult)
             if d == 1:
                 nc.sync.dma_start(out=out_1[0, P * tile : P * (tile + 1), :], in_=hid[tile][:])
-
-        def round_u(turn):
-            tile, d = TURNS[turn]
-            own = slice(H * d, H * (d + 1))
-            nc.vector.tensor_tensor(out=rounded[tile][:, 1, own], in0=hid[tile][:, own], in1=pair_weight[:, own], op=ALU.mult)
-
-        def round_hid(turn):
-            tile, d = TURNS[turn]
-            own = slice(H * d, H * (d + 1))
-            nc.scalar.copy(out=rounded[tile][:, 0, own], in_=hid[tile][:, own])
 
         back_ps = {}
         score_ps = {}
@@ -318,23 +303,29 @@ def tile_dependency_pb_kernel(
         hid_scales = keep.tile([P, S], U8, align_bytes=64)
 
         def flip_hid(tile):
-            back_ps[tile] = psum.tile([P, 2, 2 * P], F32, tag="bank", name="back_%d" % tile)
-            for what in range(2):
-                flip_words(back_ps[tile], what, rounded[tile][:, what, :].bitcast(F32))
+            back_ps[tile] = psum.tile([P, PACK, P], F32, tag="bank", name="back_%d" % tile)
+            for i in range(PACK):
+                nc.tensor.transpose(back_ps[tile][:, i, :], hid[tile][:, P * i : P * (i + 1)], ident_f32[:])
 
         def group_hid(tile):
-            grouped[tile] = stage.tile([P, 2 * P * PACK], BF16, tag="grouped_hid", name="grouped_hid_%d" % tile, align_bytes=64)
-            nc.scalar.copy(
-                out=grouped[tile][:].bitcast(F32).rearrange("p (r v) -> p r v", v=2), in_=back_ps[tile][:].rearrange("p v r -> p r v")
+            grouped[tile] = stage.tile([P, 2, P, PACK], BF16, tag="grouped_hid", name="grouped_hid_%d" % tile, align_bytes=64)
+            nc.scalar.copy(out=grouped[tile][:, 0, :, :], in_=back_ps[tile][:].rearrange("p t r -> p r t"))
+
+        def group_u(tile):
+            nc.vector.tensor_tensor(
+                out=grouped[tile][:, 1, :, :],
+                in0=back_ps[tile][:].rearrange("p t r -> p r t"),
+                in1=pair_weight[:].unsqueeze(1).to_broadcast([P, P, PACK]),
+                op=ALU.mult,
             )
 
         def quantise_hid(tile):
             codes["u", tile] = work.tile([P, P], U32, tag="u_codes", name="u_codes_%d" % tile, align_bytes=64)
             scales["u", tile] = work.tile([P, P], U8, tag="u_scales", name="u_scales_%d" % tile, align_bytes=64)
             own = slice(P * tile, P * (tile + 1))
-            nc.vector.quantize_mx(out=hid_codes[:, own].bitcast(FP8X4), scales=hid_scales[:, own], in_=grouped[tile][:, 0 : P * PACK])
+            nc.vector.quantize_mx(out=hid_codes[:, own].bitcast(FP8X4), scales=hid_scales[:, own], in_=grouped[tile][:, 0, :, :].rearrange("p r t -> p (r t)"))
             nc.vector.quantize_mx(
-                out=codes["u", tile][:].bitcast(FP8X4), scales=scales["u", tile][:], in_=grouped[tile][:, P * PACK : 2 * P * PACK]
+                out=codes["u", tile][:].bitcast(FP8X4), scales=scales["u", tile][:], in_=grouped[tile][:, 1, :, :].rearrange("p r t -> p (r t)")
             )
 
         def score(tile):
@@ -387,36 +378,34 @@ def tile_dependency_pb_kernel(
         for s in range(TURN_STEP + len(TURNS) + SCORE_STEP):
             mx_now = range(mx_done, mx_done + (MX_COUNTS[s] if s < len(MX_COUNTS) else 0))
             mx_done += len(mx_now)
-            for turn in at(s, HID_STEP):
-                make_hid(turn)
-            for turn in at(s, ACT_STEP):
-                activate(turn)
-            for m in mx_now:
-                mx_product(m)
-            for chunk in flips_of(s - 1):
-                save_chunk(chunk)
-            for turn in at(s, ACT_STEP):
-                keep_cell(turn)
-            for tile in finished(s, SCORE_STEP):
-                score(tile)
-            for turn in at(s, ACT_STEP):
-                fresh_cell(turn)
             for tile in finished(s, GROUP_STEP):
                 group_hid(tile)
-            for turn in at(s, TANH_STEP):
-                tanh_cell(turn)
+            for turn in at(s, ACT_STEP):
+                activate(turn)
+            for turn in at(s, HID_STEP):
+                make_hid(turn)
+            for chunk in flips_of(s - 1):
+                save_chunk(chunk)
             for m in mx_now:
-                save_mx_product(m)
+                mx_product(m)
+            for tile in finished(s, GROUP_STEP):
+                group_u(tile)
             for chunk in flips_of(s - 1):
                 quantise_chunk(chunk)
-            for turn in at(s, HID_STEP):
-                round_hid(turn)
-            for tile in finished(s, SCORE_STEP):
-                store_scores(tile)
-            for turn in at(s, HID_STEP):
-                round_u(turn)
+            for turn in at(s, ACT_STEP):
+                keep_cell(turn)
             for tile in finished(s, GROUP_STEP):
                 quantise_hid(tile)
+            for m in mx_now:
+                save_mx_product(m)
+            for turn in at(s, TANH_STEP):
+                tanh_cell(turn)
+            for turn in at(s, ACT_STEP):
+                fresh_cell(turn)
+            for tile in finished(s, SCORE_STEP):
+                score(tile)
+            for tile in finished(s, SCORE_STEP):
+                store_scores(tile)
             for turn in at(s, ACT_STEP):
                 add_cell(turn)
             for turn in at(s, 0):
@@ -427,5 +416,5 @@ def tile_dependency_pb_kernel(
                 flip_chunk(chunk)
             if s in BIAS_STEPS:
                 flip_biases(BIAS_STEPS.index(s))
-            if s == SPREAD_STEP:
-                spread_pair()
+            if s == PAIR_STEP:
+                flip_pair()

@@ -17,10 +17,12 @@ S = 1024
 H = 256
 D = 2 * H
 DIRECTIONS = 2
+GATES = 4
 K_TILES = H // P
 GATE_TILES = 4 * H // P
 CHUNK = 512
 ROW_TILES = CHUNK // P
+SUMT = {(1, 0): 6, (1, 1): 6, (0, 0): 6, (0, 1): 8}
 BANKS = 2
 TOKEN_TILES = S // P
 
@@ -35,18 +37,22 @@ FLIPS = (
     ("wih", 1, 0), ("wih", 1, 1), ("h0", 1, 1), ("whh", 1, 0), ("whh", 1, 1), ("y", 0, 0),
     ("h0", 0, 0), ("h0", 1, 0),
 )
-FLIP_STEP = (0, 1, 2, 3, 4, 5, 6, 7, 7, 8, 9, 9, 10, 11)
-MX_COUNTS = (0, 0, 0, 3, 3, 0, 2, 0, 4, 4, 0, 4, 4, 4, 4)
+FLIP_STEP = (0, 1, 2, 3, 4, 5, 6, 6, 7, 7, 8, 8, 9, 9)
+MX_COUNTS = (0, 0, 0, 4, 4, 0, 0, 0, 4, 4, 0, 3, 3, 3, 3, 3, 1)
 TURN_STEP = 6
+TURN_STEPS = ((0,), (1,), (2,), (3,), (4,), (5,), (6,), (7,), (8,), (9,), (10,), (11,), (12,), (13,), (14,), (15,))
 BIAS_STEPS = (1, 7)
-PAIR_STEP = 6
+SPREAD_STEP = 6
+OUT_BIAS_STEP = 3
+MX_ON_SCALAR = ((0, 2, 4, 6), (0, 1, 2, 4, 5, 6), (0, 1, 2, 4, 5, 6), (0, 1, 2, 4, 5, 6))
 
 ACT_STEP = 1
 TANH_STEP = 2
 HID_STEP = 3
 FLIP_BACK_STEP = 4
-GROUP_STEP = 6
-SCORE_STEP = 8
+GROUP_STEP = 5
+GU_STEP = 5
+SCORE_AT = (28, 26, 24, 23, 20, 19, 18, 17)
 
 FLOPS = 2 * S * (4 * H) * D * DIRECTIONS + 2 * S * (4 * H) * H * DIRECTIONS + 2 * S * S * D
 
@@ -57,6 +63,8 @@ def load_chunks():
         chunks.append(chunk)
         if chunk == ("y", 0, 1):
             chunks.append(("bias", 0, 0))
+        if chunk == ("wih", 0, 1):
+            chunks.append(("out_bias", 0, 0))
         if chunk == ("whh", 0, 1):
             chunks.extend([("c0", 0, 1), ("pair", 0, 0)])
         if chunk == ("wih", 1, 0):
@@ -100,6 +108,8 @@ def tile_dependency_pb_kernel(
         make_identity(nc, ident_f32[:])
         ident_bf16 = const.tile([P, P], BF16)
         make_identity(nc, ident_bf16[:])
+        ones = const.tile([P, P], BF16)
+        nc.gpsimd.memset(ones[:], 1.0)
         on_or_above = const.tile([P, CHUNK], F32)
         nc.gpsimd.memset(on_or_above[:], 1.0)
         nc.gpsimd.affine_select(
@@ -121,27 +131,40 @@ def tile_dependency_pb_kernel(
         raw = {}
         bias_rows = []
         for d in range(DIRECTIONS):
-            bias_rows.append(raws.tile([P, P], BF16, name="bias_rows_%d" % d))
+            bias_rows.append(raws.tile([P, H], BF16, name="bias_rows_%d" % d))
             nc.vector.memset(bias_rows[d][:], 0.0)
         pair_rows = raws.tile([P, P], BF16)
         nc.vector.memset(pair_rows[:], 0.0)
+        out_bias_rows = raws.tile([P, DIRECTIONS, H], BF16)
+        nc.vector.memset(out_bias_rows[:], 0.0)
         for chunk in load_chunks():
             kind, d, c = chunk
             if kind == "bias":
                 for i, vec in enumerate(biases[d]):
-                    nc.sync.dma_start(out=bias_rows[d][GATE_TILES * i : GATE_TILES * (i + 1), :], in_=vec.rearrange("(r c) -> r c", c=P))
+                    nc.sync.dma_start(out=bias_rows[d][GATES * i : GATES * (i + 1), :], in_=vec.rearrange("(r c) -> r c", c=H))
+            elif kind == "out_bias":
+                for d in range(DIRECTIONS):
+                    for i, vec in enumerate(biases[d]):
+                        nc.sync.dma_start(out=out_bias_rows[i : i + 1, d, :], in_=vec[3 * H : 4 * H].unsqueeze(0))
             elif kind == "pair":
                 for i, vec in enumerate((wd, fc_w[0])):
                     nc.sync.dma_start(out=pair_rows[PACK * i : PACK * (i + 1), :], in_=vec.rearrange("(r c) -> r c", c=P))
             else:
                 rows = matrices[kind][d][CHUNK * c : CHUNK * (c + 1), :]
                 raw[chunk] = raws.tile([P, ROW_TILES, rows.shape[1]], BF16, name="%s_raw_%d_%d" % chunk)
-                pieces = 2 if kind in ("y", "wih") else 1
-                for i in range(pieces):
-                    slots = slice(ROW_TILES * i // pieces, ROW_TILES * (i + 1) // pieces)
-                    nc.sync.dma_start(
-                        out=raw[chunk][:, slots, :], in_=rows[P * slots.start : P * slots.stop, :].rearrange("(a p) k -> p a k", p=P)
-                    )
+                if kind in ("wih", "whh"):
+                    for q in range(CHUNK // H):
+                        nc.sync.dma_start(
+                            out=raw[chunk][:, 2 * q : 2 * q + 2, :].rearrange("p a k -> p (a k)"),
+                            in_=rows[H * q : H * (q + 1), :].rearrange("(p a) k -> p (a k)", p=P),
+                        )
+                else:
+                    pieces = 2 if kind == "y" else 1
+                    for i in range(pieces):
+                        slots = slice(ROW_TILES * i // pieces, ROW_TILES * (i + 1) // pieces)
+                        nc.sync.dma_start(
+                            out=raw[chunk][:, slots, :], in_=rows[P * slots.start : P * slots.stop, :].rearrange("(a p) k -> p a k", p=P)
+                        )
         fc_b_bf16 = const.tile([P, 1], BF16)
         nc.sync.dma_start(out=fc_b_bf16[:], in_=fc_b.partition_broadcast(P))
         for tile in range(1, TOKEN_TILES):
@@ -169,6 +192,13 @@ def tile_dependency_pb_kernel(
                         flip_words(words_T, i, raw[chunk][:, 2 * pair + i, :].bitcast(F32))
                     flips[chunk].append(words_T)
             else:
+                if True:
+                    flip = psum.tile([P, K_TILES, ROW_TILES, P], BF16, tag="bank", name="flip_%s_%d_%d" % chunk)
+                    for j in range(K_TILES):
+                        for a in range(ROW_TILES):
+                            nc.tensor.transpose(flip[:, j, a, :], raw[chunk][:, a, P * j : P * (j + 1)], ident_bf16[:])
+                    flips[chunk].append(flip)
+                    return
                 for j in range(K_TILES):
                     flip = psum.tile([P, ROW_TILES, P], BF16, tag="bank", name="flip_%s_%d_%d_%d" % (chunk + (j,)))
                     for a in range(ROW_TILES):
@@ -179,12 +209,15 @@ def tile_dependency_pb_kernel(
             if chunk[0] in ("wih", "y"):
                 grouped[chunk] = stage.tile([P, CHUNK * PACK], BF16, tag="grouped", name="grouped_%s_%d_%d" % chunk, align_bytes=64)
                 grouped_words = grouped[chunk][:].bitcast(F32).rearrange("p (r v) -> p r v", v=2)
-                for pair in range(ROW_TILES // 2):
-                    nc.scalar.copy(out=grouped_words[:, 2 * P * pair : 2 * P * (pair + 1), :], in_=flips[chunk][pair][:].rearrange("p v r -> p r v"))
+                for pair, copy in enumerate((nc.scalar.copy, nc.scalar.copy) if chunk in FLIPS[:3] else (nc.scalar.copy, nc.scalar.copy)):
+                    copy(out=grouped_words[:, 2 * P * pair : 2 * P * (pair + 1), :], in_=flips[chunk][pair][:].rearrange("p v r -> p r v"))
             else:
                 flipped[chunk] = keep.tile([P, K_TILES, CHUNK], BF16, name="%sT_%d_%d" % chunk)
-                for j, copy in enumerate((nc.scalar.copy, nc.vector.tensor_copy)):
-                    copy(out=flipped[chunk][:, j, :], in_=flips[chunk][j][:].rearrange("p a r -> p (a r)"))
+                if True:
+                    (nc.scalar.copy, nc.vector.tensor_copy)[FLIPS.index(chunk) % 2](out=flipped[chunk][:], in_=flips[chunk][0][:].rearrange("p j a r -> p j (a r)"))
+                    return
+                for j in range(K_TILES):
+                    (nc.scalar.copy, nc.vector.tensor_copy)[j](out=flipped[chunk][:, j, :], in_=flips[chunk][j][:].rearrange("p a r -> p (a r)"))
 
         def quantise_chunk(chunk):
             if chunk[0] in ("wih", "y"):
@@ -193,11 +226,20 @@ def tile_dependency_pb_kernel(
                 nc.vector.quantize_mx(out=codes[chunk][:].bitcast(FP8X4), scales=scales[chunk][:], in_=grouped[chunk][:])
 
         def flip_biases(d):
-            cols_ps = psum.tile([P, P], BF16, tag="bank", name="flip_bias_%d" % d)
-            nc.tensor.transpose(cols_ps[:], bias_rows[d][:], ident_bf16[:])
+            cols_ps = psum.tile([P, P], F32, tag="bank", name="flip_bias_%d" % d)
+            nc.tensor.transpose(cols_ps[:], bias_rows[d][:].bitcast(F32), ident_f32[:])
             cols = const.tile([P, 2, GATE_TILES], F32, name="bias_cols_%d" % d)
-            nc.vector.tensor_copy(out=cols[:], in_=cols_ps[:, 0 : 2 * GATE_TILES].rearrange("p (i g) -> p i g", i=2))
+            nc.vector.tensor_copy(out=cols[:], in_=cols_ps[:, 0 : 2 * GATES].bitcast(BF16).rearrange("p (i g) -> p i g", i=2))
             nc.vector.tensor_tensor(out=bias[:, d, :], in0=cols[:, 0, :], in1=cols[:, 1, :], op=ALU.add)
+
+        out_bias = const.tile([P, DIRECTIONS, H], F32)
+
+        def spread_out_bias():
+            spread = psum.tile([P, DIRECTIONS, H], F32, tag="bank", name="spread_out_bias")
+            nc.tensor.matmul(
+                spread[:].rearrange("p d f -> p (d f)"), lhsT=ones[:], rhs=out_bias_rows[:].rearrange("p d f -> p (d f)"), start=True, stop=True
+            )
+            nc.scalar.copy(out=out_bias[:], in_=spread[:])
 
         def flip_pair():
             cols_ps = psum.tile([P, P], BF16, tag="bank", name="flip_pair")
@@ -207,6 +249,7 @@ def tile_dependency_pb_kernel(
             nc.vector.tensor_tensor(out=pair_weight[:], in0=cols[:, 0, :], in1=cols[:, 1, :], op=ALU.mult)
 
         mx_ps = {}
+        out_rows = {}
         mx_rows = {}
 
         def mx_product(m):
@@ -214,6 +257,20 @@ def tile_dependency_pb_kernel(
             n, d = MX_ORDER[order]
             wih, cols = ("wih", d, g // ROW_TILES), slice(P * (g % ROW_TILES), P * (g % ROW_TILES + 1))
             mx_ps[m] = psum.tile([P, CHUNK], F32, tag="bank", name="mx_%d" % m)
+            if g >= SUMT[n, d]:
+                pair = GATE_TILES - 1 - g
+                for i in range(2):
+                    tokens = slice(P * (2 * pair + i), P * (2 * pair + i + 1))
+                    nc.tensor.matmul_mx(
+                        out=mx_ps[m][:, H * i : H * (i + 1)],
+                        lhsT=codes["y", 0, n][:, tokens].bitcast(FP8X4),
+                        lhsT_scale=scales["y", 0, n][:, tokens],
+                        rhs=codes["wih", d, 1][:, H : 2 * H].bitcast(FP8X4),
+                        rhs_scale=scales["wih", d, 1][:, H : 2 * H],
+                        start=True,
+                        stop=True,
+                    )
+                return
             nc.tensor.matmul_mx(
                 out=mx_ps[m][:],
                 lhsT=codes[wih][:, cols].bitcast(FP8X4),
@@ -229,16 +286,27 @@ def tile_dependency_pb_kernel(
             n, d = MX_ORDER[order]
             if g == 0:
                 mx_rows[n, d] = keep.tile([P, GATE_TILES, CHUNK], F32, tag="mx_rows", name="mx_rows_%d_%d" % (n, d), bufs=3)
+            if g >= SUMT[n, d]:
+                if g == SUMT[n, d]:
+                    out_rows[n, d] = keep.tile([P, ROW_TILES, H], F32, tag="out_rows", name="out_rows_%d_%d" % (n, d), bufs=3)
+                pair = GATE_TILES - 1 - g
+                nc.vector.tensor_tensor(
+                    out=out_rows[n, d][:, 2 * pair : 2 * pair + 2, :].rearrange("p i (a q) -> p i a q", a=2),
+                    in0=mx_ps[m][:].rearrange("p (i a q) -> p i a q", i=2, a=2),
+                    in1=out_bias[:, d, :].rearrange("p (q a) -> p a q", a=2).unsqueeze(1).to_broadcast([P, 2, 2, P]),
+                    op=ALU.add,
+                )
+                return
             bias_col = bias[:, d, g : g + 1]
-            if g % 2 == 0:
+            if g in (((0, 1, 3, 4, 6, 7), (0, 1, 3, 4, 6, 7), (0, 1, 3, 4, 6, 7), (0, 1, 3, 4, 6, 7)))[order]:
                 nc.scalar.activation(out=mx_rows[n, d][:, g, :], in_=mx_ps[m][:], func=ACT.Identity, bias=bias_col, scale=1.0)
             else:
                 nc.vector.tensor_scalar(out=mx_rows[n, d][:, g, :], in0=mx_ps[m][:], scalar1=bias_col, scalar2=None, op0=ALU.add)
 
         gates_ps = {}
-        forget_in, candidate, out_gate, kept, fresh, cell, tanh_c = {}, {}, {}, {}, {}, {}, {}
+        forget_in, candidate, out_sum, out_gate, kept, fresh, cell, tanh_c = {}, {}, {}, {}, {}, {}, {}, {}
 
-        def products(turn):
+        def plain_products(turn):
             tile, d = TURNS[turn]
             n, a = divmod(tile, ROW_TILES)
             tokens = slice(P * a, P * (a + 1))
@@ -250,24 +318,53 @@ def tile_dependency_pb_kernel(
                     nc.tensor.matmul(
                         bank[:], lhsT=flipped["h0", d, n][:, k, tokens], rhs=flipped["whh", d, b][:, k, :], start=(k == 0), stop=False
                     )
+
+        def add_mx_products(turn):
+            tile, d = TURNS[turn]
+            n, a = divmod(tile, ROW_TILES)
+            tokens = slice(P * a, P * (a + 1))
             for b in range(BANKS):
-                for q in range(ROW_TILES):
+                summed = min(ROW_TILES, SUMT[n, d] - ROW_TILES * b)
+                for q in range(summed):
                     nc.tensor.matmul(
                         gates_ps[turn][b][:, P * q : P * (q + 1)],
                         lhsT=mx_rows[n, d][:, ROW_TILES * b + q, tokens],
                         rhs=ident_f32[:],
                         start=False,
-                        stop=(q == ROW_TILES - 1),
+                        stop=(q == summed - 1),
                         is_transpose=True,
                     )
 
         def activate(turn):
             forget_in[turn] = work.tile([P, 2, H], F32, tag="in_forget", name="in_forget_%d" % turn)
-            nc.scalar.activation(out=forget_in[turn][:].rearrange("p i f -> p (i f)"), in_=gates_ps[turn][0][:], func=ACT.Sigmoid)
+            nc.scalar.activation(
+                out=forget_in[turn][:].rearrange("p i (q a) -> p i q a", a=2),
+                in_=gates_ps[turn][0][:].rearrange("p (i a q) -> p i q a", i=2, a=2),
+                func=ACT.Sigmoid,
+            )
             candidate[turn] = work.tile([P, H], F32, tag="candidate", name="candidate_%d" % turn)
-            nc.scalar.activation(out=candidate[turn][:], in_=gates_ps[turn][1][:, 0:H], func=ACT.Tanh)
+            nc.scalar.activation(
+                out=candidate[turn][:].rearrange("p (q a) -> p q a", a=2),
+                in_=gates_ps[turn][1][:, 0:H].rearrange("p (a q) -> p q a", a=2),
+                func=ACT.Tanh,
+            )
+
+        def sum_out_gate(turn):
+            tile, d = TURNS[turn]
+            n, a = divmod(tile, ROW_TILES)
+            if SUMT[n, d] == GATE_TILES:
+                return
+            out_sum[turn] = work.tile([P, H], F32, tag="out_sum", name="out_sum_%d" % turn)
+            nc.vector.tensor_tensor(out=out_sum[turn][:], in0=gates_ps[turn][1][:, H : 2 * H], in1=out_rows[n, d][:, a, :], op=ALU.add)
+
+        def activate_out_gate(turn):
             out_gate[turn] = work.tile([P, H], F32, tag="out_gate", name="out_gate_%d" % turn)
-            nc.scalar.activation(out=out_gate[turn][:], in_=gates_ps[turn][1][:, H : 2 * H], func=ACT.Sigmoid)
+            tile, d = TURNS[turn]
+            n = tile // ROW_TILES
+            pre = out_sum[turn][:] if SUMT[n, d] < GATE_TILES else gates_ps[turn][1][:, H : 2 * H]
+            nc.scalar.activation(
+                out=out_gate[turn][:].rearrange("p (q a) -> p q a", a=2), in_=pre.rearrange("p (a q) -> p q a", a=2), func=ACT.Sigmoid
+            )
 
         def keep_cell(turn):
             tile, d = TURNS[turn]
@@ -292,7 +389,7 @@ def tile_dependency_pb_kernel(
         def make_hid(turn):
             tile, d = TURNS[turn]
             if d == 0:
-                hid[tile] = outs.tile([P, D], F32, tag="hid", name="hid_%d" % tile, bufs=6)
+                hid[tile] = outs.tile([P, D], F32, tag="hid", name="hid_%d" % tile, bufs=5)
             nc.vector.tensor_tensor(out=hid[tile][:, H * d : H * (d + 1)], in0=out_gate[turn][:], in1=tanh_c[turn][:], op=ALU.mult)
             if d == 1:
                 nc.sync.dma_start(out=out_1[0, P * tile : P * (tile + 1), :], in_=hid[tile][:])
@@ -323,6 +420,11 @@ def tile_dependency_pb_kernel(
             codes["u", tile] = work.tile([P, P], U32, tag="u_codes", name="u_codes_%d" % tile, align_bytes=64)
             scales["u", tile] = work.tile([P, P], U8, tag="u_scales", name="u_scales_%d" % tile, align_bytes=64)
             own = slice(P * tile, P * (tile + 1))
+            if False:
+                codes["both", tile] = keep.tile([P, 2 * P], U32, name="both_codes_%d" % tile, align_bytes=64)
+                scales["both", tile] = keep.tile([P, 2 * P], U8, name="both_scales_%d" % tile, align_bytes=64)
+                nc.vector.quantize_mx(out=codes["both", tile][:].bitcast(FP8X4), scales=scales["both", tile][:], in_=grouped[tile][:].rearrange("p i r t -> p (i r t)"))
+                return
             nc.vector.quantize_mx(out=hid_codes[:, own].bitcast(FP8X4), scales=hid_scales[:, own], in_=grouped[tile][:, 0, :, :].rearrange("p r t -> p (r t)"))
             nc.vector.quantize_mx(
                 out=codes["u", tile][:].bitcast(FP8X4), scales=scales["u", tile][:], in_=grouped[tile][:, 1, :, :].rearrange("p r t -> p (r t)")
@@ -333,6 +435,20 @@ def tile_dependency_pb_kernel(
             for i, pieces in enumerate(score_pieces(tile)):
                 bank = psum.tile([P, CHUNK], F32, tag="bank", name="score_%d_%d" % (tile, i))
                 score_ps[tile].append(bank)
+                if False:
+                    start = pieces[0][0]
+                    end = pieces[-1][0] + pieces[-1][1]
+                    for c in range(start // P, end // P):
+                        nc.tensor.matmul_mx(
+                            out=bank[:, P * c - start : P * (c + 1) - start],
+                            lhsT=codes["both", tile][:, P : 2 * P].bitcast(FP8X4),
+                            lhsT_scale=scales["both", tile][:, P : 2 * P],
+                            rhs=codes["both", c][:, 0:P].bitcast(FP8X4),
+                            rhs_scale=scales["both", c][:, 0:P],
+                            start=True,
+                            stop=True,
+                        )
+                    continue
                 for first, width in pieces:
                     cols = slice(first, first + width)
                     at = first - pieces[0][0]
@@ -351,7 +467,7 @@ def tile_dependency_pb_kernel(
             for i, bank in enumerate(score_ps[tile]):
                 width = min(CHUNK, S - first)
                 piece = outs.tile([P, CHUNK], F32, tag="piece", name="piece_%d_%d" % (tile, i), bufs=8)
-                if i == 0:
+                if i == 0 and False:
                     nc.vector.scalar_tensor_tensor(
                         out=piece[:, 0:P], in0=bank[:, 0:P], scalar=fc_b_col[:, 0:1], in1=on_or_above[:, 0:P], op0=ALU.add, op1=ALU.mult
                     )
@@ -359,62 +475,82 @@ def tile_dependency_pb_kernel(
                         nc.scalar.activation(
                             out=piece[:, P:width], in_=bank[:, P:width], func=ACT.Identity, bias=fc_b_col[:, 0:1], scale=1.0
                         )
+                elif i == 0:
+                    nc.vector.scalar_tensor_tensor(
+                        out=piece[:, 0:width],
+                        in0=bank[:, 0:width],
+                        scalar=fc_b_col[:, 0:1],
+                        in1=on_or_above[:, 0:width],
+                        op0=ALU.add,
+                        op1=ALU.mult,
+                    )
                 else:
                     nc.scalar.activation(out=piece[:, 0:width], in_=bank[:, 0:width], func=ACT.Identity, bias=fc_b_col[:, 0:1], scale=1.0)
                 nc.sync.dma_start(out=out_0[P * tile : P * (tile + 1), first : first + width], in_=piece[:, 0:width])
                 first += width
 
         def at(step, offset):
-            turn = step - TURN_STEP - offset
-            return [turn] if 0 <= turn < len(TURNS) else []
+            i = step - TURN_STEP - offset
+            return TURN_STEPS[i] if 0 <= i < len(TURN_STEPS) else ()
 
         def finished(step, offset):
             return [TURNS[turn][0] for turn in at(step, offset) if TURNS[turn][1] == 1]
 
-        def flips_of(step):
-            return [chunk for i, chunk in enumerate(FLIPS) if FLIP_STEP[i] == step]
+        def scored(step):
+            return [tile for tile in reversed(range(TOKEN_TILES)) if SCORE_AT[tile] == step]
 
         mx_done = 0
-        for s in range(TURN_STEP + len(TURNS) + SCORE_STEP):
+        for s in range(max(SCORE_AT) + 1):
             mx_now = range(mx_done, mx_done + (MX_COUNTS[s] if s < len(MX_COUNTS) else 0))
             mx_done += len(mx_now)
+            for turn in at(s, HID_STEP):
+                make_hid(turn)
+            for turn in at(s, ACT_STEP):
+                activate(turn)
+            for turn in at(s, ACT_STEP):
+                sum_out_gate(turn)
+            for i, step in enumerate(FLIP_STEP):
+                if step == s - 1:
+                    save_chunk(FLIPS[i])
+            for tile in scored(s):
+                score(tile)
+            for m in mx_now:
+                mx_product(m)
+            for turn in at(s, ACT_STEP):
+                keep_cell(turn)
+            for i, step in enumerate(FLIP_STEP):
+                if step == s - 1:
+                    quantise_chunk(FLIPS[i])
             for tile in finished(s, GROUP_STEP):
                 group_hid(tile)
             for turn in at(s, ACT_STEP):
-                activate(turn)
-            for turn in at(s, HID_STEP):
-                make_hid(turn)
-            for chunk in flips_of(s - 1):
-                save_chunk(chunk)
-            for m in mx_now:
-                mx_product(m)
-            for tile in finished(s, GROUP_STEP):
-                group_u(tile)
-            for chunk in flips_of(s - 1):
-                quantise_chunk(chunk)
-            for turn in at(s, ACT_STEP):
-                keep_cell(turn)
-            for tile in finished(s, GROUP_STEP):
-                quantise_hid(tile)
+                fresh_cell(turn)
             for m in mx_now:
                 save_mx_product(m)
+            for tile in finished(s, GU_STEP):
+                group_u(tile)
             for turn in at(s, TANH_STEP):
                 tanh_cell(turn)
             for turn in at(s, ACT_STEP):
-                fresh_cell(turn)
-            for tile in finished(s, SCORE_STEP):
-                score(tile)
-            for tile in finished(s, SCORE_STEP):
+                activate_out_gate(turn)
+            for tile in scored(s):
                 store_scores(tile)
             for turn in at(s, ACT_STEP):
                 add_cell(turn)
+            for tile in finished(s, GU_STEP):
+                quantise_hid(tile)
             for turn in at(s, 0):
-                products(turn)
+                plain_products(turn)
+            for turn in at(s, 0):
+                add_mx_products(turn)
             for tile in finished(s, FLIP_BACK_STEP):
                 flip_hid(tile)
-            for chunk in flips_of(s):
-                flip_chunk(chunk)
+            for i, step in enumerate(FLIP_STEP):
+                if step == s:
+                    flip_chunk(FLIPS[i])
             if s in BIAS_STEPS:
                 flip_biases(BIAS_STEPS.index(s))
-            if s == PAIR_STEP:
+            if s == SPREAD_STEP:
                 flip_pair()
+            if s == OUT_BIAS_STEP:
+                spread_out_bias()

@@ -18,75 +18,62 @@ H = 256
 D = 2 * H
 DIRECTIONS = 2
 GATES = 4
-K_TILES = H // P
-GATE_TILES = 4 * H // P
+SLOTS = H // P
+GATE_TILES = GATES * SLOTS
 CHUNK = 512
 ROW_TILES = CHUNK // P
-SUMT = {(1, 0): 6, (1, 1): 6, (0, 0): 6, (0, 1): 8}
-BANKS = 2
 TOKEN_TILES = S // P
 
-TURNS = (
-    (7, 0), (6, 0), (5, 0), (4, 0), (7, 1), (6, 1), (5, 1), (4, 1),
-    (3, 0), (2, 0), (3, 1), (2, 1), (1, 0), (1, 1), (0, 0), (0, 1),
-)
-MX_ORDER = ((1, 0), (1, 1), (0, 0), (0, 1))
+TURNS = tuple((tile, d) for tiles in ((7, 6, 5, 4), (3, 2), (1,), (0,)) for d in range(DIRECTIONS) for tile in tiles)
+SUMMED_TILES = {(1, 0): 3 * SLOTS, (1, 1): 3 * SLOTS, (0, 0): 3 * SLOTS, (0, 1): GATE_TILES}
 
 FLIPS = (
     ("y", 0, 1), ("wih", 0, 0), ("wih", 0, 1), ("h0", 0, 1), ("whh", 0, 0), ("whh", 0, 1),
-    ("wih", 1, 0), ("wih", 1, 1), ("h0", 1, 1), ("whh", 1, 0), ("whh", 1, 1), ("y", 0, 0),
-    ("h0", 0, 0), ("h0", 1, 0),
+    ("wih", 1, 0), ("wih", 1, 1), ("h0", 1, 1), ("whh", 1, 0), ("whh", 1, 1),
+    ("y", 0, 0), ("h0", 0, 0), ("h0", 1, 0),
 )
-FLIP_STEP = (0, 1, 2, 3, 4, 5, 6, 6, 7, 7, 8, 8, 9, 9)
-MX_COUNTS = (0, 0, 0, 4, 4, 0, 0, 0, 4, 4, 0, 3, 3, 3, 3, 3, 1)
+SINGLE_FLIPS = 5
+MX_RUNS = ((3, 4, GATE_TILES), (8, 4, GATE_TILES), (10, 3, 2 * GATE_TILES))
 TURN_STEP = 6
-TURN_STEPS = ((0,), (1,), (2,), (3,), (4,), (5,), (6,), (7,), (8,), (9,), (10,), (11,), (12,), (13,), (14,), (15,))
 BIAS_STEPS = (1, 7)
-SPREAD_STEP = 6
-OUT_BIAS_STEP = 3
-MX_ON_SCALAR = ((0, 2, 4, 6), (0, 1, 2, 4, 5, 6), (0, 1, 2, 4, 5, 6), (0, 1, 2, 4, 5, 6))
-
+ROW_BIAS_STEP = 3
+PAIR_STEP = 5
 ACT_STEP = 1
 TANH_STEP = 2
 HID_STEP = 3
-FLIP_BACK_STEP = 4
+BACK_STEP = 4
 GROUP_STEP = 5
-GU_STEP = 5
-SCORE_AT = (28, 26, 24, 23, 20, 19, 18, 17)
+SCORE_STEPS = (7, 9)
 
 FLOPS = 2 * S * (4 * H) * D * DIRECTIONS + 2 * S * (4 * H) * H * DIRECTIONS + 2 * S * S * D
 
 
-def load_chunks():
-    chunks = []
+def load_order():
+    others = {
+        ("wih", 0, 0): [("bias", 0, 0)],
+        ("wih", 0, 1): [("row_bias", 0, 0)],
+        ("whh", 0, 1): [("c0", 0, 1), ("pair", 0, 0)],
+        ("wih", 1, 0): [("bias", 1, 0)],
+        ("whh", 1, 1): [("c0", 1, 1)],
+        ("h0", 1, 0): [("c0", 0, 0), ("c0", 1, 0)],
+    }
+    loads = []
     for chunk in FLIPS:
-        chunks.append(chunk)
-        if chunk == ("y", 0, 1):
-            chunks.append(("bias", 0, 0))
-        if chunk == ("wih", 0, 1):
-            chunks.append(("out_bias", 0, 0))
-        if chunk == ("whh", 0, 1):
-            chunks.extend([("c0", 0, 1), ("pair", 0, 0)])
-        if chunk == ("wih", 1, 0):
-            chunks.append(("bias", 1, 0))
-        if chunk == ("whh", 1, 1):
-            chunks.append(("c0", 1, 1))
-    chunks.extend([("c0", 0, 0), ("c0", 1, 0)])
-    return chunks
+        loads.append(chunk)
+        loads.extend(others.get(chunk, []))
+    return loads
 
 
-def score_pieces(tile):
+def score_banks(tile):
     banks, first = [], P * tile
     while first < S:
-        bank, room = [], CHUNK
-        while first < S and room:
-            width = CHUNK
-            while width > min(room, S - first):
-                width //= 2
-            bank.append((first, width))
+        passes, room = [], P if tile and not banks else min(CHUNK, S - first)
+        while room:
+            width = max(w for w in (P, 2 * P, 4 * P) if w <= room)
+            passes.append((first, width))
             first += width
             room -= width
-        banks.append(bank)
+        banks.append(passes)
     return banks
 
 
@@ -101,7 +88,7 @@ def tile_dependency_pb_kernel(
         keep = stack.enter_context(tc.tile_pool(name="keep", bufs=1))
         stage = stack.enter_context(tc.tile_pool(name="stage", bufs=3))
         work = stack.enter_context(tc.tile_pool(name="work", bufs=3))
-        outs = stack.enter_context(tc.tile_pool(name="outs", bufs=3))
+        outs = stack.enter_context(tc.tile_pool(name="outs", bufs=1))
         psum = stack.enter_context(tc.psum_pool(name="psum", bufs=8))
 
         ident_f32 = const.tile([P, P], F32)
@@ -135,38 +122,41 @@ def tile_dependency_pb_kernel(
             nc.vector.memset(bias_rows[d][:], 0.0)
         pair_rows = raws.tile([P, P], BF16)
         nc.vector.memset(pair_rows[:], 0.0)
-        out_bias_rows = raws.tile([P, DIRECTIONS, H], BF16)
-        nc.vector.memset(out_bias_rows[:], 0.0)
-        for chunk in load_chunks():
-            kind, d, c = chunk
+        row_bias_rows = raws.tile([P, DIRECTIONS, H], BF16)
+        nc.vector.memset(row_bias_rows[:], 0.0)
+        for load in load_order():
+            kind, d, c = load
             if kind == "bias":
                 for i, vec in enumerate(biases[d]):
                     nc.sync.dma_start(out=bias_rows[d][GATES * i : GATES * (i + 1), :], in_=vec.rearrange("(r c) -> r c", c=H))
-            elif kind == "out_bias":
-                for d in range(DIRECTIONS):
-                    for i, vec in enumerate(biases[d]):
-                        nc.sync.dma_start(out=out_bias_rows[i : i + 1, d, :], in_=vec[3 * H : 4 * H].unsqueeze(0))
+            elif kind == "row_bias":
+                for d2 in range(DIRECTIONS):
+                    for i, vec in enumerate(biases[d2]):
+                        nc.sync.dma_start(out=row_bias_rows[i : i + 1, d2, :], in_=vec[3 * H : 4 * H].unsqueeze(0))
             elif kind == "pair":
                 for i, vec in enumerate((wd, fc_w[0])):
                     nc.sync.dma_start(out=pair_rows[PACK * i : PACK * (i + 1), :], in_=vec.rearrange("(r c) -> r c", c=P))
             else:
                 rows = matrices[kind][d][CHUNK * c : CHUNK * (c + 1), :]
-                raw[chunk] = raws.tile([P, ROW_TILES, rows.shape[1]], BF16, name="%s_raw_%d_%d" % chunk)
+                raw[load] = raws.tile([P, ROW_TILES, rows.shape[1]], BF16, name="%s_raw_%d_%d" % load)
                 if kind in ("wih", "whh"):
                     for q in range(CHUNK // H):
                         nc.sync.dma_start(
-                            out=raw[chunk][:, 2 * q : 2 * q + 2, :].rearrange("p a k -> p (a k)"),
+                            out=raw[load][:, SLOTS * q : SLOTS * (q + 1), :].rearrange("p a k -> p (a k)"),
                             in_=rows[H * q : H * (q + 1), :].rearrange("(p a) k -> p (a k)", p=P),
                         )
                 else:
-                    pieces = 2 if kind == "y" else 1
-                    for i in range(pieces):
-                        slots = slice(ROW_TILES * i // pieces, ROW_TILES * (i + 1) // pieces)
+                    halves = 2 if kind == "y" else 1
+                    n_slots = ROW_TILES // halves
+                    for i in range(halves):
                         nc.sync.dma_start(
-                            out=raw[chunk][:, slots, :], in_=rows[P * slots.start : P * slots.stop, :].rearrange("(a p) k -> p a k", p=P)
+                            out=raw[load][:, n_slots * i : n_slots * (i + 1), :],
+                            in_=rows[P * n_slots * i : P * n_slots * (i + 1), :].rearrange("(a p) k -> p a k", p=P),
                         )
         fc_b_bf16 = const.tile([P, 1], BF16)
         nc.sync.dma_start(out=fc_b_bf16[:], in_=fc_b.partition_broadcast(P))
+        fc_b_col = const.tile([P, 1], F32)
+        nc.gpsimd.tensor_copy(out=fc_b_col[:], in_=fc_b_bf16[:])
         for tile in range(1, TOKEN_TILES):
             nc.sync.dma_start(out=out_0[P * tile : P * (tile + 1), 0 : P * tile], in_=zeros[:, 0 : P * tile])
 
@@ -174,50 +164,35 @@ def tile_dependency_pb_kernel(
         flipped = {}
         grouped = {}
         codes, scales = {}, {}
-        bias = const.tile([P, DIRECTIONS, GATE_TILES], F32)
-        pair_weight = const.tile([P, PACK], F32)
-        fc_b_col = const.tile([P, 1], F32)
-        nc.gpsimd.tensor_copy(out=fc_b_col[:], in_=fc_b_bf16[:])
-
-        def flip_words(words_T, i, row_words):
-            for v in range(2):
-                nc.tensor.transpose(words_T[:, v, P * i : P * (i + 1)], row_words[:, P * v : P * (v + 1)], ident_f32[:])
 
         def flip_chunk(chunk):
+            kind = chunk[0]
             flips[chunk] = []
-            if chunk[0] in ("wih", "y"):
+            if kind in ("wih", "y"):
                 for pair in range(ROW_TILES // 2):
-                    words_T = psum.tile([P, 2, 2 * P], F32, tag="bank", name="flip_%s_%d_%d_%d" % (chunk + (pair,)))
+                    bank = psum.tile([P, 2, 2 * P], F32, tag="bank", name="flip_%s_%d_%d_%d" % (chunk + (pair,)))
                     for i in range(2):
-                        flip_words(words_T, i, raw[chunk][:, 2 * pair + i, :].bitcast(F32))
-                    flips[chunk].append(words_T)
+                        words = raw[chunk][:, 2 * pair + i, :].bitcast(F32)
+                        for v in range(2):
+                            nc.tensor.transpose(bank[:, v, P * i : P * (i + 1)], words[:, P * v : P * (v + 1)], ident_f32[:])
+                    flips[chunk].append(bank)
             else:
-                if True:
-                    flip = psum.tile([P, K_TILES, ROW_TILES, P], BF16, tag="bank", name="flip_%s_%d_%d" % chunk)
-                    for j in range(K_TILES):
-                        for a in range(ROW_TILES):
-                            nc.tensor.transpose(flip[:, j, a, :], raw[chunk][:, a, P * j : P * (j + 1)], ident_bf16[:])
-                    flips[chunk].append(flip)
-                    return
-                for j in range(K_TILES):
-                    flip = psum.tile([P, ROW_TILES, P], BF16, tag="bank", name="flip_%s_%d_%d_%d" % (chunk + (j,)))
+                bank = psum.tile([P, SLOTS, ROW_TILES, P], BF16, tag="bank", name="flip_%s_%d_%d" % chunk)
+                for j in range(SLOTS):
                     for a in range(ROW_TILES):
-                        nc.tensor.transpose(flip[:, a, :], raw[chunk][:, a, P * j : P * (j + 1)], ident_bf16[:])
-                    flips[chunk].append(flip)
+                        nc.tensor.transpose(bank[:, j, a, :], raw[chunk][:, a, P * j : P * (j + 1)], ident_bf16[:])
+                flips[chunk].append(bank)
 
         def save_chunk(chunk):
             if chunk[0] in ("wih", "y"):
                 grouped[chunk] = stage.tile([P, CHUNK * PACK], BF16, tag="grouped", name="grouped_%s_%d_%d" % chunk, align_bytes=64)
-                grouped_words = grouped[chunk][:].bitcast(F32).rearrange("p (r v) -> p r v", v=2)
-                for pair, copy in enumerate((nc.scalar.copy, nc.scalar.copy) if chunk in FLIPS[:3] else (nc.scalar.copy, nc.scalar.copy)):
-                    copy(out=grouped_words[:, 2 * P * pair : 2 * P * (pair + 1), :], in_=flips[chunk][pair][:].rearrange("p v r -> p r v"))
+                words = grouped[chunk][:].bitcast(F32).rearrange("p (r v) -> p r v", v=2)
+                second_copy = nc.scalar.copy if FLIPS.index(chunk) < SINGLE_FLIPS else nc.vector.tensor_copy
+                for pair, copy in enumerate((nc.scalar.copy, second_copy)):
+                    copy(out=words[:, 2 * P * pair : 2 * P * (pair + 1), :], in_=flips[chunk][pair][:].rearrange("p v r -> p r v"))
             else:
-                flipped[chunk] = keep.tile([P, K_TILES, CHUNK], BF16, name="%sT_%d_%d" % chunk)
-                if True:
-                    (nc.scalar.copy, nc.vector.tensor_copy)[FLIPS.index(chunk) % 2](out=flipped[chunk][:], in_=flips[chunk][0][:].rearrange("p j a r -> p j (a r)"))
-                    return
-                for j in range(K_TILES):
-                    (nc.scalar.copy, nc.vector.tensor_copy)[j](out=flipped[chunk][:, j, :], in_=flips[chunk][j][:].rearrange("p a r -> p (a r)"))
+                flipped[chunk] = keep.tile([P, SLOTS, CHUNK], BF16, name="%sT_%d_%d" % chunk)
+                nc.scalar.copy(out=flipped[chunk][:], in_=flips[chunk][0][:].rearrange("p j a r -> p j (a r)"))
 
         def quantise_chunk(chunk):
             if chunk[0] in ("wih", "y"):
@@ -225,150 +200,156 @@ def tile_dependency_pb_kernel(
                 scales[chunk] = keep.tile([P, CHUNK], U8, name="%s_scales_%d_%d" % chunk, align_bytes=64)
                 nc.vector.quantize_mx(out=codes[chunk][:].bitcast(FP8X4), scales=scales[chunk][:], in_=grouped[chunk][:])
 
-        def flip_biases(d):
-            cols_ps = psum.tile([P, P], F32, tag="bank", name="flip_bias_%d" % d)
-            nc.tensor.transpose(cols_ps[:], bias_rows[d][:].bitcast(F32), ident_f32[:])
+        bias = const.tile([P, DIRECTIONS, GATE_TILES], F32)
+        row_bias = const.tile([P, DIRECTIONS, H], F32)
+        pair_weight = const.tile([P, PACK], F32)
+
+        def flip_bias(d):
+            bank = psum.tile([P, P], F32, tag="bank", name="flip_bias_%d" % d)
+            nc.tensor.transpose(bank[:], bias_rows[d][:].bitcast(F32), ident_f32[:])
             cols = const.tile([P, 2, GATE_TILES], F32, name="bias_cols_%d" % d)
-            nc.vector.tensor_copy(out=cols[:], in_=cols_ps[:, 0 : 2 * GATES].bitcast(BF16).rearrange("p (i g) -> p i g", i=2))
+            nc.vector.tensor_copy(out=cols[:], in_=bank[:, 0 : 2 * GATES].bitcast(BF16).rearrange("p (i g) -> p i g", i=2))
             nc.vector.tensor_tensor(out=bias[:, d, :], in0=cols[:, 0, :], in1=cols[:, 1, :], op=ALU.add)
 
-        out_bias = const.tile([P, DIRECTIONS, H], F32)
-
-        def spread_out_bias():
-            spread = psum.tile([P, DIRECTIONS, H], F32, tag="bank", name="spread_out_bias")
+        def spread_row_bias():
+            bank = psum.tile([P, DIRECTIONS, H], F32, tag="bank", name="spread_row_bias")
             nc.tensor.matmul(
-                spread[:].rearrange("p d f -> p (d f)"), lhsT=ones[:], rhs=out_bias_rows[:].rearrange("p d f -> p (d f)"), start=True, stop=True
+                bank[:].rearrange("p d f -> p (d f)"),
+                lhsT=ones[:],
+                rhs=row_bias_rows[:].rearrange("p d f -> p (d f)"),
+                start=True,
+                stop=True,
             )
-            nc.scalar.copy(out=out_bias[:], in_=spread[:])
+            nc.scalar.copy(out=row_bias[:], in_=bank[:])
 
         def flip_pair():
-            cols_ps = psum.tile([P, P], BF16, tag="bank", name="flip_pair")
-            nc.tensor.transpose(cols_ps[:], pair_rows[:], ident_bf16[:])
+            bank = psum.tile([P, P], BF16, tag="bank", name="flip_pair")
+            nc.tensor.transpose(bank[:], pair_rows[:], ident_bf16[:])
             cols = const.tile([P, 2, PACK], F32, name="pair_cols")
-            nc.vector.tensor_copy(out=cols[:], in_=cols_ps[:, 0 : 2 * PACK].rearrange("p (i t) -> p i t", i=2))
+            nc.vector.tensor_copy(out=cols[:], in_=bank[:, 0 : 2 * PACK].rearrange("p (i t) -> p i t", i=2))
             nc.vector.tensor_tensor(out=pair_weight[:], in0=cols[:, 0, :], in1=cols[:, 1, :], op=ALU.mult)
 
         mx_ps = {}
-        out_rows = {}
+        mx_cols = {}
         mx_rows = {}
 
-        def mx_product(m):
-            order, g = divmod(m, GATE_TILES)
-            n, d = MX_ORDER[order]
-            wih, cols = ("wih", d, g // ROW_TILES), slice(P * (g % ROW_TILES), P * (g % ROW_TILES + 1))
-            mx_ps[m] = psum.tile([P, CHUNK], F32, tag="bank", name="mx_%d" % m)
-            if g >= SUMT[n, d]:
-                pair = GATE_TILES - 1 - g
-                for i in range(2):
-                    tokens = slice(P * (2 * pair + i), P * (2 * pair + i + 1))
-                    nc.tensor.matmul_mx(
-                        out=mx_ps[m][:, H * i : H * (i + 1)],
-                        lhsT=codes["y", 0, n][:, tokens].bitcast(FP8X4),
-                        lhsT_scale=scales["y", 0, n][:, tokens],
-                        rhs=codes["wih", d, 1][:, H : 2 * H].bitcast(FP8X4),
-                        rhs_scale=scales["wih", d, 1][:, H : 2 * H],
-                        start=True,
-                        stop=True,
-                    )
-                return
+        def matmul_mx(out, stationary, stationary_cols, moving, moving_cols):
             nc.tensor.matmul_mx(
-                out=mx_ps[m][:],
-                lhsT=codes[wih][:, cols].bitcast(FP8X4),
-                lhsT_scale=scales[wih][:, cols],
-                rhs=codes["y", 0, n][:].bitcast(FP8X4),
-                rhs_scale=scales["y", 0, n][:],
+                out=out,
+                lhsT=codes[stationary][:, stationary_cols].bitcast(FP8X4),
+                lhsT_scale=scales[stationary][:, stationary_cols],
+                rhs=codes[moving][:, moving_cols].bitcast(FP8X4),
+                rhs_scale=scales[moving][:, moving_cols],
                 start=True,
                 stop=True,
             )
 
+        def mx_place(m):
+            half, g = divmod(m, GATE_TILES)
+            return list(SUMMED_TILES)[half] + (g,)
+
+        def mx_product(m):
+            n, d, g = mx_place(m)
+            mx_ps[m] = psum.tile([P, CHUNK], F32, tag="bank", name="mx_%d" % m)
+            if g < SUMMED_TILES[n, d]:
+                c, slot = divmod(g, ROW_TILES)
+                matmul_mx(mx_ps[m][:], ("wih", d, c), slice(P * slot, P * (slot + 1)), ("y", 0, n), slice(0, CHUNK))
+            else:
+                for i in range(2):
+                    a = 2 * (GATE_TILES - 1 - g) + i
+                    matmul_mx(mx_ps[m][:, H * i : H * (i + 1)], ("y", 0, n), slice(P * a, P * (a + 1)), ("wih", d, 1), slice(H, 2 * H))
+
         def save_mx_product(m):
-            order, g = divmod(m, GATE_TILES)
-            n, d = MX_ORDER[order]
+            n, d, g = mx_place(m)
             if g == 0:
-                mx_rows[n, d] = keep.tile([P, GATE_TILES, CHUNK], F32, tag="mx_rows", name="mx_rows_%d_%d" % (n, d), bufs=3)
-            if g >= SUMT[n, d]:
-                if g == SUMT[n, d]:
-                    out_rows[n, d] = keep.tile([P, ROW_TILES, H], F32, tag="out_rows", name="out_rows_%d_%d" % (n, d), bufs=3)
-                pair = GATE_TILES - 1 - g
+                mx_cols[n, d] = keep.tile([P, GATE_TILES, CHUNK], F32, tag="mx_cols", name="mx_cols_%d_%d" % (n, d), bufs=3)
+                mx_rows[n, d] = keep.tile([P, ROW_TILES, H], F32, tag="mx_rows", name="mx_rows_%d_%d" % (n, d), bufs=3)
+            if g >= SUMMED_TILES[n, d]:
+                a = 2 * (GATE_TILES - 1 - g)
                 nc.vector.tensor_tensor(
-                    out=out_rows[n, d][:, 2 * pair : 2 * pair + 2, :].rearrange("p i (a q) -> p i a q", a=2),
-                    in0=mx_ps[m][:].rearrange("p (i a q) -> p i a q", i=2, a=2),
-                    in1=out_bias[:, d, :].rearrange("p (q a) -> p a q", a=2).unsqueeze(1).to_broadcast([P, 2, 2, P]),
+                    out=mx_rows[n, d][:, a : a + 2, :].rearrange("p i (a q) -> p i a q", a=SLOTS),
+                    in0=mx_ps[m][:].rearrange("p (i a q) -> p i a q", i=2, a=SLOTS),
+                    in1=row_bias[:, d, :].rearrange("p (q a) -> p a q", a=SLOTS).unsqueeze(1).to_broadcast([P, 2, SLOTS, P]),
                     op=ALU.add,
                 )
-                return
-            bias_col = bias[:, d, g : g + 1]
-            if g in (((0, 1, 3, 4, 6, 7), (0, 1, 3, 4, 6, 7), (0, 1, 3, 4, 6, 7), (0, 1, 3, 4, 6, 7)))[order]:
-                nc.scalar.activation(out=mx_rows[n, d][:, g, :], in_=mx_ps[m][:], func=ACT.Identity, bias=bias_col, scale=1.0)
+            elif g % 3 < 2:
+                nc.scalar.activation(
+                    out=mx_cols[n, d][:, g, :], in_=mx_ps[m][:], func=ACT.Identity, bias=bias[:, d, g : g + 1], scale=1.0
+                )
             else:
-                nc.vector.tensor_scalar(out=mx_rows[n, d][:, g, :], in0=mx_ps[m][:], scalar1=bias_col, scalar2=None, op0=ALU.add)
+                nc.vector.tensor_scalar(
+                    out=mx_cols[n, d][:, g, :], in0=mx_ps[m][:], scalar1=bias[:, d, g : g + 1], scalar2=None, op0=ALU.add
+                )
 
         gates_ps = {}
-        forget_in, candidate, out_sum, out_gate, kept, fresh, cell, tanh_c = {}, {}, {}, {}, {}, {}, {}, {}
+        forget_in, candidate, out_sum, out_gate = {}, {}, {}, {}
+        kept, fresh, cell, tanh_c = {}, {}, {}, {}
+
+        def place(turn):
+            tile, d = TURNS[turn]
+            return (tile, d) + divmod(tile, ROW_TILES)
 
         def plain_products(turn):
-            tile, d = TURNS[turn]
-            n, a = divmod(tile, ROW_TILES)
-            tokens = slice(P * a, P * (a + 1))
+            tile, d, n, a = place(turn)
             gates_ps[turn] = []
-            for b in range(BANKS):
+            for b in range(2):
                 bank = psum.tile([P, CHUNK], F32, tag="bank", name="gates_%d_%d" % (turn, b))
                 gates_ps[turn].append(bank)
-                for k in range(K_TILES):
+                for k in range(SLOTS):
                     nc.tensor.matmul(
-                        bank[:], lhsT=flipped["h0", d, n][:, k, tokens], rhs=flipped["whh", d, b][:, k, :], start=(k == 0), stop=False
+                        bank[:],
+                        lhsT=flipped["h0", d, n][:, k, P * a : P * (a + 1)],
+                        rhs=flipped["whh", d, b][:, k, :],
+                        start=(k == 0),
+                        stop=False,
                     )
 
         def add_mx_products(turn):
-            tile, d = TURNS[turn]
-            n, a = divmod(tile, ROW_TILES)
-            tokens = slice(P * a, P * (a + 1))
-            for b in range(BANKS):
-                summed = min(ROW_TILES, SUMT[n, d] - ROW_TILES * b)
-                for q in range(summed):
-                    nc.tensor.matmul(
-                        gates_ps[turn][b][:, P * q : P * (q + 1)],
-                        lhsT=mx_rows[n, d][:, ROW_TILES * b + q, tokens],
-                        rhs=ident_f32[:],
-                        start=False,
-                        stop=(q == summed - 1),
-                        is_transpose=True,
-                    )
+            tile, d, n, a = place(turn)
+            for g in range(SUMMED_TILES[n, d]):
+                b, slot = divmod(g, ROW_TILES)
+                nc.tensor.matmul(
+                    gates_ps[turn][b][:, P * slot : P * (slot + 1)],
+                    lhsT=mx_cols[n, d][:, g, P * a : P * (a + 1)],
+                    rhs=ident_f32[:],
+                    start=False,
+                    stop=(g in (ROW_TILES - 1, SUMMED_TILES[n, d] - 1)),
+                    is_transpose=True,
+                )
 
         def activate(turn):
-            forget_in[turn] = work.tile([P, 2, H], F32, tag="in_forget", name="in_forget_%d" % turn)
+            forget_in[turn] = work.tile([P, 2, H], F32, tag="forget_in", name="forget_in_%d" % turn)
             nc.scalar.activation(
-                out=forget_in[turn][:].rearrange("p i (q a) -> p i q a", a=2),
-                in_=gates_ps[turn][0][:].rearrange("p (i a q) -> p i q a", i=2, a=2),
+                out=forget_in[turn][:].rearrange("p i (q a) -> p i q a", a=SLOTS),
+                in_=gates_ps[turn][0][:].rearrange("p (i a q) -> p i q a", i=2, a=SLOTS),
                 func=ACT.Sigmoid,
             )
             candidate[turn] = work.tile([P, H], F32, tag="candidate", name="candidate_%d" % turn)
             nc.scalar.activation(
-                out=candidate[turn][:].rearrange("p (q a) -> p q a", a=2),
-                in_=gates_ps[turn][1][:, 0:H].rearrange("p (a q) -> p q a", a=2),
+                out=candidate[turn][:].rearrange("p (q a) -> p q a", a=SLOTS),
+                in_=gates_ps[turn][1][:, 0:H].rearrange("p (a q) -> p q a", a=SLOTS),
                 func=ACT.Tanh,
             )
 
         def sum_out_gate(turn):
-            tile, d = TURNS[turn]
-            n, a = divmod(tile, ROW_TILES)
-            if SUMT[n, d] == GATE_TILES:
+            tile, d, n, a = place(turn)
+            if SUMMED_TILES[n, d] == GATE_TILES:
+                out_sum[turn] = gates_ps[turn][1][:, H : 2 * H]
                 return
             out_sum[turn] = work.tile([P, H], F32, tag="out_sum", name="out_sum_%d" % turn)
-            nc.vector.tensor_tensor(out=out_sum[turn][:], in0=gates_ps[turn][1][:, H : 2 * H], in1=out_rows[n, d][:, a, :], op=ALU.add)
+            out_sum[turn] = out_sum[turn][:]
+            nc.vector.tensor_tensor(out=out_sum[turn], in0=gates_ps[turn][1][:, H : 2 * H], in1=mx_rows[n, d][:, a, :], op=ALU.add)
 
         def activate_out_gate(turn):
             out_gate[turn] = work.tile([P, H], F32, tag="out_gate", name="out_gate_%d" % turn)
-            tile, d = TURNS[turn]
-            n = tile // ROW_TILES
-            pre = out_sum[turn][:] if SUMT[n, d] < GATE_TILES else gates_ps[turn][1][:, H : 2 * H]
             nc.scalar.activation(
-                out=out_gate[turn][:].rearrange("p (q a) -> p q a", a=2), in_=pre.rearrange("p (a q) -> p q a", a=2), func=ACT.Sigmoid
+                out=out_gate[turn][:].rearrange("p (q a) -> p q a", a=SLOTS),
+                in_=out_sum[turn].rearrange("p (a q) -> p q a", a=SLOTS),
+                func=ACT.Sigmoid,
             )
 
         def keep_cell(turn):
-            tile, d = TURNS[turn]
-            n, a = divmod(tile, ROW_TILES)
+            tile, d, n, a = place(turn)
             kept[turn] = work.tile([P, H], F32, tag="kept", name="kept_%d" % turn)
             nc.vector.tensor_tensor(out=kept[turn][:], in0=forget_in[turn][:, 1, :], in1=raw["c0", d, n][:, a, :], op=ALU.mult)
 
@@ -384,25 +365,22 @@ def tile_dependency_pb_kernel(
             tanh_c[turn] = work.tile([P, H], F32, tag="tanh_c", name="tanh_c_%d" % turn)
             nc.scalar.activation(out=tanh_c[turn][:], in_=cell[turn][:], func=ACT.Tanh)
 
-        hid = {}
+        hid, back_ps, score_ps, u_codes, u_scales = {}, {}, {}, {}, {}
+        hid_codes = keep.tile([P, S], U32, align_bytes=64)
+        hid_scales = keep.tile([P, S], U8, align_bytes=64)
 
         def make_hid(turn):
-            tile, d = TURNS[turn]
+            tile, d, n, a = place(turn)
             if d == 0:
                 hid[tile] = outs.tile([P, D], F32, tag="hid", name="hid_%d" % tile, bufs=5)
             nc.vector.tensor_tensor(out=hid[tile][:, H * d : H * (d + 1)], in0=out_gate[turn][:], in1=tanh_c[turn][:], op=ALU.mult)
             if d == 1:
                 nc.sync.dma_start(out=out_1[0, P * tile : P * (tile + 1), :], in_=hid[tile][:])
 
-        back_ps = {}
-        score_ps = {}
-        hid_codes = keep.tile([P, S], U32, align_bytes=64)
-        hid_scales = keep.tile([P, S], U8, align_bytes=64)
-
         def flip_hid(tile):
             back_ps[tile] = psum.tile([P, PACK, P], F32, tag="bank", name="back_%d" % tile)
-            for i in range(PACK):
-                nc.tensor.transpose(back_ps[tile][:, i, :], hid[tile][:, P * i : P * (i + 1)], ident_f32[:])
+            for t in range(PACK):
+                nc.tensor.transpose(back_ps[tile][:, t, :], hid[tile][:, P * t : P * (t + 1)], ident_f32[:])
 
         def group_hid(tile):
             grouped[tile] = stage.tile([P, 2, P, PACK], BF16, tag="grouped_hid", name="grouped_hid_%d" % tile, align_bytes=64)
@@ -416,66 +394,36 @@ def tile_dependency_pb_kernel(
                 op=ALU.mult,
             )
 
-        def quantise_hid(tile):
-            codes["u", tile] = work.tile([P, P], U32, tag="u_codes", name="u_codes_%d" % tile, align_bytes=64)
-            scales["u", tile] = work.tile([P, P], U8, tag="u_scales", name="u_scales_%d" % tile, align_bytes=64)
-            own = slice(P * tile, P * (tile + 1))
-            if False:
-                codes["both", tile] = keep.tile([P, 2 * P], U32, name="both_codes_%d" % tile, align_bytes=64)
-                scales["both", tile] = keep.tile([P, 2 * P], U8, name="both_scales_%d" % tile, align_bytes=64)
-                nc.vector.quantize_mx(out=codes["both", tile][:].bitcast(FP8X4), scales=scales["both", tile][:], in_=grouped[tile][:].rearrange("p i r t -> p (i r t)"))
-                return
-            nc.vector.quantize_mx(out=hid_codes[:, own].bitcast(FP8X4), scales=hid_scales[:, own], in_=grouped[tile][:, 0, :, :].rearrange("p r t -> p (r t)"))
-            nc.vector.quantize_mx(
-                out=codes["u", tile][:].bitcast(FP8X4), scales=scales["u", tile][:], in_=grouped[tile][:, 1, :, :].rearrange("p r t -> p (r t)")
-            )
+        def quantise_tile(tile):
+            cols = slice(P * tile, P * (tile + 1))
+            u_codes[tile] = work.tile([P, P], U32, tag="u_codes", name="u_codes_%d" % tile, align_bytes=64)
+            u_scales[tile] = work.tile([P, P], U8, tag="u_scales", name="u_scales_%d" % tile, align_bytes=64)
+            for i, (code, scale) in enumerate(((hid_codes[:, cols], hid_scales[:, cols]), (u_codes[tile][:], u_scales[tile][:]))):
+                nc.vector.quantize_mx(out=code.bitcast(FP8X4), scales=scale, in_=grouped[tile][:, i, :, :].rearrange("p r t -> p (r t)"))
 
         def score(tile):
             score_ps[tile] = []
-            for i, pieces in enumerate(score_pieces(tile)):
+            for i, passes in enumerate(score_banks(tile)):
                 bank = psum.tile([P, CHUNK], F32, tag="bank", name="score_%d_%d" % (tile, i))
                 score_ps[tile].append(bank)
-                if False:
-                    start = pieces[0][0]
-                    end = pieces[-1][0] + pieces[-1][1]
-                    for c in range(start // P, end // P):
-                        nc.tensor.matmul_mx(
-                            out=bank[:, P * c - start : P * (c + 1) - start],
-                            lhsT=codes["both", tile][:, P : 2 * P].bitcast(FP8X4),
-                            lhsT_scale=scales["both", tile][:, P : 2 * P],
-                            rhs=codes["both", c][:, 0:P].bitcast(FP8X4),
-                            rhs_scale=scales["both", c][:, 0:P],
-                            start=True,
-                            stop=True,
-                        )
-                    continue
-                for first, width in pieces:
-                    cols = slice(first, first + width)
-                    at = first - pieces[0][0]
+                for first, width in passes:
+                    start = first - passes[0][0]
                     nc.tensor.matmul_mx(
-                        out=bank[:, at : at + width],
-                        lhsT=codes["u", tile][:].bitcast(FP8X4),
-                        lhsT_scale=scales["u", tile][:],
-                        rhs=hid_codes[:, cols].bitcast(FP8X4),
-                        rhs_scale=hid_scales[:, cols],
+                        out=bank[:, start : start + width],
+                        lhsT=u_codes[tile][:].bitcast(FP8X4),
+                        lhsT_scale=u_scales[tile][:],
+                        rhs=hid_codes[:, first : first + width].bitcast(FP8X4),
+                        rhs_scale=hid_scales[:, first : first + width],
                         start=True,
                         stop=True,
                     )
 
         def store_scores(tile):
-            first = P * tile
-            for i, bank in enumerate(score_ps[tile]):
-                width = min(CHUNK, S - first)
+            for i, passes in enumerate(score_banks(tile)):
+                bank = score_ps[tile][i]
+                first, width = passes[0][0], sum(w for f, w in passes)
                 piece = outs.tile([P, CHUNK], F32, tag="piece", name="piece_%d_%d" % (tile, i), bufs=8)
-                if i == 0 and False:
-                    nc.vector.scalar_tensor_tensor(
-                        out=piece[:, 0:P], in0=bank[:, 0:P], scalar=fc_b_col[:, 0:1], in1=on_or_above[:, 0:P], op0=ALU.add, op1=ALU.mult
-                    )
-                    if width > P:
-                        nc.scalar.activation(
-                            out=piece[:, P:width], in_=bank[:, P:width], func=ACT.Identity, bias=fc_b_col[:, 0:1], scale=1.0
-                        )
-                elif i == 0:
+                if i == 0:
                     nc.vector.scalar_tensor_tensor(
                         out=piece[:, 0:width],
                         in0=bank[:, 0:width],
@@ -487,70 +435,70 @@ def tile_dependency_pb_kernel(
                 else:
                     nc.scalar.activation(out=piece[:, 0:width], in_=bank[:, 0:width], func=ACT.Identity, bias=fc_b_col[:, 0:1], scale=1.0)
                 nc.sync.dma_start(out=out_0[P * tile : P * (tile + 1), first : first + width], in_=piece[:, 0:width])
-                first += width
 
-        def at(step, offset):
-            i = step - TURN_STEP - offset
-            return TURN_STEPS[i] if 0 <= i < len(TURN_STEPS) else ()
+        def flipped_in(step):
+            return [chunk for i, chunk in enumerate(FLIPS) if step == i - max(0, i - SINGLE_FLIPS + 1) // 2]
 
-        def finished(step, offset):
-            return [TURNS[turn][0] for turn in at(step, offset) if TURNS[turn][1] == 1]
+        mx_steps = [first + m // rate for first, rate, count in MX_RUNS for m in range(count)]
 
-        def scored(step):
-            return [tile for tile in reversed(range(TOKEN_TILES)) if SCORE_AT[tile] == step]
+        def turns_at(step, offset):
+            turn = step - TURN_STEP - offset
+            return [turn] if 0 <= turn < len(TURNS) else []
 
-        mx_done = 0
-        for s in range(max(SCORE_AT) + 1):
-            mx_now = range(mx_done, mx_done + (MX_COUNTS[s] if s < len(MX_COUNTS) else 0))
-            mx_done += len(mx_now)
-            for turn in at(s, HID_STEP):
+        def tiles_at(step, offset):
+            return [TURNS[turn][0] for turn in turns_at(step, offset) if TURNS[turn][1] == 1]
+
+        def scored_at(step):
+            return [tile for n, offset in enumerate(SCORE_STEPS) for tile in tiles_at(step, offset) if tile // ROW_TILES == n]
+
+        for s in range(TURN_STEP + len(TURNS) + max(SCORE_STEPS)):
+            mx_now = [m for m, step in enumerate(mx_steps) if step == s]
+            for turn in turns_at(s, HID_STEP):
                 make_hid(turn)
-            for turn in at(s, ACT_STEP):
+            for turn in turns_at(s, ACT_STEP):
                 activate(turn)
-            for turn in at(s, ACT_STEP):
-                sum_out_gate(turn)
-            for i, step in enumerate(FLIP_STEP):
-                if step == s - 1:
-                    save_chunk(FLIPS[i])
-            for tile in scored(s):
-                score(tile)
+            for chunk in flipped_in(s - 1):
+                save_chunk(chunk)
             for m in mx_now:
                 mx_product(m)
-            for turn in at(s, ACT_STEP):
+            for turn in turns_at(s, ACT_STEP):
                 keep_cell(turn)
-            for i, step in enumerate(FLIP_STEP):
-                if step == s - 1:
-                    quantise_chunk(FLIPS[i])
-            for tile in finished(s, GROUP_STEP):
+            for tile in scored_at(s):
+                score(tile)
+            for turn in turns_at(s, ACT_STEP):
+                sum_out_gate(turn)
+            for tile in tiles_at(s, GROUP_STEP):
                 group_hid(tile)
-            for turn in at(s, ACT_STEP):
+            for turn in turns_at(s, ACT_STEP):
                 fresh_cell(turn)
+            for chunk in flipped_in(s - 1):
+                quantise_chunk(chunk)
+            for tile in tiles_at(s, GROUP_STEP):
+                group_u(tile)
+            for turn in turns_at(s, TANH_STEP):
+                tanh_cell(turn)
+            for turn in turns_at(s, ACT_STEP):
+                add_cell(turn)
+            for tile in tiles_at(s, GROUP_STEP):
+                quantise_tile(tile)
             for m in mx_now:
                 save_mx_product(m)
-            for tile in finished(s, GU_STEP):
-                group_u(tile)
-            for turn in at(s, TANH_STEP):
-                tanh_cell(turn)
-            for turn in at(s, ACT_STEP):
+            for turn in turns_at(s, ACT_STEP):
                 activate_out_gate(turn)
-            for tile in scored(s):
+            for tile in scored_at(s):
                 store_scores(tile)
-            for turn in at(s, ACT_STEP):
-                add_cell(turn)
-            for tile in finished(s, GU_STEP):
-                quantise_hid(tile)
-            for turn in at(s, 0):
+            for turn in turns_at(s, 0):
                 plain_products(turn)
-            for turn in at(s, 0):
+            for turn in turns_at(s, 0):
                 add_mx_products(turn)
-            for tile in finished(s, FLIP_BACK_STEP):
+            for tile in tiles_at(s, BACK_STEP):
                 flip_hid(tile)
-            for i, step in enumerate(FLIP_STEP):
+            for chunk in flipped_in(s):
+                flip_chunk(chunk)
+            for d, step in enumerate(BIAS_STEPS):
                 if step == s:
-                    flip_chunk(FLIPS[i])
-            if s in BIAS_STEPS:
-                flip_biases(BIAS_STEPS.index(s))
-            if s == SPREAD_STEP:
+                    flip_bias(d)
+            if s == PAIR_STEP:
                 flip_pair()
-            if s == OUT_BIAS_STEP:
-                spread_out_bias()
+            if s == ROW_BIAS_STEP:
+                spread_row_bias()

@@ -37,6 +37,7 @@ MX_RUNS = ((3, 4, GATE_TILES), (8, 4, GATE_TILES), (10, 3, 2 * GATE_TILES))
 TURN_STEP = 6
 BIAS_STEPS = (1, 7)
 ROW_BIAS_STEP = 3
+WARM_STEPS = (1, 2)
 PAIR_STEP = 5
 ACT_STEP = 1
 TANH_STEP = 2
@@ -97,6 +98,8 @@ def tile_dependency_pb_kernel(
         make_identity(nc, ident_bf16[:])
         ones = const.tile([P, P], BF16)
         nc.gpsimd.memset(ones[:], 1.0)
+        idle_operand = const.tile([P, CHUNK], BF16)
+        nc.gpsimd.memset(idle_operand[:], 0.0)
         on_or_above = const.tile([P, CHUNK], F32)
         nc.gpsimd.memset(on_or_above[:], 1.0)
         nc.gpsimd.affine_select(
@@ -199,6 +202,10 @@ def tile_dependency_pb_kernel(
                 codes[chunk] = keep.tile([P, CHUNK], U32, name="%s_codes_%d_%d" % chunk, align_bytes=64)
                 scales[chunk] = keep.tile([P, CHUNK], U8, name="%s_scales_%d_%d" % chunk, align_bytes=64)
                 nc.vector.quantize_mx(out=codes[chunk][:].bitcast(FP8X4), scales=scales[chunk][:], in_=grouped[chunk][:])
+
+        def warm_up(s):
+            bank = psum.tile([P, CHUNK], F32, tag="bank", name="warm_up_%d" % s)
+            nc.tensor.matmul(bank[:], lhsT=ones[:], rhs=idle_operand[:], start=True, stop=True)
 
         bias = const.tile([P, DIRECTIONS, GATE_TILES], F32)
         row_bias = const.tile([P, DIRECTIONS, H], F32)
@@ -495,6 +502,9 @@ def tile_dependency_pb_kernel(
                 flip_hid(tile)
             for chunk in flipped_in(s):
                 flip_chunk(chunk)
+            if s in WARM_STEPS:
+                warm_up(s)
+                warm_up(s + 100)
             for d, step in enumerate(BIAS_STEPS):
                 if step == s:
                     flip_bias(d)

from contextlib import ExitStack

import concourse.mybir as mybir
from concourse.masks import make_identity

BF16 = mybir.dt.bfloat16
F32 = mybir.dt.float32
U32 = mybir.dt.uint32
U8 = mybir.dt.uint8
FP8X4 = mybir.dt.float8_e4m3fn_x4
ACT = mybir.ActivationFunctionType
ALU = mybir.AluOpType

P = 128
PACK = 4
S = 1024
H = 256
D = 2 * H
DIRECTIONS = 2
GATES = 4
SLOTS = H // P
GATE_TILES = GATES * SLOTS
CHUNK = 512
ROW_TILES = CHUNK // P
TOKEN_TILES = S // P

TURNS = tuple((tile, d) for tiles in ((7, 6, 5, 4), (3, 2), (1,), (0,)) for d in range(DIRECTIONS) for tile in tiles)
SUMMED_TILES = {(1, 0): 3 * SLOTS, (1, 1): 3 * SLOTS, (0, 0): 3 * SLOTS, (0, 1): GATE_TILES}

FLIPS = (
    ("y", 0, 1), ("wih", 0, 0), ("wih", 0, 1), ("h0", 0, 1), ("whh", 0, 0), ("whh", 0, 1),
    ("wih", 1, 0), ("wih", 1, 1), ("h0", 1, 1), ("whh", 1, 0), ("whh", 1, 1),
    ("y", 0, 0), ("h0", 0, 0), ("h0", 1, 0),
)
SINGLE_FLIPS = 5
MX_RUNS = ((3, 4, GATE_TILES), (8, 4, GATE_TILES), (10, 3, 2 * GATE_TILES))
TURN_STEP = 6
BIAS_STEPS = (1, 7)
ROW_BIAS_STEP = 3
WARM_STEPS = (1, 2)
PAIR_STEP = 5
ACT_STEP = 1
TANH_STEP = 2
HID_STEP = 3
BACK_STEP = 4
GROUP_STEP = 5
SCORE_STEPS = (7, 9)

FLOPS = 2 * S * (4 * H) * D * DIRECTIONS + 2 * S * (4 * H) * H * DIRECTIONS + 2 * S * S * D


def load_order():
    others = {
        ("wih", 0, 0): [("bias", 0, 0)],
        ("wih", 0, 1): [("row_bias", 0, 0)],
        ("whh", 0, 1): [("c0", 0, 1), ("pair", 0, 0)],
        ("wih", 1, 0): [("bias", 1, 0)],
        ("whh", 1, 1): [("c0", 1, 1)],
        ("h0", 1, 0): [("c0", 0, 0), ("c0", 1, 0)],
    }
    loads = []
    for chunk in FLIPS:
        loads.append(chunk)
        loads.extend(others.get(chunk, []))
    return loads


def score_banks(tile):
    banks, first = [], P * tile
    while first < S:
        passes, room = [], P if tile and not banks else min(CHUNK, S - first)
        while room:
            width = max(w for w in (P, 2 * P, 4 * P) if w <= room)
            passes.append((first, width))
            first += width
            room -= width
        banks.append(passes)
    return banks


def tile_dependency_pb_kernel(
    tc, y, h0, c0, wih_f, whh_f, bih_f, bhh_f, wih_b, whh_b, bih_b, bhh_b, wd, fc_w, fc_b, out_0, out_1
):
    nc = tc.nc
    with ExitStack() as stack:
        stack.enter_context(tc.manual_schedule())
        const = stack.enter_context(tc.tile_pool(name="const", bufs=1))
        raws = stack.enter_context(tc.tile_pool(name="raws", bufs=1))
        keep = stack.enter_context(tc.tile_pool(name="keep", bufs=1))
        stage = stack.enter_context(tc.tile_pool(name="stage", bufs=3))
        work = stack.enter_context(tc.tile_pool(name="work", bufs=3))
        outs = stack.enter_context(tc.tile_pool(name="outs", bufs=1))
        psum = stack.enter_context(tc.psum_pool(name="psum", bufs=8))

        ident_f32 = const.tile([P, P], F32)
        make_identity(nc, ident_f32[:])
        ident_bf16 = const.tile([P, P], BF16)
        make_identity(nc, ident_bf16[:])
        ones = const.tile([P, P], BF16)
        nc.gpsimd.memset(ones[:], 1.0)
        idle_operand = const.tile([P, CHUNK], BF16)
        nc.gpsimd.memset(idle_operand[:], 0.0)
        on_or_above = const.tile([P, CHUNK], F32)
        nc.gpsimd.memset(on_or_above[:], 1.0)
        nc.gpsimd.affine_select(
            out=on_or_above[:],
            in_=on_or_above[:],
            pattern=[[1, CHUNK]],
            compare_op=ALU.is_ge,
            fill=0.0,
            base=0,
            channel_multiplier=-1,
        )
        zeros = const.tile([P, S - P], F32)
        nc.vector.memset(zeros[:], 0.0)
        first_sigmoid = const.tile([P, 1], F32)
        nc.scalar.activation(out=first_sigmoid[:], in_=zeros[:, 0:1], func=ACT.Sigmoid)

        matrices = {"y": (y, y), "h0": (h0[0], h0[1]), "c0": (c0[0], c0[1]), "wih": (wih_f, wih_b), "whh": (whh_f, whh_b)}
        biases = ((bih_f, bhh_f), (bih_b, bhh_b))
        raw = {}
        bias_rows = []
        for d in range(DIRECTIONS):
            bias_rows.append(raws.tile([P, H], BF16, name="bias_rows_%d" % d))
            nc.vector.memset(bias_rows[d][:], 0.0)
        pair_rows = raws.tile([P, P], BF16)
        nc.vector.memset(pair_rows[:], 0.0)
        row_bias_rows = raws.tile([P, DIRECTIONS, H], BF16)
        nc.vector.memset(row_bias_rows[:], 0.0)
        for load in load_order():
            kind, d, c = load
            if kind == "bias":
                for i, vec in enumerate(biases[d]):
                    nc.sync.dma_start(out=bias_rows[d][GATES * i : GATES * (i + 1), :], in_=vec.rearrange("(r c) -> r c", c=H))
            elif kind == "row_bias":
                for d2 in range(DIRECTIONS):
                    for i, vec in enumerate(biases[d2]):
                        nc.sync.dma_start(out=row_bias_rows[i : i + 1, d2, :], in_=vec[3 * H : 4 * H].unsqueeze(0))
            elif kind == "pair":
                for i, vec in enumerate((wd, fc_w[0])):
                    nc.sync.dma_start(out=pair_rows[PACK * i : PACK * (i + 1), :], in_=vec.rearrange("(r c) -> r c", c=P))
            else:
                rows = matrices[kind][d][CHUNK * c : CHUNK * (c + 1), :]
                raw[load] = raws.tile([P, ROW_TILES, rows.shape[1]], BF16, name="%s_raw_%d_%d" % load)
                if kind in ("wih", "whh"):
                    for q in range(CHUNK // H):
                        nc.sync.dma_start(
                            out=raw[load][:, SLOTS * q : SLOTS * (q + 1), :].rearrange("p a k -> p (a k)"),
                            in_=rows[H * q : H * (q + 1), :].rearrange("(p a) k -> p (a k)", p=P),
                        )
                else:
                    halves = 2 if kind == "y" else 1
                    n_slots = ROW_TILES // halves
                    for i in range(halves):
                        nc.sync.dma_start(
                            out=raw[load][:, n_slots * i : n_slots * (i + 1), :],
                            in_=rows[P * n_slots * i : P * n_slots * (i + 1), :].rearrange("(a p) k -> p a k", p=P),
                        )
        fc_b_bf16 = const.tile([P, 1], BF16)
        nc.sync.dma_start(out=fc_b_bf16[:], in_=fc_b.partition_broadcast(P))
        fc_b_col = const.tile([P, 1], F32)
        nc.gpsimd.tensor_copy(out=fc_b_col[:], in_=fc_b_bf16[:])
        for tile in range(1, TOKEN_TILES):
            nc.sync.dma_start(out=out_0[P * tile : P * (tile + 1), 0 : P * tile], in_=zeros[:, 0 : P * tile])

        flips = {}
        flipped = {}
        grouped = {}
        codes, scales = {}, {}

        def flip_chunk(chunk):
            kind = chunk[0]
            flips[chunk] = []
            if kind in ("wih", "y"):
                for pair in range(ROW_TILES // 2):
                    bank = psum.tile([P, 2, 2 * P], F32, tag="bank", name="flip_%s_%d_%d_%d" % (chunk + (pair,)))
                    for i in range(2):
                        words = raw[chunk][:, 2 * pair + i, :].bitcast(F32)
                        for v in range(2):
                            nc.tensor.transpose(bank[:, v, P * i : P * (i + 1)], words[:, P * v : P * (v + 1)], ident_f32[:])
                    flips[chunk].append(bank)
            else:
                bank = psum.tile([P, SLOTS, ROW_TILES, P], BF16, tag="bank", name="flip_%s_%d_%d" % chunk)
                for j in range(SLOTS):
                    for a in range(ROW_TILES):
                        nc.tensor.transpose(bank[:, j, a, :], raw[chunk][:, a, P * j : P * (j + 1)], ident_bf16[:])
                flips[chunk].append(bank)

        def save_chunk(chunk):
            if chunk[0] in ("wih", "y"):
                grouped[chunk] = stage.tile([P, CHUNK * PACK], BF16, tag="grouped", name="grouped_%s_%d_%d" % chunk, align_bytes=64)
                words = grouped[chunk][:].bitcast(F32).rearrange("p (r v) -> p r v", v=2)
                second_copy = nc.scalar.copy if FLIPS.index(chunk) < SINGLE_FLIPS else nc.vector.tensor_copy
                for pair, copy in enumerate((nc.scalar.copy, second_copy)):
                    copy(out=words[:, 2 * P * pair : 2 * P * (pair + 1), :], in_=flips[chunk][pair][:].rearrange("p v r -> p r v"))
            else:
                flipped[chunk] = keep.tile([P, SLOTS, CHUNK], BF16, name="%sT_%d_%d" % chunk)
                nc.scalar.copy(out=flipped[chunk][:], in_=flips[chunk][0][:].rearrange("p j a r -> p j (a r)"))

        def quantise_chunk(chunk):
            if chunk[0] in ("wih", "y"):
                codes[chunk] = keep.tile([P, CHUNK], U32, name="%s_codes_%d_%d" % chunk, align_bytes=64)
                scales[chunk] = keep.tile([P, CHUNK], U8, name="%s_scales_%d_%d" % chunk, align_bytes=64)
                nc.vector.quantize_mx(out=codes[chunk][:].bitcast(FP8X4), scales=scales[chunk][:], in_=grouped[chunk][:])

        def warm_up(s):
            bank = psum.tile([P, CHUNK], F32, tag="bank", name="warm_up_%d" % s)
            nc.tensor.matmul(bank[:], lhsT=ones[:], rhs=idle_operand[:], start=True, stop=True)

        bias = const.tile([P, DIRECTIONS, GATE_TILES], F32)
        row_bias = const.tile([P, DIRECTIONS, H], F32)
        pair_weight = const.tile([P, PACK], F32)

        def flip_bias(d):
            bank = psum.tile([P, P], F32, tag="bank", name="flip_bias_%d" % d)
            nc.tensor.transpose(bank[:], bias_rows[d][:].bitcast(F32), ident_f32[:])
            cols = const.tile([P, 2, GATE_TILES], F32, name="bias_cols_%d" % d)
            nc.vector.tensor_copy(out=cols[:], in_=bank[:, 0 : 2 * GATES].bitcast(BF16).rearrange("p (i g) -> p i g", i=2))
            nc.vector.tensor_tensor(out=bias[:, d, :], in0=cols[:, 0, :], in1=cols[:, 1, :], op=ALU.add)

        def spread_row_bias():
            bank = psum.tile([P, DIRECTIONS, H], F32, tag="bank", name="spread_row_bias")
            nc.tensor.matmul(
                bank[:].rearrange("p d f -> p (d f)"),
                lhsT=ones[:],
                rhs=row_bias_rows[:].rearrange("p d f -> p (d f)"),
                start=True,
                stop=True,
            )
            nc.scalar.copy(out=row_bias[:], in_=bank[:])

        def flip_pair():
            bank = psum.tile([P, P], BF16, tag="bank", name="flip_pair")
            nc.tensor.transpose(bank[:], pair_rows[:], ident_bf16[:])
            cols = const.tile([P, 2, PACK], F32, name="pair_cols")
            nc.vector.tensor_copy(out=cols[:], in_=bank[:, 0 : 2 * PACK].rearrange("p (i t) -> p i t", i=2))
            nc.vector.tensor_tensor(out=pair_weight[:], in0=cols[:, 0, :], in1=cols[:, 1, :], op=ALU.mult)

        mx_ps = {}
        mx_cols = {}
        mx_rows = {}

        def matmul_mx(out, stationary, stationary_cols, moving, moving_cols):
            nc.tensor.matmul_mx(
                out=out,
                lhsT=codes[stationary][:, stationary_cols].bitcast(FP8X4),
                lhsT_scale=scales[stationary][:, stationary_cols],
                rhs=codes[moving][:, moving_cols].bitcast(FP8X4),
                rhs_scale=scales[moving][:, moving_cols],
                start=True,
                stop=True,
            )

        def mx_place(m):
            half, g = divmod(m, GATE_TILES)
            return list(SUMMED_TILES)[half] + (g,)

        def mx_product(m):
            n, d, g = mx_place(m)
            mx_ps[m] = psum.tile([P, CHUNK], F32, tag="bank", name="mx_%d" % m)
            if g < SUMMED_TILES[n, d]:
                c, slot = divmod(g, ROW_TILES)
                matmul_mx(mx_ps[m][:], ("wih", d, c), slice(P * slot, P * (slot + 1)), ("y", 0, n), slice(0, CHUNK))
            else:
                for i in range(2):
                    a = 2 * (GATE_TILES - 1 - g) + i
                    matmul_mx(mx_ps[m][:, H * i : H * (i + 1)], ("y", 0, n), slice(P * a, P * (a + 1)), ("wih", d, 1), slice(H, 2 * H))

        def save_mx_product(m):
            n, d, g = mx_place(m)
            if g == 0:
                mx_cols[n, d] = keep.tile([P, GATE_TILES, CHUNK], F32, tag="mx_cols", name="mx_cols_%d_%d" % (n, d), bufs=3)
                mx_rows[n, d] = keep.tile([P, ROW_TILES, H], F32, tag="mx_rows", name="mx_rows_%d_%d" % (n, d), bufs=3)
            if g >= SUMMED_TILES[n, d]:
                a = 2 * (GATE_TILES - 1 - g)
                nc.vector.tensor_tensor(
                    out=mx_rows[n, d][:, a : a + 2, :].rearrange("p i (a q) -> p i a q", a=SLOTS),
                    in0=mx_ps[m][:].rearrange("p (i a q) -> p i a q", i=2, a=SLOTS),
                    in1=row_bias[:, d, :].rearrange("p (q a) -> p a q", a=SLOTS).unsqueeze(1).to_broadcast([P, 2, SLOTS, P]),
                    op=ALU.add,
                )
            elif g % 3 < 2:
                nc.scalar.activation(
                    out=mx_cols[n, d][:, g, :], in_=mx_ps[m][:], func=ACT.Identity, bias=bias[:, d, g : g + 1], scale=1.0
                )
            else:
                nc.vector.tensor_scalar(
                    out=mx_cols[n, d][:, g, :], in0=mx_ps[m][:], scalar1=bias[:, d, g : g + 1], scalar2=None, op0=ALU.add
                )

        gates_ps = {}
        forget_in, candidate, out_sum, out_gate = {}, {}, {}, {}
        kept, fresh, cell, tanh_c = {}, {}, {}, {}

        def place(turn):
            tile, d = TURNS[turn]
            return (tile, d) + divmod(tile, ROW_TILES)

        def plain_products(turn):
            tile, d, n, a = place(turn)
            gates_ps[turn] = []
            for b in range(2):
                bank = psum.tile([P, CHUNK], F32, tag="bank", name="gates_%d_%d" % (turn, b))
                gates_ps[turn].append(bank)
                for k in range(SLOTS):
                    nc.tensor.matmul(
                        bank[:],
                        lhsT=flipped["h0", d, n][:, k, P * a : P * (a + 1)],
                        rhs=flipped["whh", d, b][:, k, :],
                        start=(k == 0),
                        stop=False,
                    )

        def add_mx_products(turn):
            tile, d, n, a = place(turn)
            for g in range(SUMMED_TILES[n, d]):
                b, slot = divmod(g, ROW_TILES)
                nc.tensor.matmul(
                    gates_ps[turn][b][:, P * slot : P * (slot + 1)],
                    lhsT=mx_cols[n, d][:, g, P * a : P * (a + 1)],
                    rhs=ident_f32[:],
                    start=False,
                    stop=(g in (ROW_TILES - 1, SUMMED_TILES[n, d] - 1)),
                    is_transpose=True,
                )

        def activate(turn):
            forget_in[turn] = work.tile([P, 2, H], F32, tag="forget_in", name="forget_in_%d" % turn)
            nc.scalar.activation(
                out=forget_in[turn][:].rearrange("p i (q a) -> p i q a", a=SLOTS),
                in_=gates_ps[turn][0][:].rearrange("p (i a q) -> p i q a", i=2, a=SLOTS),
                func=ACT.Sigmoid,
            )
            candidate[turn] = work.tile([P, H], F32, tag="candidate", name="candidate_%d" % turn)
            nc.scalar.activation(
                out=candidate[turn][:].rearrange("p (q a) -> p q a", a=SLOTS),
                in_=gates_ps[turn][1][:, 0:H].rearrange("p (a q) -> p q a", a=SLOTS),
                func=ACT.Tanh,
            )

        def sum_out_gate(turn):
            tile, d, n, a = place(turn)
            if SUMMED_TILES[n, d] == GATE_TILES:
                out_sum[turn] = gates_ps[turn][1][:, H : 2 * H]
                return
            out_sum[turn] = work.tile([P, H], F32, tag="out_sum", name="out_sum_%d" % turn)
            out_sum[turn] = out_sum[turn][:]
            nc.vector.tensor_tensor(out=out_sum[turn], in0=gates_ps[turn][1][:, H : 2 * H], in1=mx_rows[n, d][:, a, :], op=ALU.add)

        def activate_out_gate(turn):
            out_gate[turn] = work.tile([P, H], F32, tag="out_gate", name="out_gate_%d" % turn)
            nc.scalar.activation(
                out=out_gate[turn][:].rearrange("p (q a) -> p q a", a=SLOTS),
                in_=out_sum[turn].rearrange("p (a q) -> p q a", a=SLOTS),
                func=ACT.Sigmoid,
            )

        def keep_cell(turn):
            tile, d, n, a = place(turn)
            kept[turn] = work.tile([P, H], F32, tag="kept", name="kept_%d" % turn)
            nc.vector.tensor_tensor(out=kept[turn][:], in0=forget_in[turn][:, 1, :], in1=raw["c0", d, n][:, a, :], op=ALU.mult)

        def fresh_cell(turn):
            fresh[turn] = work.tile([P, H], F32, tag="fresh", name="fresh_%d" % turn)
            nc.vector.tensor_tensor(out=fresh[turn][:], in0=forget_in[turn][:, 0, :], in1=candidate[turn][:], op=ALU.mult)

        def add_cell(turn):
            cell[turn] = work.tile([P, H], F32, tag="cell", name="cell_%d" % turn)
            nc.vector.tensor_tensor(out=cell[turn][:], in0=kept[turn][:], in1=fresh[turn][:], op=ALU.add)

        def tanh_cell(turn):
            tanh_c[turn] = work.tile([P, H], F32, tag="tanh_c", name="tanh_c_%d" % turn)
            nc.scalar.activation(out=tanh_c[turn][:], in_=cell[turn][:], func=ACT.Tanh)

        hid, back_ps, score_ps, u_codes, u_scales = {}, {}, {}, {}, {}
        hid_codes = keep.tile([P, S], U32, align_bytes=64)
        hid_scales = keep.tile([P, S], U8, align_bytes=64)

        def make_hid(turn):
            tile, d, n, a = place(turn)
            if d == 0:
                hid[tile] = outs.tile([P, D], F32, tag="hid", name="hid_%d" % tile, bufs=5)
            nc.vector.tensor_tensor(out=hid[tile][:, H * d : H * (d + 1)], in0=out_gate[turn][:], in1=tanh_c[turn][:], op=ALU.mult)
            if d == 1:
                nc.sync.dma_start(out=out_1[0, P * tile : P * (tile + 1), :], in_=hid[tile][:])

        def flip_hid(tile):
            back_ps[tile] = psum.tile([P, PACK, P], F32, tag="bank", name="back_%d" % tile)
            for t in range(PACK):
                nc.tensor.transpose(back_ps[tile][:, t, :], hid[tile][:, P * t : P * (t + 1)], ident_f32[:])

        def group_hid(tile):
            grouped[tile] = stage.tile([P, 2, P, PACK], BF16, tag="grouped_hid", name="grouped_hid_%d" % tile, align_bytes=64)
            nc.scalar.copy(out=grouped[tile][:, 0, :, :], in_=back_ps[tile][:].rearrange("p t r -> p r t"))

        def group_u(tile):
            nc.vector.tensor_tensor(
                out=grouped[tile][:, 1, :, :],
                in0=back_ps[tile][:].rearrange("p t r -> p r t"),
                in1=pair_weight[:].unsqueeze(1).to_broadcast([P, P, PACK]),
                op=ALU.mult,
            )

        def quantise_tile(tile):
            cols = slice(P * tile, P * (tile + 1))
            u_codes[tile] = work.tile([P, P], U32, tag="u_codes", name="u_codes_%d" % tile, align_bytes=64)
            u_scales[tile] = work.tile([P, P], U8, tag="u_scales", name="u_scales_%d" % tile, align_bytes=64)
            for i, (code, scale) in enumerate(((hid_codes[:, cols], hid_scales[:, cols]), (u_codes[tile][:], u_scales[tile][:]))):
                nc.vector.quantize_mx(out=code.bitcast(FP8X4), scales=scale, in_=grouped[tile][:, i, :, :].rearrange("p r t -> p (r t)"))

        def score(tile):
            score_ps[tile] = []
            for i, passes in enumerate(score_banks(tile)):
                bank = psum.tile([P, CHUNK], F32, tag="bank", name="score_%d_%d" % (tile, i))
                score_ps[tile].append(bank)
                for first, width in passes:
                    start = first - passes[0][0]
                    nc.tensor.matmul_mx(
                        out=bank[:, start : start + width],
                        lhsT=u_codes[tile][:].bitcast(FP8X4),
                        lhsT_scale=u_scales[tile][:],
                        rhs=hid_codes[:, first : first + width].bitcast(FP8X4),
                        rhs_scale=hid_scales[:, first : first + width],
                        start=True,
                        stop=True,
                    )

        def store_scores(tile):
            for i, passes in enumerate(score_banks(tile)):
                bank = score_ps[tile][i]
                first, width = passes[0][0], sum(w for f, w in passes)
                piece = outs.tile([P, CHUNK], F32, tag="piece", name="piece_%d_%d" % (tile, i), bufs=8)
                if i == 0:
                    nc.vector.scalar_tensor_tensor(
                        out=piece[:, 0:width],
                        in0=bank[:, 0:width],
                        scalar=fc_b_col[:, 0:1],
                        in1=on_or_above[:, 0:width],
                        op0=ALU.add,
                        op1=ALU.mult,
                    )
                else:
                    nc.scalar.activation(out=piece[:, 0:width], in_=bank[:, 0:width], func=ACT.Identity, bias=fc_b_col[:, 0:1], scale=1.0)
                nc.sync.dma_start(out=out_0[P * tile : P * (tile + 1), first : first + width], in_=piece[:, 0:width])

        def flipped_in(step):
            return [chunk for i, chunk in enumerate(FLIPS) if step == i - max(0, i - SINGLE_FLIPS + 1) // 2]

        mx_steps = [first + m // rate for first, rate, count in MX_RUNS for m in range(count)]

        def turns_at(step, offset):
            turn = step - TURN_STEP - offset
            return [turn] if 0 <= turn < len(TURNS) else []

        def tiles_at(step, offset):
            return [TURNS[turn][0] for turn in turns_at(step, offset) if TURNS[turn][1] == 1]

        def scored_at(step):
            return [tile for n, offset in enumerate(SCORE_STEPS) for tile in tiles_at(step, offset) if tile // ROW_TILES == n]

        for s in range(TURN_STEP + len(TURNS) + max(SCORE_STEPS)):
            mx_now = [m for m, step in enumerate(mx_steps) if step == s]
            for turn in turns_at(s, HID_STEP):
                make_hid(turn)
            for turn in turns_at(s, ACT_STEP):
                activate(turn)
            for chunk in flipped_in(s - 1):
                save_chunk(chunk)
            for m in mx_now:
                mx_product(m)
            for turn in turns_at(s, ACT_STEP):
                keep_cell(turn)
            for tile in scored_at(s):
                score(tile)
            for turn in turns_at(s, ACT_STEP):
                sum_out_gate(turn)
            for tile in tiles_at(s, GROUP_STEP):
                group_hid(tile)
            for turn in turns_at(s, ACT_STEP):
                fresh_cell(turn)
            for chunk in flipped_in(s - 1):
                quantise_chunk(chunk)
            for tile in tiles_at(s, GROUP_STEP):
                group_u(tile)
            for turn in turns_at(s, TANH_STEP):
                tanh_cell(turn)
            for turn in turns_at(s, ACT_STEP):
                add_cell(turn)
            for tile in tiles_at(s, GROUP_STEP):
                quantise_tile(tile)
            for m in mx_now:
                save_mx_product(m)
            for turn in turns_at(s, ACT_STEP):
                activate_out_gate(turn)
            for tile in scored_at(s):
                store_scores(tile)
            for turn in turns_at(s, 0):
                plain_products(turn)
            for turn in turns_at(s, 0):
                add_mx_products(turn)
            for tile in tiles_at(s, BACK_STEP):
                flip_hid(tile)
            for chunk in flipped_in(s):
                flip_chunk(chunk)
            if s in WARM_STEPS:
                warm_up(s)
                warm_up(s + 100)
            for d, step in enumerate(BIAS_STEPS):
                if step == s:
                    flip_bias(d)
            if s == PAIR_STEP:
                flip_pair()
            if s == ROW_BIAS_STEP:
                spread_row_bias()
